import numpy as np
import ml_dtypes


def mxq(x, axis, fmt="e4m3"):
    dtype, down = {"e4m3": (ml_dtypes.float8_e4m3fn, 7), "e5m2": (ml_dtypes.float8_e5m2, 14)}[fmt]
    v = np.moveaxis(np.asarray(x, np.float32).astype(ml_dtypes.bfloat16).astype(np.float64), axis, -1)
    blocks = v.reshape(v.shape[:-1] + (-1, 32))
    amax = np.abs(blocks).max(-1, keepdims=True)
    byte = np.maximum(np.where(amax > 0, np.frexp(amax)[1] - 1 + 127, 0) - down, 1)
    scale = np.exp2(byte - 127.0)
    codes = (blocks / scale).astype(np.float32).astype(dtype).astype(np.float64)
    return np.moveaxis((codes * scale).reshape(v.shape), -1, axis)


WIDE = False


def mx_kscale(k):
    if not WIDE:
        return np.ones(k)
    levels = np.array([10, -10, 5, -5, 0])
    a = np.random.permutation(np.resize(levels, k // 512 * 4)).reshape(k // 512, 4)
    idx = np.arange(k)
    return np.exp2(a[idx // 512, idx % 128 // 32])


BF16 = ml_dtypes.bfloat16


def bf(x):
    return np.asarray(x, np.float32).astype(BF16)


def f64(x):
    return np.asarray(x).astype(np.float64)


E2M1 = np.array([0.0, 0.5, 1.0, 1.5, 2.0, 3.0, 4.0, 6.0, -0.0, -0.5, -1.0, -1.5, -2.0, -3.0, -4.0, -6.0])


def pack_weight(w, fmt):
    k, n = w.shape
    w = f64(bf(w)).reshape(k // 32, 32, n)
    amax = np.abs(w).max(1)
    if fmt == "e4m3":
        byte = np.frexp(amax)[1] - 1 + 127 - 7
    else:
        mant, ex = np.frexp(amax / 6.0)
        byte = np.where(mant > 0.5, ex, ex - 1) + 127
    byte = np.clip(np.where(amax > 0, byte, 1), 1, 254)
    scaled = (w * np.exp2(127.0 - byte)[:, None, :]).reshape(k, n).astype(np.float32)
    by_word = np.ascontiguousarray(scaled.reshape(k // 512, 128, 4, n).transpose(0, 1, 3, 2))
    if fmt == "e4m3":
        words = by_word.astype(ml_dtypes.float8_e4m3fn).view(np.uint8)
    else:
        c = by_word.astype(ml_dtypes.float4_e2m1fn).view(np.uint8) & 0xF
        words = c[..., 0::2] | (c[..., 1::2] << 4)
    return np.ascontiguousarray(words), np.ascontiguousarray(byte.astype(np.uint8).reshape(k // 512, 16, n))


def unpack_weight(words, scales, fmt):
    g, p, n, _ = words.shape
    if fmt == "e4m3":
        vals = np.ascontiguousarray(words).view(ml_dtypes.float8_e4m3fn).astype(np.float64)
    else:
        nib = np.empty((g, p, n, 4), np.uint8)
        nib[..., 0::2] = words & 0xF
        nib[..., 1::2] = words >> 4
        vals = E2M1[nib]
    vals = vals * np.repeat(np.exp2(scales.astype(np.float64) - 127.0), 8, axis=1)[..., None]
    return vals.transpose(0, 1, 3, 2).reshape(g * 512, n)

def pack4(w):
    words, scales = pack_weight(w, "e2m1")
    return words.reshape(words.shape[0], 128, -1), scales


def unpack4(words, scales):
    return unpack_weight(words.reshape(words.shape[0], 128, -1, 2), scales, "e2m1")


B, V, H = 4096, 128, 512
G = 4 * H
EPS = 1e-5


def sigmoid(v):
    return 1.0 / (1.0 + np.exp(-v))


def layer_norm(v, w, b):
    mu = v.mean(-1, keepdims=True)
    var = ((v - mu) ** 2).mean(-1, keepdims=True)
    return (v - mu) / np.sqrt(var + EPS) * w + b


def setup_inputs():
    s = mx_kscale(H)
    x = bf(np.random.standard_normal((B, V)))
    h0 = bf(np.random.standard_normal((B, H)) * s)
    c0 = bf(np.random.standard_normal((B, H)))
    w_ih1 = bf(np.random.standard_normal((G, V)) / np.sqrt(V))
    w_hh1 = np.random.standard_normal((G, H)) / np.sqrt(H) / s
    w_hh1_words, w_hh1_scales = pack4(np.ascontiguousarray(w_hh1.T))
    return {"x": x,
            "h0": h0,
            "c0": c0,
            "w_ih1": w_ih1,
            "w_hh1_words": w_hh1_words,
            "w_hh1_scales": w_hh1_scales,
            "lni_w1": bf(1.0 + 0.1 * np.random.standard_normal(G)),
            "lni_b1": bf(0.1 * np.random.standard_normal(G)),
            "lnh_w1": bf(1.0 + 0.1 * np.random.standard_normal(G)),
            "lnh_b1": bf(0.1 * np.random.standard_normal(G)),
            "lnc_w1": bf(1.0 + 0.1 * np.random.standard_normal(H)),
            "lnc_b1": bf(0.1 * np.random.standard_normal(H))}


def reference(x, h0, c0, w_ih1, w_hh1_words, w_hh1_scales, lni_w1, lni_b1, lnh_w1, lnh_b1, lnc_w1, lnc_b1):
    a = f64(x) @ f64(w_ih1).T
    r = mxq(f64(h0), 1, "e4m3") @ unpack4(w_hh1_words, w_hh1_scales)
    gates = layer_norm(a, f64(lni_w1), f64(lni_b1)) + layer_norm(r, f64(lnh_w1), f64(lnh_b1))
    i, f, g, o = np.split(gates, 4, axis=1)
    cy = layer_norm(sigmoid(f) * f64(c0) + sigmoid(i) * np.tanh(g), f64(lnc_w1), f64(lnc_b1))
    hy = sigmoid(o) * np.tanh(cy)
    return hy, cy

@@ -1,0 +1,454 @@
+from contextlib import ExitStack
+
+import concourse.mybir as mybir
+from concourse.masks import make_identity
+
+F32 = mybir.dt.float32
+BF16 = mybir.dt.bfloat16
+I32 = mybir.dt.int32
+U32 = mybir.dt.uint32
+U8 = mybir.dt.uint8
+FP8X4 = mybir.dt.float8_e4m3fn_x4
+FP4X4 = mybir.dt.float4_e2m1fn_x4
+ALU = mybir.AluOpType
+ACT = mybir.ActivationFunctionType
+AX = mybir.AxisListType
+
+P = 128
+PACK = 4
+B, V, H = 4096, 128, 512
+G = 4 * H
+EPS = 1e-5
+BANK = 512
+BANKS = G // BANK
+ROW_TILES = B // P
+GROUP = 4
+N_GROUPS = ROW_TILES // GROUP
+W_TILES = G // P
+
+FLOPS = 2 * B * G * (V + H)
+
+
+def tile_multilstm_pa_t_kernel(
+    tc,
+    x,
+    h0,
+    c0,
+    w_ih1,
+    w_hh1_words,
+    w_hh1_scales,
+    lni_w1,
+    lni_b1,
+    lnh_w1,
+    lnh_b1,
+    lnc_w1,
+    lnc_b1,
+    out_0,
+    out_1,
+):
+    nc = tc.nc
+
+    x_rows = x.rearrange("(p i) v -> p i v", i=ROW_TILES)
+    h0_rows = h0.rearrange("(p i) k -> p i k", i=ROW_TILES)
+    c0_rows = c0.rearrange("(p i) h -> p i h", i=ROW_TILES)
+    hy_rows = out_0.rearrange("(p i) h -> p i h", i=ROW_TILES)
+    cy_rows = out_1.rearrange("(p i) h -> p i h", i=ROW_TILES)
+
+    with ExitStack() as ctx:
+        const = ctx.enter_context(tc.tile_pool(name="const", bufs=1))
+        setup = ctx.enter_context(tc.tile_pool(name="setup", bufs=1))
+        stream = ctx.enter_context(tc.tile_pool(name="stream", bufs=3))
+        prepared = ctx.enter_context(tc.tile_pool(name="prepared", bufs=2))
+        wide = ctx.enter_context(tc.tile_pool(name="wide", bufs=2))
+        gate_pool = ctx.enter_context(tc.tile_pool(name="gate_pool", bufs=3))
+        cell = ctx.enter_context(tc.tile_pool(name="cell", bufs=2))
+        result = ctx.enter_context(tc.tile_pool(name="result", bufs=3))
+        small = ctx.enter_context(tc.tile_pool(name="small", bufs=8))
+        ps_r = ctx.enter_context(tc.psum_pool(name="ps_r", bufs=3))
+        ps_x = ctx.enter_context(tc.psum_pool(name="ps_x", bufs=3))
+        ps_misc = ctx.enter_context(tc.psum_pool(name="ps_misc", bufs=2))
+
+        w_nat = setup.tile([P, W_TILES, V], BF16)
+        nc.sync.dma_start(out=w_nat[:], in_=w_ih1.rearrange("(t p) v -> p t v", p=P))
+
+        vec_rows = setup.tile([P, P], BF16)
+        nc.vector.memset(vec_rows[:], 0.0)
+        for slot, vec in enumerate((lni_w1, lni_b1, lnh_b1)):
+            nc.sync.dma_start(
+                out=vec_rows[slot * W_TILES : (slot + 1) * W_TILES, :],
+                in_=vec.rearrange("(t p) -> t p", p=P),
+            )
+
+        x_all = const.tile([P, ROW_TILES, V], BF16)
+        nc.sync.dma_start(out=x_all[:], in_=x_rows)
+
+        w_words = const.tile([P, 2 * G], U8, align_bytes=64)
+        nc.sync.dma_start(out=w_words[:].bitcast(I32), in_=w_hh1_words[0].bitcast(I32))
+        w_scales = const.tile([P, G], U8, align_bytes=64)
+        nc.vector.memset(w_scales[:].bitcast(I32), 0)
+        for quad in range(4):
+            nc.sync.dma_start(
+                out=w_scales[32 * quad : 32 * quad + 4, :].bitcast(I32),
+                in_=w_hh1_scales[0, 4 * quad : 4 * quad + 4, :].bitcast(I32),
+            )
+
+        gain_h = const.tile([P, G], BF16)
+        nc.sync.dma_start(out=gain_h[:], in_=lnh_w1.partition_broadcast(P))
+        gain_c = const.tile([P, H], BF16)
+        nc.sync.dma_start(out=gain_c[:], in_=lnc_w1.partition_broadcast(P))
+        bias_c = const.tile([P, H], BF16)
+        nc.sync.dma_start(out=bias_c[:], in_=lnc_b1.partition_broadcast(P))
+
+        ident_bf = const.tile([P, P], BF16)
+        make_identity(nc, ident_bf[:])
+        ident_f32 = const.tile([P, P], F32)
+        make_identity(nc, ident_f32[:])
+        ones_bf = const.tile([P, P], BF16)
+        nc.vector.memset(ones_bf[:], 1.0)
+        neg_half = const.tile([P, GROUP], F32)
+        nc.vector.memset(neg_half[:], -0.5)
+
+        def inverse_std(sum_sq, count, width):
+            var_eps = small.tile([P, width], F32)
+            nc.gpsimd.tensor_scalar(
+                out=var_eps[:], in0=sum_sq, scalar1=1.0 / count, scalar2=EPS, op0=ALU.mult, op1=ALU.add
+            )
+            rstd = small.tile([P, width], F32)
+            nc.gpsimd.tensor_tensor(out=rstd[:], in0=var_eps[:], in1=neg_half[:, 0:width], op=ALU.pow)
+            return rstd
+
+        vec_ps = ps_misc.tile([P, P], BF16, tag="misc")
+        nc.tensor.transpose(out=vec_ps[:], in_=vec_rows[:], identity=ident_bf[:])
+        vec_cols = const.tile([P, 3 * W_TILES], F32)
+        nc.vector.tensor_copy(out=vec_cols[:], in_=vec_ps[:, 0 : 3 * W_TILES])
+        gain_i_cols = vec_cols[:, 0:W_TILES]
+        bias_cols = const.tile([P, W_TILES], F32)
+        nc.vector.tensor_tensor(
+            out=bias_cols[:],
+            in0=vec_cols[:, W_TILES : 2 * W_TILES],
+            in1=vec_cols[:, 2 * W_TILES : 3 * W_TILES],
+            op=ALU.add,
+        )
+
+        wsum_ps = ps_misc.tile([P, V], F32, tag="misc")
+        for t in range(W_TILES):
+            nc.tensor.matmul(
+                out=wsum_ps[:], lhsT=ones_bf[:], rhs=w_nat[:, t, :], start=(t == 0), stop=(t == W_TILES - 1)
+            )
+        w_centred = setup.tile([P, W_TILES, V], F32)
+        nc.vector.scalar_tensor_tensor(
+            out=w_centred[:],
+            in0=wsum_ps[:].unsqueeze(1).to_broadcast([P, W_TILES, V]),
+            scalar=-1.0 / G,
+            in1=w_nat[:],
+            op0=ALU.mult,
+            op1=ALU.add,
+        )
+        cov_ps = ps_misc.tile([V, V], F32, tag="misc")
+        for t in range(W_TILES):
+            nc.tensor.matmul(
+                out=cov_ps[:],
+                lhsT=w_centred[:, t, :],
+                rhs=w_centred[:, t, :],
+                start=(t == 0),
+                stop=(t == W_TILES - 1),
+            )
+        cov = const.tile([V, V], F32)
+        nc.scalar.mul(out=cov[:], in_=cov_ps[:], mul=1.0 / G)
+
+        w_gained = setup.tile([P, W_TILES, V], F32)
+        nc.vector.tensor_tensor(
+            out=w_gained[:],
+            in0=w_centred[:],
+            in1=gain_i_cols.unsqueeze(2).to_broadcast([P, W_TILES, V]),
+            op=ALU.mult,
+        )
+        w_x = const.tile([V, G], F32)
+        for j in range(BANKS):
+            wt_ps = ps_misc.tile([V, BANK], F32, tag="misc")
+            for q in range(BANK // P):
+                nc.tensor.transpose(
+                    out=wt_ps[:, q * P : (q + 1) * P],
+                    in_=w_gained[:, j * (BANK // P) + q, :],
+                    identity=ident_f32[:],
+                )
+            nc.scalar.copy(out=w_x[:, j * BANK : (j + 1) * BANK], in_=wt_ps[:])
+
+        groups = {}
+
+        def load_group(grp):
+            tiles = slice(grp * GROUP, (grp + 1) * GROUP)
+            h0_grp = stream.tile([P, GROUP, H], BF16)
+            nc.sync.dma_start(out=h0_grp[:], in_=h0_rows[:, tiles, :])
+            c0_grp = stream.tile([P, GROUP, H], BF16)
+            nc.sync.dma_start(out=c0_grp[:], in_=c0_rows[:, tiles, :])
+            groups[grp] = {"h0": h0_grp, "c0": c0_grp}
+
+        def transpose_h0(grp):
+            grouped = prepared.tile([P, GROUP * P * PACK], BF16, align_bytes=64)
+            grouped_words = grouped[:].bitcast(F32).rearrange("p (t b u) -> p t b u", t=GROUP, u=2)
+            for half in range(2):
+                hT_ps = ps_misc.tile([P, 2, 2, P], F32, tag="misc")
+                for t in range(2):
+                    words = groups[grp]["h0"][:, 2 * half + t, :].bitcast(F32)
+                    for u in range(2):
+                        nc.tensor.transpose(
+                            out=hT_ps[:, t, u, :], in_=words[:, u : H // 2 : 2], identity=ident_f32[:]
+                        )
+                nc.scalar.copy(
+                    out=grouped_words[:, 2 * half : 2 * half + 2, :, :],
+                    in_=hT_ps[:].rearrange("p t u b -> p t b u"),
+                )
+            groups[grp]["grouped"] = grouped
+
+        def quantise_h0(grp):
+            h_codes = prepared.tile([P, GROUP * P], U32, align_bytes=64)
+            h_scales = prepared.tile([P, GROUP * P], U8, align_bytes=64)
+            nc.vector.quantize_mx(
+                out=h_codes[:].bitcast(FP8X4), scales=h_scales[:], in_=groups[grp]["grouped"][:]
+            )
+            groups[grp]["h_codes"] = h_codes
+            groups[grp]["h_scales"] = h_scales
+
+        def transpose_x(grp):
+            xT_ps = ps_misc.tile([V, GROUP, P], BF16, tag="misc")
+            for t in range(GROUP):
+                nc.tensor.transpose(out=xT_ps[:, t, :], in_=x_all[:, grp * GROUP + t, :], identity=ident_bf[:])
+            xT = prepared.tile([V, GROUP, P], F32)
+            nc.scalar.copy(out=xT[:], in_=xT_ps[:])
+            groups[grp]["xT"] = xT
+
+        def inverse_std_of_a(grp):
+            tiles = slice(grp * GROUP, (grp + 1) * GROUP)
+            xcov_ps = ps_misc.tile([P, GROUP, V], F32, tag="misc")
+            for t in range(GROUP):
+                nc.tensor.matmul(
+                    out=xcov_ps[:, t, :], lhsT=groups[grp]["xT"][:, t, :], rhs=cov[:], start=True, stop=True
+                )
+            xcovx = prepared.tile([P, GROUP, V], F32)
+            nc.vector.tensor_tensor(out=xcovx[:], in0=xcov_ps[:], in1=x_all[:, tiles, :], op=ALU.mult)
+            var_a = small.tile([P, GROUP], F32)
+            nc.vector.tensor_reduce(out=var_a[:], in_=xcovx[:], axis=AX.X, op=ALU.add)
+            groups[grp]["rstd_a"] = inverse_std(var_a[:], 1.0, GROUP)
+
+        def scale_x(grp):
+            tiles = slice(grp * GROUP, (grp + 1) * GROUP)
+            xhat = prepared.tile([P, GROUP, V], F32)
+            nc.vector.tensor_tensor(
+                out=xhat[:],
+                in0=x_all[:, tiles, :],
+                in1=groups[grp]["rstd_a"][:].unsqueeze(2).to_broadcast([P, GROUP, V]),
+                op=ALU.mult,
+            )
+            groups[grp]["xhat"] = xhat
+
+        def transpose_xhat(grp):
+            xhatT_ps = ps_misc.tile([V, GROUP, P], F32, tag="misc")
+            for t in range(GROUP):
+                nc.tensor.transpose(
+                    out=xhatT_ps[:, t, :], in_=groups[grp]["xhat"][:, t, :], identity=ident_f32[:]
+                )
+            xhatT = prepared.tile([V, GROUP, P], F32)
+            nc.scalar.copy(out=xhatT[:], in_=xhatT_ps[:])
+            groups[grp]["xhatT"] = xhatT
+
+        state = {}
+        gate_func = (ACT.Sigmoid, ACT.Sigmoid, ACT.Tanh, ACT.Sigmoid)
+
+        def bank(j):
+            return slice(j * BANK, (j + 1) * BANK)
+
+        def recurrent_bank(i, j):
+            if j == 0:
+                r = wide.tile([P, G], F32)
+                r_sums = small.tile([P, BANKS], F32)
+                state[i] = {"r": r, "r_sums": r_sums}
+            ops = groups[i // GROUP]
+            rows = slice((i % GROUP) * P, (i % GROUP + 1) * P)
+            r_ps = ps_r.tile([P, BANK], F32)
+            nc.tensor.matmul_mx(
+                out=r_ps[:],
+                lhsT=ops["h_codes"][:, rows].bitcast(FP8X4),
+                lhsT_scale=ops["h_scales"][:, rows],
+                rhs=w_words[:, 2 * j * BANK : 2 * (j + 1) * BANK].bitcast(FP4X4),
+                rhs_scale=w_scales[:, bank(j)],
+                start=True,
+                stop=True,
+            )
+            nc.scalar.activation(
+                out=state[i]["r"][:, bank(j)], in_=r_ps[:], func=ACT.Identity,
+                accum_out=state[i]["r_sums"][:, j : j + 1],
+            )
+
+        def mean_of_r(i):
+            r_parts = small.tile([P, BANKS], F32)
+            neg_mean_r = small.tile([P, 1], F32)
+            nc.vector.tensor_scalar(
+                out=r_parts[:], in0=state[i]["r_sums"][:], scalar1=-1.0 / G, scalar2=None,
+                op0=ALU.mult, op1=ALU.add, accum_out=neg_mean_r[:],
+            )
+            state[i]["neg_mean_r"] = neg_mean_r
+
+        def inverse_std_of_r(i):
+            squares = wide.tile([P, G], BF16)
+            r_sum_sq = small.tile([P, 1], F32)
+            nc.scalar.activation(
+                out=squares[:], in_=state[i]["r"][:], func=ACT.Square, bias=state[i]["neg_mean_r"][:],
+                accum_out=r_sum_sq[:],
+            )
+            state[i]["rstd_r"] = inverse_std(r_sum_sq[:], G, 1)
+
+        def gain_r(i):
+            r_gained = wide.tile([P, G], F32)
+            nc.vector.scalar_tensor_tensor(
+                out=r_gained[:], in0=state[i]["r"][:], scalar=state[i]["neg_mean_r"][:], in1=gain_h[:],
+                op0=ALU.add, op1=ALU.mult,
+            )
+            state[i]["r_gained"] = r_gained
+
+        def gate_bank(i, j):
+            if j == 0:
+                gates = gate_pool.tile([P, G], F32)
+                state[i]["gates"] = gates
+            x_ps = ps_x.tile([P, BANK], F32)
+            nc.tensor.matmul(
+                out=x_ps[:], lhsT=groups[i // GROUP]["xhatT"][:, i % GROUP, :], rhs=w_x[:, bank(j)],
+                start=True, stop=False,
+            )
+            for q in range(BANK // P):
+                col = j * (BANK // P) + q
+                nc.tensor.matmul(
+                    out=x_ps[:, q * P : (q + 1) * P],
+                    lhsT=bias_cols[:, col : col + 1].to_broadcast([P, P]),
+                    rhs=ident_f32[:],
+                    is_transpose=True,
+                    start=False,
+                    stop=(q == BANK // P - 1),
+                )
+            gate = state[i]["gates"][:, bank(j)]
+            nc.vector.scalar_tensor_tensor(
+                out=gate, in0=state[i]["r_gained"][:, bank(j)], scalar=state[i]["rstd_r"][:], in1=x_ps[:],
+                op0=ALU.mult, op1=ALU.add,
+            )
+            nc.scalar.activation(out=gate, in_=gate, func=gate_func[j])
+
+        def keep_old_cell(i):
+            kept = cell.tile([P, H], F32)
+            nc.vector.tensor_tensor(
+                out=kept[:], in0=state[i]["gates"][:, bank(1)], in1=groups[i // GROUP]["c0"][:, i % GROUP, :],
+                op=ALU.mult,
+            )
+            state[i]["kept"] = kept
+
+        def make_fresh_cell(i):
+            fresh = cell.tile([P, H], F32)
+            nc.vector.tensor_tensor(
+                out=fresh[:], in0=state[i]["gates"][:, bank(0)], in1=state[i]["gates"][:, bank(2)], op=ALU.mult
+            )
+            state[i]["fresh"] = fresh
+
+        def sum_cell(i):
+            c_new = cell.tile([P, H], F32)
+            c_sum = small.tile([P, 1], F32)
+            nc.vector.scalar_tensor_tensor(
+                out=c_new[:], in0=state[i]["kept"][:], scalar=1.0, in1=state[i]["fresh"][:],
+                op0=ALU.mult, op1=ALU.add, accum_out=c_sum[:],
+            )
+            neg_mean_c = small.tile([P, 1], F32)
+            nc.vector.tensor_scalar_mul(out=neg_mean_c[:], in0=c_sum[:], scalar1=-1.0 / H)
+            state[i]["c_new"] = c_new
+            state[i]["neg_mean_c"] = neg_mean_c
+
+        def inverse_std_of_cell(i):
+            c_squares = cell.tile([P, H], BF16)
+            c_sum_sq = small.tile([P, 1], F32)
+            nc.scalar.activation(
+                out=c_squares[:], in_=state[i]["c_new"][:], func=ACT.Square, bias=state[i]["neg_mean_c"][:],
+                accum_out=c_sum_sq[:],
+            )
+            state[i]["rstd_c"] = inverse_std(c_sum_sq[:], H, 1)
+
+        def gain_cell(i):
+            c_gained = cell.tile([P, H], F32)
+            nc.vector.scalar_tensor_tensor(
+                out=c_gained[:], in0=state[i]["c_new"][:], scalar=state[i]["neg_mean_c"][:], in1=gain_c[:],
+                op0=ALU.add, op1=ALU.mult,
+            )
+            state[i]["c_gained"] = c_gained
+
+        def finish_cy(i):
+            cy = result.tile([P, H], F32)
+            nc.vector.scalar_tensor_tensor(
+                out=cy[:], in0=state[i]["c_gained"][:], scalar=state[i]["rstd_c"][:], in1=bias_c[:],
+                op0=ALU.mult, op1=ALU.add,
+            )
+            nc.sync.dma_start(out=cy_rows[:, i, :], in_=cy[:])
+            state[i]["cy"] = cy
+
+        def tanh_of_cy(i):
+            tanh_cy = cell.tile([P, H], F32)
+            nc.scalar.activation(out=tanh_cy[:], in_=state[i]["cy"][:], func=ACT.Tanh)
+            state[i]["tanh_cy"] = tanh_cy
+
+        def finish_hy(i):
+            hy = result.tile([P, H], F32)
+            nc.vector.tensor_tensor(
+                out=hy[:], in0=state[i]["gates"][:, bank(3)], in1=state[i]["tanh_cy"][:], op=ALU.mult
+            )
+            nc.sync.dma_start(out=hy_rows[:, i, :], in_=hy[:])
+
+        def is_tile(i):
+            return 0 <= i < ROW_TILES
+
+        load_group(0)
+        load_group(1)
+        transpose_h0(0)
+        quantise_h0(0)
+        transpose_x(0)
+        inverse_std_of_a(0)
+        scale_x(0)
+        transpose_xhat(0)
+
+        with tc.manual_schedule():
+            for step in range(ROW_TILES + 2):
+                first, second, third = step, step - 1, step - 2
+                phase, coming = step % GROUP, step // GROUP + 1
+                prepare = coming < N_GROUPS
+                if prepare and phase == 3:
+                    scale_x(coming)
+                for j in range(BANKS):
+                    if is_tile(first):
+                        recurrent_bank(first, j)
+                    if is_tile(second):
+                        gate_bank(second, j)
+                if is_tile(second):
+                    keep_old_cell(second)
+                if is_tile(third):
+                    finish_cy(third)
+                if is_tile(second):
+                    make_fresh_cell(second)
+                if is_tile(first):
+                    mean_of_r(first)
+                    inverse_std_of_r(first)
+                if is_tile(second):
+                    sum_cell(second)
+                    inverse_std_of_cell(second)
+                if is_tile(third):
+                    tanh_of_cy(third)
+                if is_tile(first):
+                    gain_r(first)
+                if is_tile(second):
+                    gain_cell(second)
+                if is_tile(third):
+                    finish_hy(third)
+                if prepare and phase == 0:
+                    transpose_h0(coming)
+                if prepare and phase == 1:
+                    quantise_h0(coming)
+                    transpose_x(coming)
+                if prepare and phase == 2:
+                    inverse_std_of_a(coming)
+                    if coming + 1 < N_GROUPS:
+                        load_group(coming + 1)
+                if prepare and phase == 3:
+                    transpose_xhat(coming)

@@ -25,6 +25,8 @@ ROW_TILES = B // P
 GROUP = 4
 N_GROUPS = ROW_TILES // GROUP
 W_TILES = G // P
+AHEAD = 3
+assert BANKS == AHEAD + 1
 
 FLOPS = 2 * B * G * (V + H)
 
@@ -60,12 +62,12 @@ def tile_multilstm_pa_t_kernel(
         stream = ctx.enter_context(tc.tile_pool(name="stream", bufs=3))
         prepared = ctx.enter_context(tc.tile_pool(name="prepared", bufs=2))
         wide = ctx.enter_context(tc.tile_pool(name="wide", bufs=2))
-        gate_pool = ctx.enter_context(tc.tile_pool(name="gate_pool", bufs=3))
+        gate_pool = ctx.enter_context(tc.tile_pool(name="gate_pool", bufs=4))
         cell = ctx.enter_context(tc.tile_pool(name="cell", bufs=2))
         result = ctx.enter_context(tc.tile_pool(name="result", bufs=3))
         small = ctx.enter_context(tc.tile_pool(name="small", bufs=8))
-        ps_r = ctx.enter_context(tc.psum_pool(name="ps_r", bufs=3))
-        ps_x = ctx.enter_context(tc.psum_pool(name="ps_x", bufs=3))
+        ps_r = ctx.enter_context(tc.psum_pool(name="ps_r", bufs=AHEAD))
+        ps_x = ctx.enter_context(tc.psum_pool(name="ps_x", bufs=AHEAD))
         ps_misc = ctx.enter_context(tc.psum_pool(name="ps_misc", bufs=2))
 
         w_nat = setup.tile([P, W_TILES, V], BF16)
@@ -184,22 +186,20 @@ def tile_multilstm_pa_t_kernel(
             nc.sync.dma_start(out=c0_grp[:], in_=c0_rows[:, tiles, :])
             groups[grp] = {"h0": h0_grp, "c0": c0_grp}
 
-        def transpose_h0(grp):
-            grouped = prepared.tile([P, GROUP * P * PACK], BF16, align_bytes=64)
-            grouped_words = grouped[:].bitcast(F32).rearrange("p (t b u) -> p t b u", t=GROUP, u=2)
-            for half in range(2):
-                hT_ps = ps_misc.tile([P, 2, 2, P], F32, tag="misc")
-                for t in range(2):
-                    words = groups[grp]["h0"][:, 2 * half + t, :].bitcast(F32)
-                    for u in range(2):
-                        nc.tensor.transpose(
-                            out=hT_ps[:, t, u, :], in_=words[:, u : H // 2 : 2], identity=ident_f32[:]
-                        )
-                nc.scalar.copy(
-                    out=grouped_words[:, 2 * half : 2 * half + 2, :, :],
-                    in_=hT_ps[:].rearrange("p t u b -> p t b u"),
-                )
-            groups[grp]["grouped"] = grouped
+        def transpose_h0(grp, half):
+            if half == 0:
+                grouped = prepared.tile([P, GROUP * P * PACK], BF16, align_bytes=64)
+                groups[grp]["grouped"] = grouped
+            grouped_words = groups[grp]["grouped"][:].bitcast(F32).rearrange("p (t b u) -> p t b u", t=GROUP, u=2)
+            hT_ps = ps_misc.tile([P, 2, 2, P], F32, tag="misc")
+            for t in range(2):
+                words = groups[grp]["h0"][:, 2 * half + t, :].bitcast(F32)
+                for u in range(2):
+                    nc.tensor.transpose(out=hT_ps[:, t, u, :], in_=words[:, u : H // 2 : 2], identity=ident_f32[:])
+            nc.scalar.copy(
+                out=grouped_words[:, 2 * half : 2 * half + 2, :, :],
+                in_=hT_ps[:].rearrange("p t u b -> p t b u"),
+            )
 
         def quantise_h0(grp):
             h_codes = prepared.tile([P, GROUP * P], U32, align_bytes=64)
@@ -258,11 +258,7 @@ def tile_multilstm_pa_t_kernel(
         def bank(j):
             return slice(j * BANK, (j + 1) * BANK)
 
-        def recurrent_bank(i, j):
-            if j == 0:
-                r = wide.tile([P, G], F32)
-                r_sums = small.tile([P, BANKS], F32)
-                state[i] = {"r": r, "r_sums": r_sums}
+        def recurrent_matmul(i, j):
             ops = groups[i // GROUP]
             rows = slice((i % GROUP) * P, (i % GROUP + 1) * P)
             r_ps = ps_r.tile([P, BANK], F32)
@@ -275,8 +271,18 @@ def tile_multilstm_pa_t_kernel(
                 start=True,
                 stop=True,
             )
+            if j == 0:
+                state[i] = {}
+            state[i]["r_ps", j] = r_ps
+
+        def recurrent_out(i, j):
+            if j == 0:
+                r = wide.tile([P, G], F32)
+                r_sums = small.tile([P, BANKS], F32)
+                state[i]["r"] = r
+                state[i]["r_sums"] = r_sums
             nc.scalar.activation(
-                out=state[i]["r"][:, bank(j)], in_=r_ps[:], func=ACT.Identity,
+                out=state[i]["r"][:, bank(j)], in_=state[i]["r_ps", j][:], func=ACT.Identity,
                 accum_out=state[i]["r_sums"][:, j : j + 1],
             )
 
@@ -290,7 +296,7 @@ def tile_multilstm_pa_t_kernel(
             state[i]["neg_mean_r"] = neg_mean_r
 
         def inverse_std_of_r(i):
-            squares = wide.tile([P, G], BF16)
+            squares = wide.tile([P, G], BF16, bufs=1)
             r_sum_sq = small.tile([P, 1], F32)
             nc.scalar.activation(
                 out=squares[:], in_=state[i]["r"][:], func=ACT.Square, bias=state[i]["neg_mean_r"][:],
@@ -306,10 +312,7 @@ def tile_multilstm_pa_t_kernel(
             )
             state[i]["r_gained"] = r_gained
 
-        def gate_bank(i, j):
-            if j == 0:
-                gates = gate_pool.tile([P, G], F32)
-                state[i]["gates"] = gates
+        def x_side_matmul(i, j):
             x_ps = ps_x.tile([P, BANK], F32)
             nc.tensor.matmul(
                 out=x_ps[:], lhsT=groups[i // GROUP]["xhatT"][:, i % GROUP, :], rhs=w_x[:, bank(j)],
@@ -325,11 +328,19 @@ def tile_multilstm_pa_t_kernel(
                     start=False,
                     stop=(q == BANK // P - 1),
                 )
-            gate = state[i]["gates"][:, bank(j)]
+            state[i]["x_ps", j] = x_ps
+
+        def add_sides(i, j):
+            if j == 0:
+                gates = gate_pool.tile([P, G], F32)
+                state[i]["gates"] = gates
             nc.vector.scalar_tensor_tensor(
-                out=gate, in0=state[i]["r_gained"][:, bank(j)], scalar=state[i]["rstd_r"][:], in1=x_ps[:],
-                op0=ALU.mult, op1=ALU.add,
+                out=state[i]["gates"][:, bank(j)], in0=state[i]["r_gained"][:, bank(j)],
+                scalar=state[i]["rstd_r"][:], in1=state[i]["x_ps", j][:], op0=ALU.mult, op1=ALU.add,
             )
+
+        def gate_activation(i, j):
+            gate = state[i]["gates"][:, bank(j)]
             nc.scalar.activation(out=gate, in_=gate, func=gate_func[j])
 
         def keep_old_cell(i):
@@ -397,58 +408,64 @@ def tile_multilstm_pa_t_kernel(
             )
             nc.sync.dma_start(out=hy_rows[:, i, :], in_=hy[:])
 
-        def is_tile(i):
-            return 0 <= i < ROW_TILES
-
         load_group(0)
         load_group(1)
-        transpose_h0(0)
+        transpose_h0(0, 0)
+        transpose_h0(0, 1)
         quantise_h0(0)
         transpose_x(0)
         inverse_std_of_a(0)
         scale_x(0)
         transpose_xhat(0)
 
+        def piece_of(step, lag, piece, *args):
+            i = step - lag
+            if 0 <= i < ROW_TILES:
+                piece(i, *args)
+
         with tc.manual_schedule():
-            for step in range(ROW_TILES + 2):
-                first, second, third = step, step - 1, step - 2
-                phase, coming = step % GROUP, step // GROUP + 1
-                prepare = coming < N_GROUPS
-                if prepare and phase == 3:
-                    scale_x(coming)
+            for step in range(ROW_TILES + 5):
+                for j in range(AHEAD):
+                    piece_of(step, 0, recurrent_matmul, j)
+                for j in range(AHEAD):
+                    piece_of(step, 2, x_side_matmul, j)
+                piece_of(step, 0, recurrent_out, 0)
+                piece_of(step, 0, recurrent_matmul, AHEAD)
+                piece_of(step, 2, add_sides, 0)
+                piece_of(step, 2, x_side_matmul, AHEAD)
+                for j in range(1, BANKS):
+                    piece_of(step, 0, recurrent_out, j)
+                for j in range(1, AHEAD):
+                    piece_of(step, 2, add_sides, j)
+                piece_of(step, 3, sum_cell)
+                piece_of(step, 4, finish_cy)
+                piece_of(step, 0, mean_of_r)
+                piece_of(step, 2, add_sides, AHEAD)
+                piece_of(step, 1, inverse_std_of_r)
                 for j in range(BANKS):
-                    if is_tile(first):
-                        recurrent_bank(first, j)
-                    if is_tile(second):
-                        gate_bank(second, j)
-                if is_tile(second):
-                    keep_old_cell(second)
-                if is_tile(third):
-                    finish_cy(third)
-                if is_tile(second):
-                    make_fresh_cell(second)
-                if is_tile(first):
-                    mean_of_r(first)
-                    inverse_std_of_r(first)
-                if is_tile(second):
-                    sum_cell(second)
-                    inverse_std_of_cell(second)
-                if is_tile(third):
-                    tanh_of_cy(third)
-                if is_tile(first):
-                    gain_r(first)
-                if is_tile(second):
-                    gain_cell(second)
-                if is_tile(third):
-                    finish_hy(third)
-                if prepare and phase == 0:
-                    transpose_h0(coming)
-                if prepare and phase == 1:
+                    piece_of(step, 2, gate_activation, j)
+                piece_of(step, 3, inverse_std_of_cell)
+                piece_of(step, 4, tanh_of_cy)
+                piece_of(step, 1, gain_r)
+                piece_of(step, 3, gain_cell)
+                piece_of(step, 5, finish_hy)
+
+                phase, current = step % GROUP, step // GROUP
+                coming = current + 1
+                if coming < N_GROUPS and phase == 2:
                     quantise_h0(coming)
+                if coming < N_GROUPS and phase == 3:
+                    scale_x(coming)
+                piece_of(step, 2, keep_old_cell)
+                piece_of(step, 2, make_fresh_cell)
+                if 0 < current < N_GROUPS and phase == 0:
+                    transpose_xhat(current)
+                if coming < N_GROUPS and phase == 0:
+                    transpose_h0(coming, 0)
+                if coming < N_GROUPS and phase == 1:
+                    transpose_h0(coming, 1)
                     transpose_x(coming)
-                if prepare and phase == 2:
+                if coming < N_GROUPS and phase == 2:
                     inverse_std_of_a(coming)
-                    if coming + 1 < N_GROUPS:
-                        load_group(coming + 1)
-                if prepare and phase == 3:
-                    transpose_xhat(coming)
+                if coming + 1 < N_GROUPS and phase == 2:
+                    load_group(coming + 1)

@@ -70,8 +70,31 @@ def tile_multilstm_pa_t_kernel(
         ps_x = ctx.enter_context(tc.psum_pool(name="ps_x", bufs=AHEAD))
         ps_misc = ctx.enter_context(tc.psum_pool(name="ps_misc", bufs=2))
 
+        groups = {}
+
+        def load_h0(grp):
+            h0_grp = stream.tile([P, GROUP, H], BF16)
+            nc.sync.dma_start(out=h0_grp[:], in_=h0_rows[:, grp * GROUP : (grp + 1) * GROUP, :])
+            groups[grp] = {"h0": h0_grp}
+
+        def load_c0(grp):
+            c0_grp = stream.tile([P, GROUP, H], BF16)
+            nc.sync.dma_start(out=c0_grp[:], in_=c0_rows[:, grp * GROUP : (grp + 1) * GROUP, :])
+            groups[grp]["c0"] = c0_grp
+
         w_nat = setup.tile([P, W_TILES, V], BF16)
         nc.sync.dma_start(out=w_nat[:], in_=w_ih1.rearrange("(t p) v -> p t v", p=P))
+        load_h0(0)
+
+        w_words = const.tile([P, 2 * G], U8, align_bytes=64)
+        nc.sync.dma_start(out=w_words[:].bitcast(I32), in_=w_hh1_words[0].bitcast(I32))
+        w_scales = const.tile([P, G], U8, align_bytes=64)
+        nc.vector.memset(w_scales[:].bitcast(I32), 0)
+        for quad in range(4):
+            nc.sync.dma_start(
+                out=w_scales[32 * quad : 32 * quad + 4, :].bitcast(I32),
+                in_=w_hh1_scales[0, 4 * quad : 4 * quad + 4, :].bitcast(I32),
+            )
 
         vec_rows = setup.tile([P, P], BF16)
         nc.vector.memset(vec_rows[:], 0.0)
@@ -84,18 +107,11 @@ def tile_multilstm_pa_t_kernel(
         x_all = const.tile([P, ROW_TILES, V], BF16)
         nc.sync.dma_start(out=x_all[:], in_=x_rows)
 
-        w_words = const.tile([P, 2 * G], U8, align_bytes=64)
-        nc.sync.dma_start(out=w_words[:].bitcast(I32), in_=w_hh1_words[0].bitcast(I32))
-        w_scales = const.tile([P, G], U8, align_bytes=64)
-        nc.vector.memset(w_scales[:].bitcast(I32), 0)
-        for quad in range(4):
-            nc.sync.dma_start(
-                out=w_scales[32 * quad : 32 * quad + 4, :].bitcast(I32),
-                in_=w_hh1_scales[0, 4 * quad : 4 * quad + 4, :].bitcast(I32),
-            )
-
         gain_h = const.tile([P, G], BF16)
         nc.sync.dma_start(out=gain_h[:], in_=lnh_w1.partition_broadcast(P))
+        load_c0(0)
+        load_h0(1)
+        load_c0(1)
         gain_c = const.tile([P, H], BF16)
         nc.sync.dma_start(out=gain_c[:], in_=lnc_w1.partition_broadcast(P))
         bias_c = const.tile([P, H], BF16)
@@ -109,6 +125,8 @@ def tile_multilstm_pa_t_kernel(
         nc.vector.memset(ones_bf[:], 1.0)
         neg_half = const.tile([P, GROUP], F32)
         nc.vector.memset(neg_half[:], -0.5)
+        table_warmer = const.tile([P, 1], F32)
+        nc.scalar.activation(out=table_warmer[:], in_=neg_half[:, 0:1], func=ACT.Sigmoid)
 
         def inverse_std(sum_sq, count, width):
             var_eps = small.tile([P, width], F32)
@@ -118,73 +136,6 @@ def tile_multilstm_pa_t_kernel(
             rstd = small.tile([P, width], F32)
             nc.gpsimd.tensor_tensor(out=rstd[:], in0=var_eps[:], in1=neg_half[:, 0:width], op=ALU.pow)
             return rstd
-
-        vec_ps = ps_misc.tile([P, P], BF16, tag="misc")
-        nc.tensor.transpose(out=vec_ps[:], in_=vec_rows[:], identity=ident_bf[:])
-        vec_cols = const.tile([P, 3 * W_TILES], F32)
-        nc.vector.tensor_copy(out=vec_cols[:], in_=vec_ps[:, 0 : 3 * W_TILES])
-        gain_i_cols = vec_cols[:, 0:W_TILES]
-        bias_cols = const.tile([P, W_TILES], F32)
-        nc.vector.tensor_tensor(
-            out=bias_cols[:],
-            in0=vec_cols[:, W_TILES : 2 * W_TILES],
-            in1=vec_cols[:, 2 * W_TILES : 3 * W_TILES],
-            op=ALU.add,
-        )
-
-        wsum_ps = ps_misc.tile([P, V], F32, tag="misc")
-        for t in range(W_TILES):
-            nc.tensor.matmul(
-                out=wsum_ps[:], lhsT=ones_bf[:], rhs=w_nat[:, t, :], start=(t == 0), stop=(t == W_TILES - 1)
-            )
-        w_centred = setup.tile([P, W_TILES, V], F32)
-        nc.vector.scalar_tensor_tensor(
-            out=w_centred[:],
-            in0=wsum_ps[:].unsqueeze(1).to_broadcast([P, W_TILES, V]),
-            scalar=-1.0 / G,
-            in1=w_nat[:],
-            op0=ALU.mult,
-            op1=ALU.add,
-        )
-        cov_ps = ps_misc.tile([V, V], F32, tag="misc")
-        for t in range(W_TILES):
-            nc.tensor.matmul(
-                out=cov_ps[:],
-                lhsT=w_centred[:, t, :],
-                rhs=w_centred[:, t, :],
-                start=(t == 0),
-                stop=(t == W_TILES - 1),
-            )
-        cov = const.tile([V, V], F32)
-        nc.scalar.mul(out=cov[:], in_=cov_ps[:], mul=1.0 / G)
-
-        w_gained = setup.tile([P, W_TILES, V], F32)
-        nc.vector.tensor_tensor(
-            out=w_gained[:],
-            in0=w_centred[:],
-            in1=gain_i_cols.unsqueeze(2).to_broadcast([P, W_TILES, V]),
-            op=ALU.mult,
-        )
-        w_x = const.tile([V, G], F32)
-        for j in range(BANKS):
-            wt_ps = ps_misc.tile([V, BANK], F32, tag="misc")
-            for q in range(BANK // P):
-                nc.tensor.transpose(
-                    out=wt_ps[:, q * P : (q + 1) * P],
-                    in_=w_gained[:, j * (BANK // P) + q, :],
-                    identity=ident_f32[:],
-                )
-            nc.scalar.copy(out=w_x[:, j * BANK : (j + 1) * BANK], in_=wt_ps[:])
-
-        groups = {}
-
-        def load_group(grp):
-            tiles = slice(grp * GROUP, (grp + 1) * GROUP)
-            h0_grp = stream.tile([P, GROUP, H], BF16)
-            nc.sync.dma_start(out=h0_grp[:], in_=h0_rows[:, tiles, :])
-            c0_grp = stream.tile([P, GROUP, H], BF16)
-            nc.sync.dma_start(out=c0_grp[:], in_=c0_rows[:, tiles, :])
-            groups[grp] = {"h0": h0_grp, "c0": c0_grp}
 
         def transpose_h0(grp, half):
             if half == 0:
@@ -251,6 +202,67 @@ def tile_multilstm_pa_t_kernel(
             xhatT = prepared.tile([V, GROUP, P], F32)
             nc.scalar.copy(out=xhatT[:], in_=xhatT_ps[:])
             groups[grp]["xhatT"] = xhatT
+
+        transpose_h0(0, 0)
+        transpose_h0(0, 1)
+        quantise_h0(0)
+
+        vec_ps = ps_misc.tile([P, P], BF16, tag="misc")
+        nc.tensor.transpose(out=vec_ps[:], in_=vec_rows[:], identity=ident_bf[:])
+        vec_cols = const.tile([P, 3 * W_TILES], F32)
+        nc.vector.tensor_copy(out=vec_cols[:], in_=vec_ps[:, 0 : 3 * W_TILES])
+        gain_i_cols = vec_cols[:, 0:W_TILES]
+        bias_cols = const.tile([P, W_TILES], F32)
+        nc.vector.tensor_tensor(
+            out=bias_cols[:],
+            in0=vec_cols[:, W_TILES : 2 * W_TILES],
+            in1=vec_cols[:, 2 * W_TILES : 3 * W_TILES],
+            op=ALU.add,
+        )
+
+        wsum_ps = ps_misc.tile([P, V], F32, tag="misc")
+        for t in range(W_TILES):
+            nc.tensor.matmul(
+                out=wsum_ps[:], lhsT=ones_bf[:], rhs=w_nat[:, t, :], start=(t == 0), stop=(t == W_TILES - 1)
+            )
+        w_centred = setup.tile([P, W_TILES, V], F32)
+        nc.vector.scalar_tensor_tensor(
+            out=w_centred[:],
+            in0=wsum_ps[:].unsqueeze(1).to_broadcast([P, W_TILES, V]),
+            scalar=-1.0 / G,
+            in1=w_nat[:],
+            op0=ALU.mult,
+            op1=ALU.add,
+        )
+        cov_ps = ps_misc.tile([V, V], F32, tag="misc")
+        for t in range(W_TILES):
+            nc.tensor.matmul(
+                out=cov_ps[:],
+                lhsT=w_centred[:, t, :],
+                rhs=w_centred[:, t, :],
+                start=(t == 0),
+                stop=(t == W_TILES - 1),
+            )
+        cov = const.tile([V, V], F32)
+        nc.scalar.mul(out=cov[:], in_=cov_ps[:], mul=1.0 / G)
+
+        w_gained = setup.tile([P, W_TILES, V], F32)
+        nc.vector.tensor_tensor(
+            out=w_gained[:],
+            in0=w_centred[:],
+            in1=gain_i_cols.unsqueeze(2).to_broadcast([P, W_TILES, V]),
+            op=ALU.mult,
+        )
+        w_x = const.tile([V, G], F32)
+        for j in range(BANKS):
+            wt_ps = ps_misc.tile([V, BANK], F32, tag="misc")
+            for q in range(BANK // P):
+                nc.tensor.transpose(
+                    out=wt_ps[:, q * P : (q + 1) * P],
+                    in_=w_gained[:, j * (BANK // P) + q, :],
+                    identity=ident_f32[:],
+                )
+            nc.scalar.copy(out=w_x[:, j * BANK : (j + 1) * BANK], in_=wt_ps[:])
 
         state = {}
         gate_func = (ACT.Sigmoid, ACT.Sigmoid, ACT.Tanh, ACT.Sigmoid)
@@ -365,9 +377,12 @@ def tile_multilstm_pa_t_kernel(
                 out=c_new[:], in0=state[i]["kept"][:], scalar=1.0, in1=state[i]["fresh"][:],
                 op0=ALU.mult, op1=ALU.add, accum_out=c_sum[:],
             )
-            neg_mean_c = small.tile([P, 1], F32)
-            nc.vector.tensor_scalar_mul(out=neg_mean_c[:], in0=c_sum[:], scalar1=-1.0 / H)
             state[i]["c_new"] = c_new
+            state[i]["c_sum"] = c_sum
+
+        def mean_of_cell(i):
+            neg_mean_c = small.tile([P, 1], F32)
+            nc.vector.tensor_scalar_mul(out=neg_mean_c[:], in0=state[i]["c_sum"][:], scalar1=-1.0 / H)
             state[i]["neg_mean_c"] = neg_mean_c
 
         def inverse_std_of_cell(i):
@@ -408,11 +423,6 @@ def tile_multilstm_pa_t_kernel(
             )
             nc.sync.dma_start(out=hy_rows[:, i, :], in_=hy[:])
 
-        load_group(0)
-        load_group(1)
-        transpose_h0(0, 0)
-        transpose_h0(0, 1)
-        quantise_h0(0)
         transpose_x(0)
         inverse_std_of_a(0)
         scale_x(0)
@@ -439,6 +449,7 @@ def tile_multilstm_pa_t_kernel(
                     piece_of(step, 2, add_sides, j)
                 piece_of(step, 3, sum_cell)
                 piece_of(step, 4, finish_cy)
+                piece_of(step, 3, mean_of_cell)
                 piece_of(step, 0, mean_of_r)
                 piece_of(step, 2, add_sides, AHEAD)
                 piece_of(step, 1, inverse_std_of_r)
@@ -468,4 +479,5 @@ def tile_multilstm_pa_t_kernel(
                 if coming < N_GROUPS and phase == 2:
                     inverse_std_of_a(coming)
                 if coming + 1 < N_GROUPS and phase == 2:
-                    load_group(coming + 1)
+                    load_h0(coming + 1)
+                    load_c0(coming + 1)

@@ -25,8 +25,10 @@ ROW_TILES = B // P
 GROUP = 4
 N_GROUPS = ROW_TILES // GROUP
 W_TILES = G // P
-AHEAD = 3
-assert BANKS == AHEAD + 1
+X_BANKS = 3
+VECTOR_BANKS = (0,)
+SCALAR_BANKS = (1, 2, 3)
+STAT_WIDTH = 6 * len(VECTOR_BANKS) + 3 * len(SCALAR_BANKS)
 
 FLOPS = 2 * B * G * (V + H)
 
@@ -62,13 +64,13 @@ def tile_multilstm_pa_t_kernel(
         stream = ctx.enter_context(tc.tile_pool(name="stream", bufs=3))
         prepared = ctx.enter_context(tc.tile_pool(name="prepared", bufs=2))
         wide = ctx.enter_context(tc.tile_pool(name="wide", bufs=2))
-        gate_pool = ctx.enter_context(tc.tile_pool(name="gate_pool", bufs=4))
-        cell = ctx.enter_context(tc.tile_pool(name="cell", bufs=2))
+        gate_pool = ctx.enter_context(tc.tile_pool(name="gate_pool", bufs=5))
+        cell = ctx.enter_context(tc.tile_pool(name="cell", bufs=3))
         result = ctx.enter_context(tc.tile_pool(name="result", bufs=3))
         small = ctx.enter_context(tc.tile_pool(name="small", bufs=8))
-        ps_r = ctx.enter_context(tc.psum_pool(name="ps_r", bufs=AHEAD))
-        ps_x = ctx.enter_context(tc.psum_pool(name="ps_x", bufs=AHEAD))
-        ps_misc = ctx.enter_context(tc.psum_pool(name="ps_misc", bufs=2))
+        ps_r = ctx.enter_context(tc.psum_pool(name="ps_r", bufs=BANKS))
+        ps_x = ctx.enter_context(tc.psum_pool(name="ps_x", bufs=X_BANKS))
+        ps_misc = ctx.enter_context(tc.psum_pool(name="ps_misc", bufs=1))
 
         groups = {}
 
@@ -127,6 +129,13 @@ def tile_multilstm_pa_t_kernel(
         nc.vector.memset(neg_half[:], -0.5)
         table_warmer = const.tile([P, 1], F32)
         nc.scalar.activation(out=table_warmer[:], in_=neg_half[:, 0:1], func=ACT.Sigmoid)
+        r_stats_tiles = []
+        for k in range(3):
+            r_stats = const.tile([P, STAT_WIDTH], F32, name="r_stats%d" % k)
+            for n in range(len(SCALAR_BANKS)):
+                col = 6 * len(VECTOR_BANKS) + 3 * n
+                nc.vector.memset(r_stats[:, col : col + 1], float(BANK))
+            r_stats_tiles.append(r_stats)
 
         def inverse_std(sum_sq, count, width):
             var_eps = small.tile([P, width], F32)
@@ -137,19 +146,22 @@ def tile_multilstm_pa_t_kernel(
             nc.gpsimd.tensor_tensor(out=rstd[:], in0=var_eps[:], in1=neg_half[:, 0:width], op=ALU.pow)
             return rstd
 
-        def transpose_h0(grp, half):
+        def transpose_h0(grp, half, banks):
             if half == 0:
                 grouped = prepared.tile([P, GROUP * P * PACK], BF16, align_bytes=64)
                 groups[grp]["grouped"] = grouped
-            grouped_words = groups[grp]["grouped"][:].bitcast(F32).rearrange("p (t b u) -> p t b u", t=GROUP, u=2)
-            hT_ps = ps_misc.tile([P, 2, 2, P], F32, tag="misc")
+            hT_ps = banks.tile([P, 2, 2, P], F32, tag="bank")
             for t in range(2):
                 words = groups[grp]["h0"][:, 2 * half + t, :].bitcast(F32)
                 for u in range(2):
                     nc.tensor.transpose(out=hT_ps[:, t, u, :], in_=words[:, u : H // 2 : 2], identity=ident_f32[:])
+            groups[grp]["hT_ps"] = hT_ps
+
+        def copy_h0(grp, half):
+            grouped_words = groups[grp]["grouped"][:].bitcast(F32).rearrange("p (t b u) -> p t b u", t=GROUP, u=2)
             nc.scalar.copy(
                 out=grouped_words[:, 2 * half : 2 * half + 2, :, :],
-                in_=hT_ps[:].rearrange("p t u b -> p t b u"),
+                in_=groups[grp]["hT_ps"][:].rearrange("p t u b -> p t b u"),
             )
 
         def quantise_h0(grp):
@@ -161,26 +173,35 @@ def tile_multilstm_pa_t_kernel(
             groups[grp]["h_codes"] = h_codes
             groups[grp]["h_scales"] = h_scales
 
-        def transpose_x(grp):
-            xT_ps = ps_misc.tile([V, GROUP, P], BF16, tag="misc")
+        def transpose_x(grp, banks):
+            xT_ps = banks.tile([V, GROUP, P], BF16, tag="bank")
             for t in range(GROUP):
                 nc.tensor.transpose(out=xT_ps[:, t, :], in_=x_all[:, grp * GROUP + t, :], identity=ident_bf[:])
+            groups[grp]["xT_ps"] = xT_ps
+
+        def copy_xT(grp):
             xT = prepared.tile([V, GROUP, P], F32)
-            nc.scalar.copy(out=xT[:], in_=xT_ps[:])
+            nc.scalar.copy(out=xT[:], in_=groups[grp]["xT_ps"][:])
             groups[grp]["xT"] = xT
 
-        def inverse_std_of_a(grp):
-            tiles = slice(grp * GROUP, (grp + 1) * GROUP)
-            xcov_ps = ps_misc.tile([P, GROUP, V], F32, tag="misc")
+        def x_times_cov(grp, banks):
+            xcov_ps = banks.tile([P, GROUP, V], F32, tag="bank")
             for t in range(GROUP):
                 nc.tensor.matmul(
                     out=xcov_ps[:, t, :], lhsT=groups[grp]["xT"][:, t, :], rhs=cov[:], start=True, stop=True
                 )
+            groups[grp]["xcov_ps"] = xcov_ps
+
+        def variance_of_a(grp):
+            tiles = slice(grp * GROUP, (grp + 1) * GROUP)
             xcovx = prepared.tile([P, GROUP, V], F32)
-            nc.vector.tensor_tensor(out=xcovx[:], in0=xcov_ps[:], in1=x_all[:, tiles, :], op=ALU.mult)
+            nc.vector.tensor_tensor(out=xcovx[:], in0=groups[grp]["xcov_ps"][:], in1=x_all[:, tiles, :], op=ALU.mult)
             var_a = small.tile([P, GROUP], F32)
             nc.vector.tensor_reduce(out=var_a[:], in_=xcovx[:], axis=AX.X, op=ALU.add)
-            groups[grp]["rstd_a"] = inverse_std(var_a[:], 1.0, GROUP)
+            groups[grp]["var_a"] = var_a
+
+        def inverse_std_of_a(grp):
+            groups[grp]["rstd_a"] = inverse_std(groups[grp]["var_a"][:], 1.0, GROUP)
 
         def scale_x(grp):
             tiles = slice(grp * GROUP, (grp + 1) * GROUP)
@@ -193,21 +214,26 @@ def tile_multilstm_pa_t_kernel(
             )
             groups[grp]["xhat"] = xhat
 
-        def transpose_xhat(grp):
-            xhatT_ps = ps_misc.tile([V, GROUP, P], F32, tag="misc")
+        def transpose_xhat(grp, banks):
+            xhatT_ps = banks.tile([V, GROUP, P], F32, tag="bank")
             for t in range(GROUP):
                 nc.tensor.transpose(
                     out=xhatT_ps[:, t, :], in_=groups[grp]["xhat"][:, t, :], identity=ident_f32[:]
                 )
+            groups[grp]["xhatT_ps"] = xhatT_ps
+
+        def copy_xhatT(grp):
             xhatT = prepared.tile([V, GROUP, P], F32)
-            nc.scalar.copy(out=xhatT[:], in_=xhatT_ps[:])
+            nc.scalar.copy(out=xhatT[:], in_=groups[grp]["xhatT_ps"][:])
             groups[grp]["xhatT"] = xhatT
 
-        transpose_h0(0, 0)
-        transpose_h0(0, 1)
+        transpose_h0(0, 0, ps_x)
+        copy_h0(0, 0)
+        transpose_h0(0, 1, ps_x)
+        copy_h0(0, 1)
         quantise_h0(0)
 
-        vec_ps = ps_misc.tile([P, P], BF16, tag="misc")
+        vec_ps = ps_x.tile([P, P], BF16, tag="bank")
         nc.tensor.transpose(out=vec_ps[:], in_=vec_rows[:], identity=ident_bf[:])
         vec_cols = const.tile([P, 3 * W_TILES], F32)
         nc.vector.tensor_copy(out=vec_cols[:], in_=vec_ps[:, 0 : 3 * W_TILES])
@@ -220,7 +246,7 @@ def tile_multilstm_pa_t_kernel(
             op=ALU.add,
         )
 
-        wsum_ps = ps_misc.tile([P, V], F32, tag="misc")
+        wsum_ps = ps_x.tile([P, V], F32, tag="bank")
         for t in range(W_TILES):
             nc.tensor.matmul(
                 out=wsum_ps[:], lhsT=ones_bf[:], rhs=w_nat[:, t, :], start=(t == 0), stop=(t == W_TILES - 1)
@@ -234,7 +260,7 @@ def tile_multilstm_pa_t_kernel(
             op0=ALU.mult,
             op1=ALU.add,
         )
-        cov_ps = ps_misc.tile([V, V], F32, tag="misc")
+        cov_ps = ps_x.tile([V, V], F32, tag="bank")
         for t in range(W_TILES):
             nc.tensor.matmul(
                 out=cov_ps[:],
@@ -255,7 +281,7 @@ def tile_multilstm_pa_t_kernel(
         )
         w_x = const.tile([V, G], F32)
         for j in range(BANKS):
-            wt_ps = ps_misc.tile([V, BANK], F32, tag="misc")
+            wt_ps = ps_x.tile([V, BANK], F32, tag="bank")
             for q in range(BANK // P):
                 nc.tensor.transpose(
                     out=wt_ps[:, q * P : (q + 1) * P],
@@ -265,7 +291,6 @@ def tile_multilstm_pa_t_kernel(
             nc.scalar.copy(out=w_x[:, j * BANK : (j + 1) * BANK], in_=wt_ps[:])
 
         state = {}
-        gate_func = (ACT.Sigmoid, ACT.Sigmoid, ACT.Tanh, ACT.Sigmoid)
 
         def bank(j):
             return slice(j * BANK, (j + 1) * BANK)
@@ -287,45 +312,62 @@ def tile_multilstm_pa_t_kernel(
                 state[i] = {}
             state[i]["r_ps", j] = r_ps
 
-        def recurrent_out(i, j):
+        def scalar_mean(i, j):
+            col = 6 * len(VECTOR_BANKS) + 3 * SCALAR_BANKS.index(j)
+            unread = wide.tile([P, BANK], BF16, bufs=1)
+            nc.scalar.activation(
+                out=unread[:], in_=state[i]["r_ps", j][:], func=ACT.Identity, scale=1.0 / BANK,
+                accum_out=r_stats_tiles[i % 3][:, col + 1 : col + 2],
+            )
+
+        def scalar_squares(i, j):
+            col = 6 * len(VECTOR_BANKS) + 3 * SCALAR_BANKS.index(j)
+            unread = wide.tile([P, BANK], BF16, bufs=1)
+            nc.scalar.activation(
+                out=unread[:], in_=state[i]["r_ps", j][:], func=ACT.Square, scale=-1.0,
+                bias=r_stats_tiles[i % 3][:, col + 1 : col + 2],
+                accum_out=r_stats_tiles[i % 3][:, col + 2 : col + 3],
+            )
+
+        def vector_stats(i, j):
+            col = 6 * VECTOR_BANKS.index(j)
+            nc.vector.bn_stats(out=r_stats_tiles[i % 3][:, col : col + 6], in_=state[i]["r_ps", j][:])
+
+        moments = {}
+        inverse_stds = {}
+
+        def moments_of(m):
+            if m not in moments:
+                mean_var = small.tile([P, 4], F32)
+                moments[m] = mean_var
+            return moments[m]
+
+        def aggregate_r(i):
+            nc.vector.bn_aggr(out=moments_of(i)[:, 0:2], in_=r_stats_tiles[i % 3][:])
+
+        def take_inverse_stds(m):
+            lo = 0 if m < ROW_TILES else 1
+            hi = 2 if m >= 2 else 1
+            var_eps = small.tile([P, 2], F32)
+            nc.gpsimd.tensor_scalar(
+                out=var_eps[:, lo:hi], in0=moments[m][:, 2 * lo + 1 : 2 * hi : 2], scalar1=1.0, scalar2=EPS,
+                op0=ALU.mult, op1=ALU.add,
+            )
+            rstd = small.tile([P, 2], F32)
+            nc.gpsimd.tensor_tensor(out=rstd[:, lo:hi], in0=var_eps[:, lo:hi], in1=neg_half[:, lo:hi], op=ALU.pow)
+            inverse_stds[m] = rstd
+
+        def gain_r(i, j):
             if j == 0:
-                r = wide.tile([P, G], F32)
-                r_sums = small.tile([P, BANKS], F32)
-                state[i]["r"] = r
-                state[i]["r_sums"] = r_sums
-            nc.scalar.activation(
-                out=state[i]["r"][:, bank(j)], in_=state[i]["r_ps", j][:], func=ACT.Identity,
-                accum_out=state[i]["r_sums"][:, j : j + 1],
-            )
-
-        def mean_of_r(i):
-            r_parts = small.tile([P, BANKS], F32)
-            neg_mean_r = small.tile([P, 1], F32)
-            nc.vector.tensor_scalar(
-                out=r_parts[:], in0=state[i]["r_sums"][:], scalar1=-1.0 / G, scalar2=None,
-                op0=ALU.mult, op1=ALU.add, accum_out=neg_mean_r[:],
-            )
-            state[i]["neg_mean_r"] = neg_mean_r
-
-        def inverse_std_of_r(i):
-            squares = wide.tile([P, G], BF16, bufs=1)
-            r_sum_sq = small.tile([P, 1], F32)
-            nc.scalar.activation(
-                out=squares[:], in_=state[i]["r"][:], func=ACT.Square, bias=state[i]["neg_mean_r"][:],
-                accum_out=r_sum_sq[:],
-            )
-            state[i]["rstd_r"] = inverse_std(r_sum_sq[:], G, 1)
-
-        def gain_r(i):
-            r_gained = wide.tile([P, G], F32)
+                r_gained = wide.tile([P, G], F32)
+                state[i]["r_gained"] = r_gained
             nc.vector.scalar_tensor_tensor(
-                out=r_gained[:], in0=state[i]["r"][:], scalar=state[i]["neg_mean_r"][:], in1=gain_h[:],
-                op0=ALU.add, op1=ALU.mult,
+                out=state[i]["r_gained"][:, bank(j)], in0=state[i]["r_ps", j][:], scalar=moments[i][:, 0:1],
+                in1=gain_h[:, bank(j)], op0=ALU.subtract, op1=ALU.mult,
             )
-            state[i]["r_gained"] = r_gained
 
         def x_side_matmul(i, j):
-            x_ps = ps_x.tile([P, BANK], F32)
+            x_ps = ps_x.tile([P, BANK], F32, tag="bank")
             nc.tensor.matmul(
                 out=x_ps[:], lhsT=groups[i // GROUP]["xhatT"][:, i % GROUP, :], rhs=w_x[:, bank(j)],
                 start=True, stop=False,
@@ -348,64 +390,44 @@ def tile_multilstm_pa_t_kernel(
                 state[i]["gates"] = gates
             nc.vector.scalar_tensor_tensor(
                 out=state[i]["gates"][:, bank(j)], in0=state[i]["r_gained"][:, bank(j)],
-                scalar=state[i]["rstd_r"][:], in1=state[i]["x_ps", j][:], op0=ALU.mult, op1=ALU.add,
+                scalar=inverse_stds[i][:, 0:1], in1=state[i]["x_ps", j][:], op0=ALU.mult, op1=ALU.add,
             )
 
-        def gate_activation(i, j):
-            gate = state[i]["gates"][:, bank(j)]
-            nc.scalar.activation(out=gate, in_=gate, func=gate_func[j])
+        def gate_activation(i, first, last, func):
+            gate = state[i]["gates"][:, first * BANK : (last + 1) * BANK]
+            nc.scalar.activation(out=gate, in_=gate, func=func)
 
-        def keep_old_cell(i):
+        def new_cell(i):
             kept = cell.tile([P, H], F32)
-            nc.vector.tensor_tensor(
+            nc.gpsimd.tensor_tensor(
                 out=kept[:], in0=state[i]["gates"][:, bank(1)], in1=groups[i // GROUP]["c0"][:, i % GROUP, :],
                 op=ALU.mult,
             )
-            state[i]["kept"] = kept
-
-        def make_fresh_cell(i):
             fresh = cell.tile([P, H], F32)
-            nc.vector.tensor_tensor(
+            nc.gpsimd.tensor_tensor(
                 out=fresh[:], in0=state[i]["gates"][:, bank(0)], in1=state[i]["gates"][:, bank(2)], op=ALU.mult
             )
-            state[i]["fresh"] = fresh
-
-        def sum_cell(i):
             c_new = cell.tile([P, H], F32)
-            c_sum = small.tile([P, 1], F32)
-            nc.vector.scalar_tensor_tensor(
-                out=c_new[:], in0=state[i]["kept"][:], scalar=1.0, in1=state[i]["fresh"][:],
-                op0=ALU.mult, op1=ALU.add, accum_out=c_sum[:],
-            )
+            nc.gpsimd.tensor_tensor(out=c_new[:], in0=kept[:], in1=fresh[:], op=ALU.add)
             state[i]["c_new"] = c_new
-            state[i]["c_sum"] = c_sum
 
-        def mean_of_cell(i):
-            neg_mean_c = small.tile([P, 1], F32)
-            nc.vector.tensor_scalar_mul(out=neg_mean_c[:], in0=state[i]["c_sum"][:], scalar1=-1.0 / H)
-            state[i]["neg_mean_c"] = neg_mean_c
-
-        def inverse_std_of_cell(i):
-            c_squares = cell.tile([P, H], BF16)
-            c_sum_sq = small.tile([P, 1], F32)
-            nc.scalar.activation(
-                out=c_squares[:], in_=state[i]["c_new"][:], func=ACT.Square, bias=state[i]["neg_mean_c"][:],
-                accum_out=c_sum_sq[:],
-            )
-            state[i]["rstd_c"] = inverse_std(c_sum_sq[:], H, 1)
+        def aggregate_cell(i):
+            c_stats = small.tile([P, 6], F32)
+            nc.vector.bn_stats(out=c_stats[:], in_=state[i]["c_new"][:])
+            nc.vector.bn_aggr(out=moments_of(i + 2)[:, 2:4], in_=c_stats[:])
 
         def gain_cell(i):
             c_gained = cell.tile([P, H], F32)
             nc.vector.scalar_tensor_tensor(
-                out=c_gained[:], in0=state[i]["c_new"][:], scalar=state[i]["neg_mean_c"][:], in1=gain_c[:],
-                op0=ALU.add, op1=ALU.mult,
+                out=c_gained[:], in0=state[i]["c_new"][:], scalar=moments[i + 2][:, 2:3], in1=gain_c[:],
+                op0=ALU.subtract, op1=ALU.mult,
             )
             state[i]["c_gained"] = c_gained
 
         def finish_cy(i):
             cy = result.tile([P, H], F32)
             nc.vector.scalar_tensor_tensor(
-                out=cy[:], in0=state[i]["c_gained"][:], scalar=state[i]["rstd_c"][:], in1=bias_c[:],
+                out=cy[:], in0=state[i]["c_gained"][:], scalar=inverse_stds[i + 2][:, 1:2], in1=bias_c[:],
                 op0=ALU.mult, op1=ALU.add,
             )
             nc.sync.dma_start(out=cy_rows[:, i, :], in_=cy[:])
@@ -418,15 +440,19 @@ def tile_multilstm_pa_t_kernel(
 
         def finish_hy(i):
             hy = result.tile([P, H], F32)
-            nc.vector.tensor_tensor(
+            nc.gpsimd.tensor_tensor(
                 out=hy[:], in0=state[i]["gates"][:, bank(3)], in1=state[i]["tanh_cy"][:], op=ALU.mult
             )
             nc.sync.dma_start(out=hy_rows[:, i, :], in_=hy[:])
 
-        transpose_x(0)
+        transpose_x(0, ps_x)
+        copy_xT(0)
+        x_times_cov(0, ps_x)
+        variance_of_a(0)
         inverse_std_of_a(0)
         scale_x(0)
-        transpose_xhat(0)
+        transpose_xhat(0, ps_x)
+        copy_xhatT(0)
 
         def piece_of(step, lag, piece, *args):
             i = step - lag
@@ -434,50 +460,67 @@ def tile_multilstm_pa_t_kernel(
                 piece(i, *args)
 
         with tc.manual_schedule():
-            for step in range(ROW_TILES + 5):
-                for j in range(AHEAD):
-                    piece_of(step, 0, recurrent_matmul, j)
-                for j in range(AHEAD):
-                    piece_of(step, 2, x_side_matmul, j)
-                piece_of(step, 0, recurrent_out, 0)
-                piece_of(step, 0, recurrent_matmul, AHEAD)
-                piece_of(step, 2, add_sides, 0)
-                piece_of(step, 2, x_side_matmul, AHEAD)
-                for j in range(1, BANKS):
-                    piece_of(step, 0, recurrent_out, j)
-                for j in range(1, AHEAD):
-                    piece_of(step, 2, add_sides, j)
-                piece_of(step, 3, sum_cell)
-                piece_of(step, 4, finish_cy)
-                piece_of(step, 3, mean_of_cell)
-                piece_of(step, 0, mean_of_r)
-                piece_of(step, 2, add_sides, AHEAD)
-                piece_of(step, 1, inverse_std_of_r)
-                for j in range(BANKS):
-                    piece_of(step, 2, gate_activation, j)
-                piece_of(step, 3, inverse_std_of_cell)
-                piece_of(step, 4, tanh_of_cy)
-                piece_of(step, 1, gain_r)
-                piece_of(step, 3, gain_cell)
-                piece_of(step, 5, finish_hy)
+            for step in range(-1, ROW_TILES + 3):
+                phase, coming = step % GROUP, step // GROUP + 1
+                prepare = 1 <= coming < N_GROUPS
 
-                phase, current = step % GROUP, step // GROUP
-                coming = current + 1
-                if coming < N_GROUPS and phase == 2:
-                    quantise_h0(coming)
-                if coming < N_GROUPS and phase == 3:
+                piece_of(step, 0, aggregate_r)
+                if 0 <= step < ROW_TILES + 2:
+                    take_inverse_stds(step)
+                for j in (0, 1):
+                    piece_of(step, 0, gain_r, j)
+                for j in (0, 1):
+                    piece_of(step, -1, recurrent_matmul, j)
+                if prepare and phase == 1:
+                    x_times_cov(coming, ps_misc)
+                if prepare and phase == 2:
+                    transpose_h0(coming, 1, ps_misc)
+                for j in (2, 3):
+                    piece_of(step, 0, gain_r, j)
+                for j in (2, 3):
+                    piece_of(step, -1, recurrent_matmul, j)
+                for j in SCALAR_BANKS:
+                    piece_of(step, -1, scalar_mean, j)
+                for j in SCALAR_BANKS:
+                    piece_of(step, -1, scalar_squares, j)
+
+                piece_of(step, 0, add_sides, 0)
+                piece_of(step, 0, x_side_matmul, 3)
+                piece_of(step, 0, add_sides, 1)
+                piece_of(step, -1, x_side_matmul, 0)
+                piece_of(step, 0, add_sides, 2)
+                if prepare and phase == 1:
+                    variance_of_a(coming)
+                    transpose_h0(coming, 0, ps_misc)
+                if prepare and phase == 2:
+                    copy_h0(coming, 1)
                     scale_x(coming)
-                piece_of(step, 2, keep_old_cell)
-                piece_of(step, 2, make_fresh_cell)
-                if 0 < current < N_GROUPS and phase == 0:
-                    transpose_xhat(current)
-                if coming < N_GROUPS and phase == 0:
-                    transpose_h0(coming, 0)
-                if coming < N_GROUPS and phase == 1:
-                    transpose_h0(coming, 1)
-                    transpose_x(coming)
-                if coming < N_GROUPS and phase == 2:
+                    transpose_xhat(coming, ps_misc)
+                if prepare and phase == 0:
+                    transpose_x(coming, ps_misc)
+                piece_of(step, -1, x_side_matmul, 1)
+                piece_of(step, 0, gate_activation, 0, 1, ACT.Sigmoid)
+                for j in VECTOR_BANKS:
+                    piece_of(step, -1, vector_stats, j)
+                piece_of(step, 1, new_cell)
+                piece_of(step, 2, gain_cell)
+                piece_of(step, 2, finish_cy)
+                piece_of(step, 0, gate_activation, 2, 2, ACT.Tanh)
+                piece_of(step, 0, add_sides, 3)
+                piece_of(step, -1, x_side_matmul, 2)
+                piece_of(step, 2, tanh_of_cy)
+                piece_of(step, 0, gate_activation, 3, 3, ACT.Sigmoid)
+                piece_of(step, 3, finish_hy)
+                piece_of(step, 1, aggregate_cell)
+
+                if prepare and phase == 0:
+                    copy_xT(coming)
+                if prepare and phase == 1:
+                    copy_h0(coming, 0)
                     inverse_std_of_a(coming)
-                if coming + 1 < N_GROUPS and phase == 2:
+                if prepare and phase == 2:
+                    copy_xhatT(coming)
+                    quantise_h0(coming)
+                if 1 <= coming and coming + 1 < N_GROUPS and phase == 2:
                     load_h0(coming + 1)
                     load_c0(coming + 1)

@@ -25,7 +25,7 @@ ROW_TILES = B // P
 GROUP = 4
 N_GROUPS = ROW_TILES // GROUP
 W_TILES = G // P
-X_BANKS = 3
+X_BANKS = 2
 VECTOR_BANKS = (0,)
 SCALAR_BANKS = (1, 2, 3)
 STAT_WIDTH = 6 * len(VECTOR_BANKS) + 3 * len(SCALAR_BANKS)
@@ -71,6 +71,7 @@ def tile_multilstm_pa_t_kernel(
         ps_r = ctx.enter_context(tc.psum_pool(name="ps_r", bufs=BANKS))
         ps_x = ctx.enter_context(tc.psum_pool(name="ps_x", bufs=X_BANKS))
         ps_misc = ctx.enter_context(tc.psum_pool(name="ps_misc", bufs=1))
+        ps_const = ctx.enter_context(tc.psum_pool(name="ps_const", bufs=1))
 
         groups = {}
 
@@ -105,6 +106,11 @@ def tile_multilstm_pa_t_kernel(
                 out=vec_rows[slot * W_TILES : (slot + 1) * W_TILES, :],
                 in_=vec.rearrange("(t p) -> t p", p=P),
             )
+        for slot, vec in enumerate((lnc_w1, lnc_b1)):
+            nc.sync.dma_start(
+                out=vec_rows[3 * W_TILES + slot * (H // P) : 3 * W_TILES + (slot + 1) * (H // P), :],
+                in_=vec.rearrange("(t p) -> t p", p=P),
+            )
 
         x_all = const.tile([P, ROW_TILES, V], BF16)
         nc.sync.dma_start(out=x_all[:], in_=x_rows)
@@ -114,10 +120,6 @@ def tile_multilstm_pa_t_kernel(
         load_c0(0)
         load_h0(1)
         load_c0(1)
-        gain_c = const.tile([P, H], BF16)
-        nc.sync.dma_start(out=gain_c[:], in_=lnc_w1.partition_broadcast(P))
-        bias_c = const.tile([P, H], BF16)
-        nc.sync.dma_start(out=bias_c[:], in_=lnc_b1.partition_broadcast(P))
 
         ident_bf = const.tile([P, P], BF16)
         make_identity(nc, ident_bf[:])
@@ -204,14 +206,12 @@ def tile_multilstm_pa_t_kernel(
             groups[grp]["rstd_a"] = inverse_std(groups[grp]["var_a"][:], 1.0, GROUP)
 
         def scale_x(grp):
-            tiles = slice(grp * GROUP, (grp + 1) * GROUP)
             xhat = prepared.tile([P, GROUP, V], F32)
-            nc.vector.tensor_tensor(
-                out=xhat[:],
-                in0=x_all[:, tiles, :],
-                in1=groups[grp]["rstd_a"][:].unsqueeze(2).to_broadcast([P, GROUP, V]),
-                op=ALU.mult,
-            )
+            for t in range(GROUP):
+                nc.scalar.activation(
+                    out=xhat[:, t, :], in_=x_all[:, grp * GROUP + t, :], func=ACT.Copy,
+                    scale=groups[grp]["rstd_a"][:, t : t + 1],
+                )
             groups[grp]["xhat"] = xhat
 
         def transpose_xhat(grp, banks):
@@ -237,6 +237,17 @@ def tile_multilstm_pa_t_kernel(
         nc.tensor.transpose(out=vec_ps[:], in_=vec_rows[:], identity=ident_bf[:])
         vec_cols = const.tile([P, 3 * W_TILES], F32)
         nc.vector.tensor_copy(out=vec_cols[:], in_=vec_ps[:, 0 : 3 * W_TILES])
+        cell_cols = const.tile([P, 2 * (H // P)], BF16)
+        nc.vector.tensor_copy(out=cell_cols[:], in_=vec_ps[:, 3 * W_TILES : 3 * W_TILES + 2 * (H // P)])
+        cell_rows = ps_const.tile([P, 2, H], BF16)
+        for k in range(2 * (H // P)):
+            nc.tensor.transpose(
+                out=cell_rows[:, k // (H // P), (k % (H // P)) * P : (k % (H // P) + 1) * P],
+                in_=cell_cols[:, k : k + 1].to_broadcast([P, P]),
+                identity=ident_bf[:],
+            )
+        gain_c = cell_rows[:, 0, :]
+        bias_c = cell_rows[:, 1, :]
         gain_i_cols = vec_cols[:, 0:W_TILES]
         bias_cols = const.tile([P, W_TILES], F32)
         nc.vector.tensor_tensor(
@@ -419,7 +430,7 @@ def tile_multilstm_pa_t_kernel(
         def gain_cell(i):
             c_gained = cell.tile([P, H], F32)
             nc.vector.scalar_tensor_tensor(
-                out=c_gained[:], in0=state[i]["c_new"][:], scalar=moments[i + 2][:, 2:3], in1=gain_c[:],
+                out=c_gained[:], in0=state[i]["c_new"][:], scalar=moments[i + 2][:, 2:3], in1=gain_c,
                 op0=ALU.subtract, op1=ALU.mult,
             )
             state[i]["c_gained"] = c_gained
@@ -427,7 +438,7 @@ def tile_multilstm_pa_t_kernel(
         def finish_cy(i):
             cy = result.tile([P, H], F32)
             nc.vector.scalar_tensor_tensor(
-                out=cy[:], in0=state[i]["c_gained"][:], scalar=inverse_stds[i + 2][:, 1:2], in1=bias_c[:],
+                out=cy[:], in0=state[i]["c_gained"][:], scalar=inverse_stds[i + 2][:, 1:2], in1=bias_c,
                 op0=ALU.mult, op1=ALU.add,
             )
             nc.sync.dma_start(out=cy_rows[:, i, :], in_=cy[:])
@@ -463,64 +474,67 @@ def tile_multilstm_pa_t_kernel(
             for step in range(-1, ROW_TILES + 3):
                 phase, coming = step % GROUP, step // GROUP + 1
                 prepare = 1 <= coming < N_GROUPS
+                after_coming = phase == 3 and coming + 1 < N_GROUPS
 
+                if prepare and phase == 1:
+                    scale_x(coming)
                 piece_of(step, 0, aggregate_r)
                 if 0 <= step < ROW_TILES + 2:
                     take_inverse_stds(step)
-                for j in (0, 1):
+                for j in (0, 1, 2):
                     piece_of(step, 0, gain_r, j)
-                for j in (0, 1):
+                for j in (0, 1, 2):
                     piece_of(step, -1, recurrent_matmul, j)
-                if prepare and phase == 1:
-                    x_times_cov(coming, ps_misc)
-                if prepare and phase == 2:
-                    transpose_h0(coming, 1, ps_misc)
-                for j in (2, 3):
-                    piece_of(step, 0, gain_r, j)
-                for j in (2, 3):
-                    piece_of(step, -1, recurrent_matmul, j)
-                for j in SCALAR_BANKS:
+                for j in (1, 2):
                     piece_of(step, -1, scalar_mean, j)
+                piece_of(step, 0, add_sides, 0)
+                piece_of(step, 0, x_side_matmul, 2)
+                piece_of(step, 0, gain_r, 3)
+                piece_of(step, -1, recurrent_matmul, 3)
+                if prepare and phase == 0:
+                    x_times_cov(coming, ps_misc)
+                if prepare and phase == 1:
+                    transpose_h0(coming, 1, ps_misc)
+                piece_of(step, 0, add_sides, 1)
+                piece_of(step, 0, x_side_matmul, 3)
+                piece_of(step, 0, gate_activation, 0, 1, ACT.Sigmoid)
+                piece_of(step, -1, scalar_mean, 3)
                 for j in SCALAR_BANKS:
                     piece_of(step, -1, scalar_squares, j)
-
-                piece_of(step, 0, add_sides, 0)
-                piece_of(step, 0, x_side_matmul, 3)
-                piece_of(step, 0, add_sides, 1)
-                piece_of(step, -1, x_side_matmul, 0)
-                piece_of(step, 0, add_sides, 2)
-                if prepare and phase == 1:
-                    variance_of_a(coming)
-                    transpose_h0(coming, 0, ps_misc)
-                if prepare and phase == 2:
-                    copy_h0(coming, 1)
-                    scale_x(coming)
-                    transpose_xhat(coming, ps_misc)
-                if prepare and phase == 0:
-                    transpose_x(coming, ps_misc)
-                piece_of(step, -1, x_side_matmul, 1)
-                piece_of(step, 0, gate_activation, 0, 1, ACT.Sigmoid)
                 for j in VECTOR_BANKS:
                     piece_of(step, -1, vector_stats, j)
                 piece_of(step, 1, new_cell)
                 piece_of(step, 2, gain_cell)
-                piece_of(step, 2, finish_cy)
+                if prepare and phase == 1:
+                    copy_h0(coming, 1)
+                if prepare and phase == 2:
+                    quantise_h0(coming)
+                piece_of(step, 0, add_sides, 2)
+                piece_of(step, -1, x_side_matmul, 0)
+                if prepare and phase == 0:
+                    variance_of_a(coming)
+                if after_coming:
+                    transpose_x(coming + 1, ps_misc)
+                if prepare and phase == 0:
+                    transpose_h0(coming, 0, ps_misc)
+                if prepare and phase == 1:
+                    transpose_xhat(coming, ps_misc)
                 piece_of(step, 0, gate_activation, 2, 2, ACT.Tanh)
-                piece_of(step, 0, add_sides, 3)
-                piece_of(step, -1, x_side_matmul, 2)
+                piece_of(step, 2, finish_cy)
                 piece_of(step, 2, tanh_of_cy)
+                piece_of(step, 1, aggregate_cell)
+                piece_of(step, 0, add_sides, 3)
+                piece_of(step, -1, x_side_matmul, 1)
                 piece_of(step, 0, gate_activation, 3, 3, ACT.Sigmoid)
                 piece_of(step, 3, finish_hy)
-                piece_of(step, 1, aggregate_cell)
 
+                if after_coming:
+                    copy_xT(coming + 1)
                 if prepare and phase == 0:
-                    copy_xT(coming)
-                if prepare and phase == 1:
                     copy_h0(coming, 0)
                     inverse_std_of_a(coming)
-                if prepare and phase == 2:
+                if prepare and phase == 1:
                     copy_xhatT(coming)
-                    quantise_h0(coming)
                 if 1 <= coming and coming + 1 < N_GROUPS and phase == 2:
                     load_h0(coming + 1)
                     load_c0(coming + 1)

@@ -88,17 +88,8 @@ def tile_multilstm_pa_t_kernel(
         w_nat = setup.tile([P, W_TILES, V], BF16)
         nc.sync.dma_start(out=w_nat[:], in_=w_ih1.rearrange("(t p) v -> p t v", p=P))
         load_h0(0)
-
-        w_words = const.tile([P, 2 * G], U8, align_bytes=64)
-        nc.sync.dma_start(out=w_words[:].bitcast(I32), in_=w_hh1_words[0].bitcast(I32))
-        w_scales = const.tile([P, G], U8, align_bytes=64)
-        nc.vector.memset(w_scales[:].bitcast(I32), 0)
-        for quad in range(4):
-            nc.sync.dma_start(
-                out=w_scales[32 * quad : 32 * quad + 4, :].bitcast(I32),
-                in_=w_hh1_scales[0, 4 * quad : 4 * quad + 4, :].bitcast(I32),
-            )
-
+        x_all = const.tile([P, ROW_TILES, V], BF16)
+        nc.sync.dma_start(out=x_all[:, 0:GROUP, :], in_=x_rows[:, 0:GROUP, :])
         vec_rows = setup.tile([P, P], BF16)
         nc.vector.memset(vec_rows[:], 0.0)
         for slot, vec in enumerate((lni_w1, lni_b1, lnh_b1)):
@@ -112,11 +103,20 @@ def tile_multilstm_pa_t_kernel(
                 in_=vec.rearrange("(t p) -> t p", p=P),
             )
 
-        x_all = const.tile([P, ROW_TILES, V], BF16)
-        nc.sync.dma_start(out=x_all[:], in_=x_rows)
+        w_words = const.tile([P, 2 * G], U8, align_bytes=64)
+        nc.sync.dma_start(out=w_words[:].bitcast(I32), in_=w_hh1_words[0].bitcast(I32))
+        w_scales = const.tile([P, G], U8, align_bytes=64)
+        nc.vector.memset(w_scales[:].bitcast(I32), 0)
+        for quad in range(4):
+            nc.sync.dma_start(
+                out=w_scales[32 * quad : 32 * quad + 4, :].bitcast(I32),
+                in_=w_hh1_scales[0, 4 * quad : 4 * quad + 4, :].bitcast(I32),
+            )
+
 
         gain_h = const.tile([P, G], BF16)
         nc.sync.dma_start(out=gain_h[:], in_=lnh_w1.partition_broadcast(P))
+        nc.sync.dma_start(out=x_all[:, GROUP:ROW_TILES, :], in_=x_rows[:, GROUP:ROW_TILES, :])
         load_c0(0)
         load_h0(1)
         load_c0(1)
@@ -227,79 +227,88 @@ def tile_multilstm_pa_t_kernel(
             nc.scalar.copy(out=xhatT[:], in_=groups[grp]["xhatT_ps"][:])
             groups[grp]["xhatT"] = xhatT
 
-        transpose_h0(0, 0, ps_x)
-        copy_h0(0, 0)
-        transpose_h0(0, 1, ps_x)
-        copy_h0(0, 1)
-        quantise_h0(0)
-
-        vec_ps = ps_x.tile([P, P], BF16, tag="bank")
-        nc.tensor.transpose(out=vec_ps[:], in_=vec_rows[:], identity=ident_bf[:])
+        CHUNK = 4
+        made = {}
+        w_centred = setup.tile([P, W_TILES, V], F32)
+        w_gained = setup.tile([P, W_TILES, V], F32)
+        cov = const.tile([V, V], F32)
+        w_x = const.tile([V, G], F32)
         vec_cols = const.tile([P, 3 * W_TILES], F32)
-        nc.vector.tensor_copy(out=vec_cols[:], in_=vec_ps[:, 0 : 3 * W_TILES])
+        bias_cols = const.tile([P, W_TILES], F32)
         cell_cols = const.tile([P, 2 * (H // P)], BF16)
-        nc.vector.tensor_copy(out=cell_cols[:], in_=vec_ps[:, 3 * W_TILES : 3 * W_TILES + 2 * (H // P)])
         cell_rows = ps_const.tile([P, 2, H], BF16)
-        for k in range(2 * (H // P)):
-            nc.tensor.transpose(
-                out=cell_rows[:, k // (H // P), (k % (H // P)) * P : (k % (H // P) + 1) * P],
-                in_=cell_cols[:, k : k + 1].to_broadcast([P, P]),
-                identity=ident_bf[:],
-            )
         gain_c = cell_rows[:, 0, :]
         bias_c = cell_rows[:, 1, :]
-        gain_i_cols = vec_cols[:, 0:W_TILES]
-        bias_cols = const.tile([P, W_TILES], F32)
-        nc.vector.tensor_tensor(
-            out=bias_cols[:],
-            in0=vec_cols[:, W_TILES : 2 * W_TILES],
-            in1=vec_cols[:, 2 * W_TILES : 3 * W_TILES],
-            op=ALU.add,
-        )
 
-        wsum_ps = ps_x.tile([P, V], F32, tag="bank")
-        for t in range(W_TILES):
-            nc.tensor.matmul(
-                out=wsum_ps[:], lhsT=ones_bf[:], rhs=w_nat[:, t, :], start=(t == 0), stop=(t == W_TILES - 1)
-            )
-        w_centred = setup.tile([P, W_TILES, V], F32)
-        nc.vector.scalar_tensor_tensor(
-            out=w_centred[:],
-            in0=wsum_ps[:].unsqueeze(1).to_broadcast([P, W_TILES, V]),
-            scalar=-1.0 / G,
-            in1=w_nat[:],
-            op0=ALU.mult,
-            op1=ALU.add,
-        )
-        cov_ps = ps_x.tile([V, V], F32, tag="bank")
-        for t in range(W_TILES):
-            nc.tensor.matmul(
-                out=cov_ps[:],
-                lhsT=w_centred[:, t, :],
-                rhs=w_centred[:, t, :],
-                start=(t == 0),
-                stop=(t == W_TILES - 1),
-            )
-        cov = const.tile([V, V], F32)
-        nc.scalar.mul(out=cov[:], in_=cov_ps[:], mul=1.0 / G)
+        def column_sums(banks):
+            wsum_ps = banks.tile([P, V], F32, tag="bank")
+            for t in range(W_TILES):
+                nc.tensor.matmul(
+                    out=wsum_ps[:], lhsT=ones_bf[:], rhs=w_nat[:, t, :], start=(t == 0), stop=(t == W_TILES - 1)
+                )
+            made["wsum_ps"] = wsum_ps
 
-        w_gained = setup.tile([P, W_TILES, V], F32)
-        nc.vector.tensor_tensor(
-            out=w_gained[:],
-            in0=w_centred[:],
-            in1=gain_i_cols.unsqueeze(2).to_broadcast([P, W_TILES, V]),
-            op=ALU.mult,
-        )
-        w_x = const.tile([V, G], F32)
-        for j in range(BANKS):
-            wt_ps = ps_x.tile([V, BANK], F32, tag="bank")
+        def centre(c):
+            tiles = slice(c * CHUNK, (c + 1) * CHUNK)
+            nc.vector.scalar_tensor_tensor(
+                out=w_centred[:, tiles, :],
+                in0=made["wsum_ps"][:].unsqueeze(1).to_broadcast([P, CHUNK, V]),
+                scalar=-1.0 / G,
+                in1=w_nat[:, tiles, :],
+                op0=ALU.mult,
+                op1=ALU.add,
+            )
+
+        def covariance(c, banks):
+            if c == 0:
+                cov_ps = banks.tile([V, V], F32, tag="bank")
+                made["cov_ps"] = cov_ps
+            for t in range(c * CHUNK, (c + 1) * CHUNK):
+                nc.tensor.matmul(
+                    out=made["cov_ps"][:], lhsT=w_centred[:, t, :], rhs=w_centred[:, t, :],
+                    start=(t == 0), stop=(t == W_TILES - 1),
+                )
+
+        def scale_covariance():
+            nc.vector.tensor_scalar_mul(out=cov[:], in0=made["cov_ps"][:], scalar1=1.0 / G)
+
+        def spread_vectors(banks):
+            vec_ps = banks.tile([P, P], BF16, tag="bank")
+            nc.tensor.transpose(out=vec_ps[:], in_=vec_rows[:], identity=ident_bf[:])
+            nc.vector.tensor_copy(out=vec_cols[:], in_=vec_ps[:, 0 : 3 * W_TILES])
+            nc.vector.tensor_copy(out=cell_cols[:], in_=vec_ps[:, 3 * W_TILES : 3 * W_TILES + 2 * (H // P)])
+            nc.vector.tensor_tensor(
+                out=bias_cols[:], in0=vec_cols[:, W_TILES : 2 * W_TILES], in1=vec_cols[:, 2 * W_TILES : 3 * W_TILES],
+                op=ALU.add,
+            )
+
+        def spread_cell_vectors():
+            for k in range(2 * (H // P)):
+                nc.tensor.transpose(
+                    out=cell_rows[:, k // (H // P), (k % (H // P)) * P : (k % (H // P) + 1) * P],
+                    in_=cell_cols[:, k : k + 1].to_broadcast([P, P]),
+                    identity=ident_bf[:],
+                )
+
+        def gain_w(c):
+            tiles = slice(c * CHUNK, (c + 1) * CHUNK)
+            nc.vector.tensor_tensor(
+                out=w_gained[:, tiles, :],
+                in0=w_centred[:, tiles, :],
+                in1=vec_cols[:, tiles].unsqueeze(2).to_broadcast([P, CHUNK, V]),
+                op=ALU.mult,
+            )
+
+        def transpose_w(j, banks):
+            wt_ps = banks.tile([V, BANK], F32, tag="bank")
             for q in range(BANK // P):
                 nc.tensor.transpose(
-                    out=wt_ps[:, q * P : (q + 1) * P],
-                    in_=w_gained[:, j * (BANK // P) + q, :],
-                    identity=ident_f32[:],
+                    out=wt_ps[:, q * P : (q + 1) * P], in_=w_gained[:, j * (BANK // P) + q, :], identity=ident_f32[:]
                 )
-            nc.scalar.copy(out=w_x[:, j * BANK : (j + 1) * BANK], in_=wt_ps[:])
+            made["wt_ps", j] = wt_ps
+
+        def copy_w(j):
+            nc.scalar.copy(out=w_x[:, j * BANK : (j + 1) * BANK], in_=made["wt_ps", j][:])
 
         state = {}
 
@@ -309,7 +318,7 @@ def tile_multilstm_pa_t_kernel(
         def recurrent_matmul(i, j):
             ops = groups[i // GROUP]
             rows = slice((i % GROUP) * P, (i % GROUP + 1) * P)
-            r_ps = ps_r.tile([P, BANK], F32)
+            r_ps = ps_r.tile([P, BANK], F32, tag="bank")
             nc.tensor.matmul_mx(
                 out=r_ps[:],
                 lhsT=ops["h_codes"][:, rows].bitcast(FP8X4),
@@ -408,18 +417,22 @@ def tile_multilstm_pa_t_kernel(
             gate = state[i]["gates"][:, first * BANK : (last + 1) * BANK]
             nc.scalar.activation(out=gate, in_=gate, func=func)
 
+        def products_engine(i):
+            return nc.vector if i == ROW_TILES - 1 else nc.gpsimd
+
         def new_cell(i):
+            engine = products_engine(i)
             kept = cell.tile([P, H], F32)
-            nc.gpsimd.tensor_tensor(
+            engine.tensor_tensor(
                 out=kept[:], in0=state[i]["gates"][:, bank(1)], in1=groups[i // GROUP]["c0"][:, i % GROUP, :],
                 op=ALU.mult,
             )
             fresh = cell.tile([P, H], F32)
-            nc.gpsimd.tensor_tensor(
+            engine.tensor_tensor(
                 out=fresh[:], in0=state[i]["gates"][:, bank(0)], in1=state[i]["gates"][:, bank(2)], op=ALU.mult
             )
             c_new = cell.tile([P, H], F32)
-            nc.gpsimd.tensor_tensor(out=c_new[:], in0=kept[:], in1=fresh[:], op=ALU.add)
+            engine.tensor_tensor(out=c_new[:], in0=kept[:], in1=fresh[:], op=ALU.add)
             state[i]["c_new"] = c_new
 
         def aggregate_cell(i):
@@ -451,19 +464,11 @@ def tile_multilstm_pa_t_kernel(
 
         def finish_hy(i):
             hy = result.tile([P, H], F32)
-            nc.gpsimd.tensor_tensor(
+            products_engine(i).tensor_tensor(
                 out=hy[:], in0=state[i]["gates"][:, bank(3)], in1=state[i]["tanh_cy"][:], op=ALU.mult
             )
             nc.sync.dma_start(out=hy_rows[:, i, :], in_=hy[:])
 
-        transpose_x(0, ps_x)
-        copy_xT(0)
-        x_times_cov(0, ps_x)
-        variance_of_a(0)
-        inverse_std_of_a(0)
-        scale_x(0)
-        transpose_xhat(0, ps_x)
-        copy_xhatT(0)
 
         def piece_of(step, lag, piece, *args):
             i = step - lag
@@ -471,7 +476,52 @@ def tile_multilstm_pa_t_kernel(
                 piece(i, *args)
 
         with tc.manual_schedule():
-            for step in range(-1, ROW_TILES + 3):
+            column_sums(ps_r)
+            centre(0)
+            centre(1)
+            transpose_h0(0, 0, ps_r)
+            copy_h0(0, 0)
+            transpose_h0(0, 1, ps_r)
+            copy_h0(0, 1)
+            transpose_x(0, ps_r)
+            copy_xT(0)
+            spread_vectors(ps_misc)
+            quantise_h0(0)
+            centre(2)
+            centre(3)
+            covariance(0, ps_x)
+            covariance(1, ps_x)
+            covariance(2, ps_x)
+            for j in range(BANKS):
+                recurrent_matmul(0, j)
+            covariance(3, ps_x)
+            for j in SCALAR_BANKS:
+                scalar_mean(0, j)
+            for j in SCALAR_BANKS:
+                scalar_squares(0, j)
+            for c in range(W_TILES // CHUNK):
+                gain_w(c)
+            for j in VECTOR_BANKS:
+                vector_stats(0, j)
+            scale_covariance()
+            x_times_cov(0, ps_misc)
+            variance_of_a(0)
+            inverse_std_of_a(0)
+            for j in (0, 1, 2):
+                transpose_w(j, ps_x)
+                copy_w(j)
+            scale_x(0)
+            transpose_w(3, ps_x)
+            transpose_xhat(0, ps_misc)
+            copy_xhatT(0)
+            copy_w(3)
+            spread_cell_vectors()
+            x_side_matmul(0, 0)
+            x_side_matmul(0, 1)
+            transpose_x(1, ps_misc)
+            copy_xT(1)
+
+            for step in range(0, ROW_TILES + 3):
                 phase, coming = step % GROUP, step // GROUP + 1
                 prepare = 1 <= coming < N_GROUPS
                 after_coming = phase == 3 and coming + 1 < N_GROUPS

@@ -64,7 +64,7 @@ def tile_multilstm_pa_t_kernel(
         stream = ctx.enter_context(tc.tile_pool(name="stream", bufs=3))
         prepared = ctx.enter_context(tc.tile_pool(name="prepared", bufs=2))
         wide = ctx.enter_context(tc.tile_pool(name="wide", bufs=2))
-        gate_pool = ctx.enter_context(tc.tile_pool(name="gate_pool", bufs=5))
+        gate_pool = ctx.enter_context(tc.tile_pool(name="gate_pool", bufs=6))
         cell = ctx.enter_context(tc.tile_pool(name="cell", bufs=3))
         result = ctx.enter_context(tc.tile_pool(name="result", bufs=3))
         small = ctx.enter_context(tc.tile_pool(name="small", bufs=8))
@@ -367,7 +367,7 @@ def tile_multilstm_pa_t_kernel(
 
         def take_inverse_stds(m):
             lo = 0 if m < ROW_TILES else 1
-            hi = 2 if m >= 2 else 1
+            hi = 2 if m >= 3 else 1
             var_eps = small.tile([P, 2], F32)
             nc.gpsimd.tensor_scalar(
                 out=var_eps[:, lo:hi], in0=moments[m][:, 2 * lo + 1 : 2 * hi : 2], scalar1=1.0, scalar2=EPS,
@@ -379,7 +379,7 @@ def tile_multilstm_pa_t_kernel(
 
         def gain_r(i, j):
             if j == 0:
-                r_gained = wide.tile([P, G], F32)
+                r_gained = wide.tile([P, G], F32, bufs=3)
                 state[i]["r_gained"] = r_gained
             nc.vector.scalar_tensor_tensor(
                 out=state[i]["r_gained"][:, bank(j)], in0=state[i]["r_ps", j][:], scalar=moments[i][:, 0:1],
@@ -438,12 +438,12 @@ def tile_multilstm_pa_t_kernel(
         def aggregate_cell(i):
             c_stats = small.tile([P, 6], F32)
             nc.vector.bn_stats(out=c_stats[:], in_=state[i]["c_new"][:])
-            nc.vector.bn_aggr(out=moments_of(i + 2)[:, 2:4], in_=c_stats[:])
+            nc.vector.bn_aggr(out=moments_of(i + 3)[:, 2:4], in_=c_stats[:])
 
         def gain_cell(i):
             c_gained = cell.tile([P, H], F32)
             nc.vector.scalar_tensor_tensor(
-                out=c_gained[:], in0=state[i]["c_new"][:], scalar=moments[i + 2][:, 2:3], in1=gain_c,
+                out=c_gained[:], in0=state[i]["c_new"][:], scalar=moments[i + 3][:, 2:3], in1=gain_c,
                 op0=ALU.subtract, op1=ALU.mult,
             )
             state[i]["c_gained"] = c_gained
@@ -451,7 +451,7 @@ def tile_multilstm_pa_t_kernel(
         def finish_cy(i):
             cy = result.tile([P, H], F32)
             nc.vector.scalar_tensor_tensor(
-                out=cy[:], in0=state[i]["c_gained"][:], scalar=inverse_stds[i + 2][:, 1:2], in1=bias_c,
+                out=cy[:], in0=state[i]["c_gained"][:], scalar=inverse_stds[i + 3][:, 1:2], in1=bias_c,
                 op0=ALU.mult, op1=ALU.add,
             )
             nc.sync.dma_start(out=cy_rows[:, i, :], in_=cy[:])
@@ -516,67 +516,62 @@ def tile_multilstm_pa_t_kernel(
             copy_xhatT(0)
             copy_w(3)
             spread_cell_vectors()
-            x_side_matmul(0, 0)
-            x_side_matmul(0, 1)
             transpose_x(1, ps_misc)
             copy_xT(1)
 
-            for step in range(0, ROW_TILES + 3):
+            for step in range(0, ROW_TILES + 5):
                 phase, coming = step % GROUP, step // GROUP + 1
                 prepare = 1 <= coming < N_GROUPS
                 after_coming = phase == 3 and coming + 1 < N_GROUPS
 
                 if prepare and phase == 1:
                     scale_x(coming)
+                piece_of(step, 4, tanh_of_cy)
+                piece_of(step, 1, add_sides, 0)
+                piece_of(step, 1, x_side_matmul, 2)
+                piece_of(step, 1, add_sides, 1)
+                piece_of(step, 1, x_side_matmul, 3)
+                piece_of(step, 1, gate_activation, 0, 1, ACT.Sigmoid)
                 piece_of(step, 0, aggregate_r)
-                if 0 <= step < ROW_TILES + 2:
+                if 0 <= step < ROW_TILES + 3:
                     take_inverse_stds(step)
-                for j in (0, 1, 2):
+                for j in range(BANKS):
                     piece_of(step, 0, gain_r, j)
-                for j in (0, 1, 2):
+                for j in range(BANKS):
                     piece_of(step, -1, recurrent_matmul, j)
-                for j in (1, 2):
-                    piece_of(step, -1, scalar_mean, j)
-                piece_of(step, 0, add_sides, 0)
-                piece_of(step, 0, x_side_matmul, 2)
-                piece_of(step, 0, gain_r, 3)
-                piece_of(step, -1, recurrent_matmul, 3)
                 if prepare and phase == 0:
                     x_times_cov(coming, ps_misc)
                 if prepare and phase == 1:
                     transpose_h0(coming, 1, ps_misc)
-                piece_of(step, 0, add_sides, 1)
-                piece_of(step, 0, x_side_matmul, 3)
-                piece_of(step, 0, gate_activation, 0, 1, ACT.Sigmoid)
-                piece_of(step, -1, scalar_mean, 3)
+                for j in SCALAR_BANKS:
+                    piece_of(step, -1, scalar_mean, j)
+                piece_of(step, 2, new_cell)
+                piece_of(step, 4, finish_hy)
+                piece_of(step, 1, add_sides, 2)
+                piece_of(step, 0, x_side_matmul, 0)
+                piece_of(step, 1, gate_activation, 2, 2, ACT.Tanh)
+                if prepare and phase == 1:
+                    copy_h0(coming, 1)
                 for j in SCALAR_BANKS:
                     piece_of(step, -1, scalar_squares, j)
                 for j in VECTOR_BANKS:
                     piece_of(step, -1, vector_stats, j)
-                piece_of(step, 1, new_cell)
-                piece_of(step, 2, gain_cell)
-                if prepare and phase == 1:
-                    copy_h0(coming, 1)
+                piece_of(step, 3, gain_cell)
                 if prepare and phase == 2:
                     quantise_h0(coming)
-                piece_of(step, 0, add_sides, 2)
-                piece_of(step, -1, x_side_matmul, 0)
                 if prepare and phase == 0:
                     variance_of_a(coming)
+                piece_of(step, 1, add_sides, 3)
+                piece_of(step, 0, x_side_matmul, 1)
+                piece_of(step, 1, gate_activation, 3, 3, ACT.Sigmoid)
                 if after_coming:
                     transpose_x(coming + 1, ps_misc)
                 if prepare and phase == 0:
                     transpose_h0(coming, 0, ps_misc)
                 if prepare and phase == 1:
                     transpose_xhat(coming, ps_misc)
-                piece_of(step, 0, gate_activation, 2, 2, ACT.Tanh)
-                piece_of(step, 2, finish_cy)
-                piece_of(step, 2, tanh_of_cy)
-                piece_of(step, 1, aggregate_cell)
-                piece_of(step, 0, add_sides, 3)
-                piece_of(step, -1, x_side_matmul, 1)
-                piece_of(step, 0, gate_activation, 3, 3, ACT.Sigmoid)
-                piece_of(step, 3, finish_hy)
+                piece_of(step, 3, finish_cy)
+                piece_of(step, 2, aggregate_cell)
 
                 if after_coming:
                     copy_xT(coming + 1)

@@ -86,7 +86,9 @@ def tile_multilstm_pa_t_kernel(
             groups[grp]["c0"] = c0_grp
 
         w_nat = setup.tile([P, W_TILES, V], BF16)
-        nc.sync.dma_start(out=w_nat[:], in_=w_ih1.rearrange("(t p) v -> p t v", p=P))
+        w_tiles = w_ih1.rearrange("(t p) v -> p t v", p=P)
+        for c in range(4):
+            nc.sync.dma_start(out=w_nat[:, 4 * c : 4 * c + 4, :], in_=w_tiles[:, 4 * c : 4 * c + 4, :])
         load_h0(0)
         x_all = const.tile([P, ROW_TILES, V], BF16)
         nc.sync.dma_start(out=x_all[:, 0:GROUP, :], in_=x_rows[:, 0:GROUP, :])
@@ -441,21 +443,20 @@ def tile_multilstm_pa_t_kernel(
             nc.vector.bn_aggr(out=moments_of(i + 3)[:, 2:4], in_=c_stats[:])
 
         def gain_cell(i):
-            c_gained = cell.tile([P, H], F32)
-            nc.vector.scalar_tensor_tensor(
-                out=c_gained[:], in0=state[i]["c_new"][:], scalar=moments[i + 3][:, 2:3], in1=gain_c,
-                op0=ALU.subtract, op1=ALU.mult,
-            )
-            state[i]["c_gained"] = c_gained
-
-        def finish_cy(i):
             cy = result.tile([P, H], F32)
             nc.vector.scalar_tensor_tensor(
-                out=cy[:], in0=state[i]["c_gained"][:], scalar=inverse_stds[i + 3][:, 1:2], in1=bias_c,
+                out=cy[:], in0=state[i]["c_new"][:], scalar=moments[i + 3][:, 2:3], in1=gain_c,
+                op0=ALU.subtract, op1=ALU.mult,
+            )
+            state[i]["cy"] = cy
+
+        def finish_cy(i):
+            cy = state[i]["cy"]
+            nc.vector.scalar_tensor_tensor(
+                out=cy[:], in0=cy[:], scalar=inverse_stds[i + 3][:, 1:2], in1=bias_c,
                 op0=ALU.mult, op1=ALU.add,
             )
             nc.sync.dma_start(out=cy_rows[:, i, :], in_=cy[:])
-            state[i]["cy"] = cy
 
         def tanh_of_cy(i):
             tanh_cy = cell.tile([P, H], F32)
@@ -527,6 +528,7 @@ def tile_multilstm_pa_t_kernel(
                 if prepare and phase == 1:
                     scale_x(coming)
                 piece_of(step, 4, tanh_of_cy)
+                piece_of(step, 2, new_cell)
                 piece_of(step, 1, add_sides, 0)
                 piece_of(step, 1, x_side_matmul, 2)
                 piece_of(step, 1, add_sides, 1)
@@ -545,7 +547,6 @@ def tile_multilstm_pa_t_kernel(
                     transpose_h0(coming, 1, ps_misc)
                 for j in SCALAR_BANKS:
                     piece_of(step, -1, scalar_mean, j)
-                piece_of(step, 2, new_cell)
                 piece_of(step, 4, finish_hy)
                 piece_of(step, 1, add_sides, 2)
                 piece_of(step, 0, x_side_matmul, 0)
@@ -570,8 +571,8 @@ def tile_multilstm_pa_t_kernel(
                     transpose_h0(coming, 0, ps_misc)
                 if prepare and phase == 1:
                     transpose_xhat(coming, ps_misc)
-                piece_of(step, 3, finish_cy)
                 piece_of(step, 2, aggregate_cell)
+                piece_of(step, 3, finish_cy)
 
                 if after_coming:
                     copy_xT(coming + 1)

@@ -25,10 +25,13 @@ ROW_TILES = B // P
 GROUP = 4
 N_GROUPS = ROW_TILES // GROUP
 W_TILES = G // P
-X_BANKS = 2
-VECTOR_BANKS = (0,)
+C_STAT_WIDTH = 6 + 3
+STAT_TILES = 4
+X_BANKS = 3
+HELD_BANKS = (0, 1)
+COPIED_BANKS = (2, 3)
 SCALAR_BANKS = (1, 2, 3)
-STAT_WIDTH = 6 * len(VECTOR_BANKS) + 3 * len(SCALAR_BANKS)
+STAT_WIDTH = 6 + 3 * len(SCALAR_BANKS) + 3
 
 FLOPS = 2 * B * G * (V + H)
 
@@ -68,9 +71,9 @@ def tile_multilstm_pa_t_kernel(
         cell = ctx.enter_context(tc.tile_pool(name="cell", bufs=3))
         result = ctx.enter_context(tc.tile_pool(name="result", bufs=3))
         small = ctx.enter_context(tc.tile_pool(name="small", bufs=8))
-        ps_r = ctx.enter_context(tc.psum_pool(name="ps_r", bufs=BANKS))
+        ps_held = ctx.enter_context(tc.psum_pool(name="ps_held", bufs=len(HELD_BANKS)))
+        ps_flow = ctx.enter_context(tc.psum_pool(name="ps_flow", bufs=1))
         ps_x = ctx.enter_context(tc.psum_pool(name="ps_x", bufs=X_BANKS))
-        ps_misc = ctx.enter_context(tc.psum_pool(name="ps_misc", bufs=1))
         ps_const = ctx.enter_context(tc.psum_pool(name="ps_const", bufs=1))
 
         groups = {}
@@ -104,11 +107,15 @@ def tile_multilstm_pa_t_kernel(
                 out=vec_rows[3 * W_TILES + slot * (H // P) : 3 * W_TILES + (slot + 1) * (H // P), :],
                 in_=vec.rearrange("(t p) -> t p", p=P),
             )
+        nc.sync.dma_start(
+            out=vec_rows[3 * W_TILES + 2 * (H // P) : 3 * W_TILES + 4 * (H // P), :],
+            in_=lnh_w1[len(HELD_BANKS) * BANK : G].rearrange("(t p) -> t p", p=P),
+        )
 
         w_words = const.tile([P, 2 * G], U8, align_bytes=64)
         nc.sync.dma_start(out=w_words[:].bitcast(I32), in_=w_hh1_words[0].bitcast(I32))
         w_scales = const.tile([P, G], U8, align_bytes=64)
-        nc.vector.memset(w_scales[:].bitcast(I32), 0)
+        nc.gpsimd.memset(w_scales[:].bitcast(I32), 0)
         for quad in range(4):
             nc.sync.dma_start(
                 out=w_scales[32 * quad : 32 * quad + 4, :].bitcast(I32),
@@ -116,11 +123,14 @@ def tile_multilstm_pa_t_kernel(
             )
 
 
-        gain_h = const.tile([P, G], BF16)
-        nc.sync.dma_start(out=gain_h[:], in_=lnh_w1.partition_broadcast(P))
+        gain_h = const.tile([P, len(HELD_BANKS) * BANK], BF16)
+        nc.sync.dma_start(out=gain_h[:], in_=lnh_w1[0 : len(HELD_BANKS) * BANK].partition_broadcast(P))
+        bias_c_rows = const.tile([P, H], BF16)
+        nc.sync.dma_start(out=bias_c_rows[:], in_=lnc_b1.partition_broadcast(P))
         nc.sync.dma_start(out=x_all[:, GROUP:ROW_TILES, :], in_=x_rows[:, GROUP:ROW_TILES, :])
-        load_c0(0)
         load_h0(1)
+        load_c0(0)
+        load_h0(2)
         load_c0(1)
 
         ident_bf = const.tile([P, P], BF16)
@@ -129,26 +139,27 @@ def tile_multilstm_pa_t_kernel(
         make_identity(nc, ident_f32[:])
         ones_bf = const.tile([P, P], BF16)
         nc.vector.memset(ones_bf[:], 1.0)
+        ones_f32 = const.tile([P, 1], F32)
+        nc.vector.memset(ones_f32[:], 1.0)
         neg_half = const.tile([P, GROUP], F32)
         nc.vector.memset(neg_half[:], -0.5)
         table_warmer = const.tile([P, 1], F32)
         nc.scalar.activation(out=table_warmer[:], in_=neg_half[:, 0:1], func=ACT.Sigmoid)
         r_stats_tiles = []
-        for k in range(3):
+        c_stats_tiles = []
+        for k in range(STAT_TILES):
             r_stats = const.tile([P, STAT_WIDTH], F32, name="r_stats%d" % k)
-            for n in range(len(SCALAR_BANKS)):
-                col = 6 * len(VECTOR_BANKS) + 3 * n
-                nc.vector.memset(r_stats[:, col : col + 1], float(BANK))
+            nc.vector.memset(r_stats[:], 0.0)
             r_stats_tiles.append(r_stats)
-
-        def inverse_std(sum_sq, count, width):
-            var_eps = small.tile([P, width], F32)
-            nc.gpsimd.tensor_scalar(
-                out=var_eps[:], in0=sum_sq, scalar1=1.0 / count, scalar2=EPS, op0=ALU.mult, op1=ALU.add
-            )
-            rstd = small.tile([P, width], F32)
-            nc.gpsimd.tensor_tensor(out=rstd[:], in0=var_eps[:], in1=neg_half[:, 0:width], op=ALU.pow)
-            return rstd
+            c_stats = const.tile([P, C_STAT_WIDTH], F32, name="c_stats%d" % k)
+            nc.vector.memset(c_stats[:], 0.0)
+            c_stats_tiles.append(c_stats)
+        for r_stats, c_stats in zip(r_stats_tiles, c_stats_tiles):
+            nc.vector.memset(r_stats[:, 6 : 6 + 3 * len(SCALAR_BANKS) : 3], float(BANK))
+            for stats, width, count in ((r_stats, STAT_WIDTH, G), (c_stats, C_STAT_WIDTH, H)):
+                nc.vector.tensor_scalar_add(
+                    out=stats[:, width - 1 : width], in0=stats[:, width - 3 : width - 2], scalar1=EPS * count
+                )
 
         def transpose_h0(grp, half, banks):
             if half == 0:
@@ -184,64 +195,114 @@ def tile_multilstm_pa_t_kernel(
             groups[grp]["xT_ps"] = xT_ps
 
         def copy_xT(grp):
-            xT = prepared.tile([V, GROUP, P], F32)
+            xT = prepared.tile([V, GROUP, P], F32 if grp == 0 else BF16, name="xT_first" if grp == 0 else "xT")
             nc.scalar.copy(out=xT[:], in_=groups[grp]["xT_ps"][:])
             groups[grp]["xT"] = xT
 
-        def x_times_cov(grp, banks):
-            xcov_ps = banks.tile([P, GROUP, V], F32, tag="bank")
+        def cov_times_x(grp, banks):
+            covx_ps = banks.tile([V, GROUP, P], F32, tag="bank")
+            for half in range(2):
+                nc.tensor.matmul(
+                    out=covx_ps[:].rearrange("v t b -> v (t b)"), lhsT=cov_halves[:, half, :],
+                    rhs=groups[grp]["xT"][:].rearrange("v t b -> v (t b)"), start=(half == 0), stop=(half == 1),
+                )
+            groups[grp]["covx_ps"] = covx_ps
+
+        def weigh_covx(grp):
+            x_covx = prepared.tile([V, GROUP, P], F32)
+            nc.vector.tensor_tensor(
+                out=x_covx[:], in0=groups[grp]["covx_ps"][:], in1=groups[grp]["xT"][:], op=ALU.mult
+            )
+            groups[grp]["x_covx"] = x_covx
+
+        def sum_variance(grp, banks):
+            var_ps = banks.tile([P, GROUP], F32, tag="bank")
             for t in range(GROUP):
                 nc.tensor.matmul(
-                    out=xcov_ps[:, t, :], lhsT=groups[grp]["xT"][:, t, :], rhs=cov[:], start=True, stop=True
+                    out=var_ps[:, t : t + 1], lhsT=groups[grp]["x_covx"][:, t, :], rhs=ones_f32[:],
+                    start=True, stop=True,
                 )
-            groups[grp]["xcov_ps"] = xcov_ps
+            groups[grp]["var_ps"] = var_ps
 
-        def variance_of_a(grp):
-            tiles = slice(grp * GROUP, (grp + 1) * GROUP)
-            xcovx = prepared.tile([P, GROUP, V], F32)
-            nc.vector.tensor_tensor(out=xcovx[:], in0=groups[grp]["xcov_ps"][:], in1=x_all[:, tiles, :], op=ALU.mult)
+        def copy_variance(grp):
             var_a = small.tile([P, GROUP], F32)
-            nc.vector.tensor_reduce(out=var_a[:], in_=xcovx[:], axis=AX.X, op=ALU.add)
+            nc.scalar.copy(out=var_a[:], in_=groups[grp]["var_ps"][:])
             groups[grp]["var_a"] = var_a
 
-        def inverse_std_of_a(grp):
-            groups[grp]["rstd_a"] = inverse_std(groups[grp]["var_a"][:], 1.0, GROUP)
+        def inverse_std_of_a(grp, first=0, last=GROUP):
+            width = last - first
+            var_eps = small.tile([P, width], F32)
+            nc.gpsimd.tensor_scalar(
+                out=var_eps[:], in0=groups[grp]["var_a"][:, first:last], scalar1=1.0, scalar2=EPS,
+                op0=ALU.mult, op1=ALU.add,
+            )
+            rstd_a = small.tile([P, width], F32)
+            nc.gpsimd.tensor_tensor(out=rstd_a[:], in0=var_eps[:], in1=neg_half[:, 0:width], op=ALU.pow)
+            groups[grp]["rstd_a"] = rstd_a[:]
+            for t in range(first, last):
+                groups[grp]["rstd_a", t] = rstd_a[:, t - first : t - first + 1]
 
-        def scale_x(grp):
-            xhat = prepared.tile([P, GROUP, V], F32)
-            for t in range(GROUP):
-                nc.scalar.activation(
-                    out=xhat[:, t, :], in_=x_all[:, grp * GROUP + t, :], func=ACT.Copy,
-                    scale=groups[grp]["rstd_a"][:, t : t + 1],
+        def first_variance(tiles, banks):
+            xcov_ps = banks.tile([P, len(tiles), V], F32, tag="bank")
+            for k, t in enumerate(tiles):
+                nc.tensor.matmul(
+                    out=xcov_ps[:, k, :], lhsT=groups[0]["xT"][:, t, :], rhs=cov[:], start=True, stop=True
                 )
+                made["xcov", t] = xcov_ps[:, k, :]
+
+        def first_variance_sum(t):
+            if t == 0:
+                var_a = small.tile([P, GROUP], F32)
+                groups[0]["var_a"] = var_a
+            unread_x = setup.tile([P, V], F32)
+            nc.vector.scalar_tensor_tensor(
+                out=unread_x[:], in0=made["xcov", t], scalar=1.0, in1=x_all[:, t, :],
+                op0=ALU.mult, op1=ALU.mult, accum_out=groups[0]["var_a"][:, t : t + 1],
+            )
+
+        def scale_group(grp):
+            xhat = prepared.tile([P, GROUP, V], F32)
+            nc.gpsimd.tensor_tensor(
+                out=xhat[:], in0=x_all[:, grp * GROUP : (grp + 1) * GROUP, :],
+                in1=groups[grp]["rstd_a"].unsqueeze(2).to_broadcast([P, GROUP, V]), op=ALU.mult,
+            )
             groups[grp]["xhat"] = xhat
 
-        def transpose_xhat(grp, banks):
-            xhatT_ps = banks.tile([V, GROUP, P], F32, tag="bank")
-            for t in range(GROUP):
+        def scale_x(grp, tiles=range(GROUP)):
+            for t in tiles:
+                if t == 0:
+                    xhat = prepared.tile([P, GROUP, V], F32)
+                    groups[grp]["xhat"] = xhat
+                nc.scalar.activation(
+                    out=groups[grp]["xhat"][:, t, :], in_=x_all[:, grp * GROUP + t, :], func=ACT.Copy,
+                    scale=groups[grp]["rstd_a", t],
+                )
+
+        def transpose_xhat(grp, banks, tiles=range(GROUP)):
+            xhatT_ps = banks.tile([V, len(tiles), P], F32, tag="bank")
+            for k, t in enumerate(tiles):
                 nc.tensor.transpose(
-                    out=xhatT_ps[:, t, :], in_=groups[grp]["xhat"][:, t, :], identity=ident_f32[:]
+                    out=xhatT_ps[:, k, :], in_=groups[grp]["xhat"][:, t, :], identity=ident_f32[:]
                 )
             groups[grp]["xhatT_ps"] = xhatT_ps
 
-        def copy_xhatT(grp):
-            xhatT = prepared.tile([V, GROUP, P], F32)
-            nc.scalar.copy(out=xhatT[:], in_=groups[grp]["xhatT_ps"][:])
-            groups[grp]["xhatT"] = xhatT
+        def copy_xhatT(grp, first=0, last=GROUP):
+            if first == 0:
+                xhatT = prepared.tile([V, GROUP, P], F32)
+                groups[grp]["xhatT"] = xhatT
+            nc.scalar.copy(out=groups[grp]["xhatT"][:, first:last, :], in_=groups[grp]["xhatT_ps"][:])
 
         CHUNK = 4
         made = {}
         w_centred = setup.tile([P, W_TILES, V], F32)
         w_gained = setup.tile([P, W_TILES, V], F32)
         cov = const.tile([V, V], F32)
+        cov_halves = const.tile([V, 2, V], BF16)
         w_x = const.tile([V, G], F32)
         vec_cols = const.tile([P, 3 * W_TILES], F32)
         bias_cols = const.tile([P, W_TILES], F32)
         cell_cols = const.tile([P, 2 * (H // P)], BF16)
-        cell_rows = ps_const.tile([P, 2, H], BF16)
-        gain_c = cell_rows[:, 0, :]
-        bias_c = cell_rows[:, 1, :]
-
+        gain_cols = const.tile([P, 2 * (H // P)], BF16)
         def column_sums(banks):
             wsum_ps = banks.tile([P, V], F32, tag="bank")
             for t in range(W_TILES):
@@ -274,21 +335,33 @@ def tile_multilstm_pa_t_kernel(
         def scale_covariance():
             nc.vector.tensor_scalar_mul(out=cov[:], in0=made["cov_ps"][:], scalar1=1.0 / G)
 
+        def halve_covariance():
+            nc.gpsimd.tensor_copy(out=cov_halves[:, 0, :], in_=cov[:])
+            nc.gpsimd.tensor_tensor(
+                out=cov_halves[:, 1, :], in0=cov[:], in1=cov_halves[:, 0, :], op=ALU.subtract
+            )
+
         def spread_vectors(banks):
             vec_ps = banks.tile([P, P], BF16, tag="bank")
             nc.tensor.transpose(out=vec_ps[:], in_=vec_rows[:], identity=ident_bf[:])
             nc.vector.tensor_copy(out=vec_cols[:], in_=vec_ps[:, 0 : 3 * W_TILES])
             nc.vector.tensor_copy(out=cell_cols[:], in_=vec_ps[:, 3 * W_TILES : 3 * W_TILES + 2 * (H // P)])
+            nc.vector.tensor_scalar_mul(
+                out=gain_cols[:], in0=vec_ps[:, 3 * W_TILES + 2 * (H // P) : 3 * W_TILES + 4 * (H // P)],
+                scalar1=float(BANK),
+            )
             nc.vector.tensor_tensor(
                 out=bias_cols[:], in0=vec_cols[:, W_TILES : 2 * W_TILES], in1=vec_cols[:, 2 * W_TILES : 3 * W_TILES],
                 op=ALU.add,
             )
 
-        def spread_cell_vectors():
+        def spread_rows(name, cols):
+            rows = ps_const.tile([P, 2, H], BF16, tag=name)
+            made[name] = rows
             for k in range(2 * (H // P)):
                 nc.tensor.transpose(
-                    out=cell_rows[:, k // (H // P), (k % (H // P)) * P : (k % (H // P) + 1) * P],
-                    in_=cell_cols[:, k : k + 1].to_broadcast([P, P]),
+                    out=rows[:, k // (H // P), (k % (H // P)) * P : (k % (H // P) + 1) * P],
+                    in_=cols[:, k : k + 1].to_broadcast([P, P]),
                     identity=ident_bf[:],
                 )
 
@@ -301,16 +374,16 @@ def tile_multilstm_pa_t_kernel(
                 op=ALU.mult,
             )
 
-        def transpose_w(j, banks):
-            wt_ps = banks.tile([V, BANK], F32, tag="bank")
+        def transpose_w(j, banks, tag="bank"):
+            wt_ps = banks.tile([V, BANK], F32, tag=tag)
             for q in range(BANK // P):
                 nc.tensor.transpose(
                     out=wt_ps[:, q * P : (q + 1) * P], in_=w_gained[:, j * (BANK // P) + q, :], identity=ident_f32[:]
                 )
             made["wt_ps", j] = wt_ps
 
-        def copy_w(j):
-            nc.scalar.copy(out=w_x[:, j * BANK : (j + 1) * BANK], in_=made["wt_ps", j][:])
+        def copy_w(j, copy):
+            copy(out=w_x[:, j * BANK : (j + 1) * BANK], in_=made["wt_ps", j][:])
 
         state = {}
 
@@ -320,7 +393,8 @@ def tile_multilstm_pa_t_kernel(
         def recurrent_matmul(i, j):
             ops = groups[i // GROUP]
             rows = slice((i % GROUP) * P, (i % GROUP + 1) * P)
-            r_ps = ps_r.tile([P, BANK], F32, tag="bank")
+            banks = ps_held if j in HELD_BANKS else ps_flow
+            r_ps = banks.tile([P, BANK], F32, tag="bank")
             nc.tensor.matmul_mx(
                 out=r_ps[:],
                 lhsT=ops["h_codes"][:, rows].bitcast(FP8X4),
@@ -330,30 +404,50 @@ def tile_multilstm_pa_t_kernel(
                 start=True,
                 stop=True,
             )
-            if j == 0:
-                state[i] = {}
-            state[i]["r_ps", j] = r_ps
+            state.setdefault(i, {})["r_ps", j] = r_ps
 
-        def scalar_mean(i, j):
-            col = 6 * len(VECTOR_BANKS) + 3 * SCALAR_BANKS.index(j)
+        def mean_col(i, j):
+            col = 6 + 3 * SCALAR_BANKS.index(j) + 1
+            return r_stats_tiles[i % STAT_TILES][:, col : col + 1]
+
+        def squares_col(i, j):
+            col = 6 + 3 * SCALAR_BANKS.index(j) + 2
+            return r_stats_tiles[i % STAT_TILES][:, col : col + 1]
+
+        def held_mean(i, j):
             unread = wide.tile([P, BANK], BF16, bufs=1)
             nc.scalar.activation(
                 out=unread[:], in_=state[i]["r_ps", j][:], func=ACT.Identity, scale=1.0 / BANK,
-                accum_out=r_stats_tiles[i % 3][:, col + 1 : col + 2],
+                accum_out=mean_col(i, j),
             )
 
-        def scalar_squares(i, j):
-            col = 6 * len(VECTOR_BANKS) + 3 * SCALAR_BANKS.index(j)
+        def held_squares(i, j):
             unread = wide.tile([P, BANK], BF16, bufs=1)
             nc.scalar.activation(
                 out=unread[:], in_=state[i]["r_ps", j][:], func=ACT.Square, scale=-1.0,
-                bias=r_stats_tiles[i % 3][:, col + 1 : col + 2],
-                accum_out=r_stats_tiles[i % 3][:, col + 2 : col + 3],
+                bias=mean_col(i, j), accum_out=squares_col(i, j),
             )
 
-        def vector_stats(i, j):
-            col = 6 * VECTOR_BANKS.index(j)
-            nc.vector.bn_stats(out=r_stats_tiles[i % 3][:, col : col + 6], in_=state[i]["r_ps", j][:])
+        def copy_out(i, j):
+            if j == COPIED_BANKS[0]:
+                r_copied = wide.tile([P, len(COPIED_BANKS) * BANK], F32, bufs=4)
+                state[i]["r_copied"] = r_copied
+            k = COPIED_BANKS.index(j)
+            nc.scalar.activation(
+                out=state[i]["r_copied"][:, k * BANK : (k + 1) * BANK], in_=state[i]["r_ps", j][:],
+                func=ACT.Identity, scale=1.0 / BANK, accum_out=mean_col(i, j),
+            )
+
+        def copied_squares(i, j):
+            k = COPIED_BANKS.index(j)
+            unread = wide.tile([P, BANK], BF16, bufs=1)
+            nc.scalar.activation(
+                out=unread[:], in_=state[i]["r_copied"][:, k * BANK : (k + 1) * BANK], func=ACT.Square,
+                scale=-float(BANK), bias=mean_col(i, j), accum_out=squares_col(i, j),
+            )
+
+        def vector_stats(i):
+            nc.vector.bn_stats(out=r_stats_tiles[i % STAT_TILES][:, 0:6], in_=state[i]["r_ps", 0][:])
 
         moments = {}
         inverse_stds = {}
@@ -365,18 +459,22 @@ def tile_multilstm_pa_t_kernel(
             return moments[m]
 
         def aggregate_r(i):
-            nc.vector.bn_aggr(out=moments_of(i)[:, 0:2], in_=r_stats_tiles[i % 3][:])
+            nc.vector.bn_aggr(out=moments_of(i)[:, 0:2], in_=r_stats_tiles[i % STAT_TILES][:])
+
+        def scale_mean(i):
+            small_mean = small.tile([P, 1], F32)
+            nc.gpsimd.tensor_scalar(
+                out=small_mean[:], in0=moments[i][:, 0:1], scalar1=1.0 / BANK, scalar2=0.0, op0=ALU.mult, op1=ALU.add
+            )
+            state[i]["small_mean"] = small_mean
 
         def take_inverse_stds(m):
             lo = 0 if m < ROW_TILES else 1
             hi = 2 if m >= 3 else 1
-            var_eps = small.tile([P, 2], F32)
-            nc.gpsimd.tensor_scalar(
-                out=var_eps[:, lo:hi], in0=moments[m][:, 2 * lo + 1 : 2 * hi : 2], scalar1=1.0, scalar2=EPS,
-                op0=ALU.mult, op1=ALU.add,
-            )
             rstd = small.tile([P, 2], F32)
-            nc.gpsimd.tensor_tensor(out=rstd[:, lo:hi], in0=var_eps[:, lo:hi], in1=neg_half[:, lo:hi], op=ALU.pow)
+            nc.gpsimd.tensor_tensor(
+                out=rstd[:, lo:hi], in0=moments[m][:, 2 * lo + 1 : 2 * hi : 2], in1=neg_half[:, lo:hi], op=ALU.pow
+            )
             inverse_stds[m] = rstd
 
         def gain_r(i, j):
@@ -386,6 +484,13 @@ def tile_multilstm_pa_t_kernel(
             nc.vector.scalar_tensor_tensor(
                 out=state[i]["r_gained"][:, bank(j)], in0=state[i]["r_ps", j][:], scalar=moments[i][:, 0:1],
                 in1=gain_h[:, bank(j)], op0=ALU.subtract, op1=ALU.mult,
+            )
+
+        def gain_copied(i):
+            nc.vector.scalar_tensor_tensor(
+                out=state[i]["r_gained"][:, len(HELD_BANKS) * BANK : G], in0=state[i]["r_copied"][:],
+                scalar=state[i]["small_mean"][:], in1=made["gain"][:].rearrange("p c n -> p (c n)"),
+                op0=ALU.subtract, op1=ALU.mult,
             )
 
         def x_side_matmul(i, j):
@@ -422,38 +527,60 @@ def tile_multilstm_pa_t_kernel(
         def products_engine(i):
             return nc.vector if i == ROW_TILES - 1 else nc.gpsimd
 
-        def new_cell(i):
-            engine = products_engine(i)
+        def finishes_on_gpsimd(i):
+            return False
+
+        def kept_cell(i):
             kept = cell.tile([P, H], F32)
-            engine.tensor_tensor(
+            products_engine(i).tensor_tensor(
                 out=kept[:], in0=state[i]["gates"][:, bank(1)], in1=groups[i // GROUP]["c0"][:, i % GROUP, :],
                 op=ALU.mult,
             )
+            state[i]["kept"] = kept
+
+        def fresh_cell(i):
             fresh = cell.tile([P, H], F32)
-            engine.tensor_tensor(
+            products_engine(i).tensor_tensor(
                 out=fresh[:], in0=state[i]["gates"][:, bank(0)], in1=state[i]["gates"][:, bank(2)], op=ALU.mult
             )
+            state[i]["fresh"] = fresh
+
+        def new_cell(i):
             c_new = cell.tile([P, H], F32)
-            engine.tensor_tensor(out=c_new[:], in0=kept[:], in1=fresh[:], op=ALU.add)
+            products_engine(i).tensor_tensor(
+                out=c_new[:], in0=state[i]["kept"][:], in1=state[i]["fresh"][:], op=ALU.add
+            )
             state[i]["c_new"] = c_new
 
+        def cell_stats(i):
+            nc.vector.bn_stats(out=c_stats_tiles[i % STAT_TILES][:, 0:6], in_=state[i]["c_new"][:])
+
         def aggregate_cell(i):
-            c_stats = small.tile([P, 6], F32)
-            nc.vector.bn_stats(out=c_stats[:], in_=state[i]["c_new"][:])
-            nc.vector.bn_aggr(out=moments_of(i + 3)[:, 2:4], in_=c_stats[:])
+            nc.vector.bn_aggr(out=moments_of(i + 3)[:, 2:4], in_=c_stats_tiles[i % STAT_TILES][:])
 
         def gain_cell(i):
             cy = result.tile([P, H], F32)
             nc.vector.scalar_tensor_tensor(
-                out=cy[:], in0=state[i]["c_new"][:], scalar=moments[i + 3][:, 2:3], in1=gain_c,
+                out=cy[:], in0=state[i]["c_new"][:], scalar=moments[i + 3][:, 2:3], in1=made["cell"][:, 0, :],
                 op0=ALU.subtract, op1=ALU.mult,
             )
             state[i]["cy"] = cy
 
+        def finish_cy_gpsimd(i):
+            scaled = cell.tile([P, H], F32)
+            nc.gpsimd.tensor_scalar(
+                out=scaled[:], in0=state[i]["cy"][:], scalar1=inverse_stds[i + 3][:, 1:2], scalar2=0.0,
+                op0=ALU.mult, op1=ALU.add,
+            )
+            cy = result.tile([P, H], F32)
+            nc.gpsimd.tensor_tensor(out=cy[:], in0=scaled[:], in1=bias_c_rows[:], op=ALU.add)
+            state[i]["cy"] = cy
+            nc.sync.dma_start(out=cy_rows[:, i, :], in_=cy[:])
+
         def finish_cy(i):
             cy = state[i]["cy"]
             nc.vector.scalar_tensor_tensor(
-                out=cy[:], in0=cy[:], scalar=inverse_stds[i + 3][:, 1:2], in1=bias_c,
+                out=cy[:], in0=cy[:], scalar=inverse_stds[i + 3][:, 1:2], in1=made["cell"][:, 1, :],
                 op0=ALU.mult, op1=ALU.add,
             )
             nc.sync.dma_start(out=cy_rows[:, i, :], in_=cy[:])
@@ -477,110 +604,161 @@ def tile_multilstm_pa_t_kernel(
                 piece(i, *args)
 
         with tc.manual_schedule():
-            column_sums(ps_r)
-            centre(0)
-            centre(1)
-            transpose_h0(0, 0, ps_r)
-            copy_h0(0, 0)
-            transpose_h0(0, 1, ps_r)
-            copy_h0(0, 1)
-            transpose_x(0, ps_r)
-            copy_xT(0)
-            spread_vectors(ps_misc)
-            quantise_h0(0)
-            centre(2)
-            centre(3)
-            covariance(0, ps_x)
-            covariance(1, ps_x)
-            covariance(2, ps_x)
-            for j in range(BANKS):
-                recurrent_matmul(0, j)
-            covariance(3, ps_x)
-            for j in SCALAR_BANKS:
-                scalar_mean(0, j)
-            for j in SCALAR_BANKS:
-                scalar_squares(0, j)
+            others = tuple(range(1, GROUP))
+            column_sums(ps_flow)
             for c in range(W_TILES // CHUNK):
+                centre(c)
+            transpose_h0(0, 0, ps_held)
+            copy_h0(0, 0)
+            covariance(0, ps_x)
+            spread_vectors(ps_x)
+            transpose_h0(0, 1, ps_held)
+            copy_h0(0, 1)
+            covariance(1, ps_x)
+            gain_w(0)
+            transpose_x(0, ps_x)
+            copy_xT(0)
+            quantise_h0(0)
+            for c in range(1, W_TILES // CHUNK):
                 gain_w(c)
-            for j in VECTOR_BANKS:
-                vector_stats(0, j)
+            covariance(2, ps_x)
+            covariance(3, ps_x)
             scale_covariance()
-            x_times_cov(0, ps_misc)
-            variance_of_a(0)
-            inverse_std_of_a(0)
-            for j in (0, 1, 2):
-                transpose_w(j, ps_x)
-                copy_w(j)
-            scale_x(0)
-            transpose_w(3, ps_x)
-            transpose_xhat(0, ps_misc)
-            copy_xhatT(0)
-            copy_w(3)
-            spread_cell_vectors()
-            transpose_x(1, ps_misc)
-            copy_xT(1)
+            recurrent_matmul(0, 2)
+            recurrent_matmul(0, 0)
+            recurrent_matmul(0, 1)
+            copy_out(0, 2)
+            held_mean(0, 1)
+            vector_stats(0)
+            first_variance((0,), ps_x)
+            first_variance_sum(0)
+            inverse_std_of_a(0, 0, 1)
+            transpose_w(0, ps_x)
+            copy_w(0, nc.vector.tensor_copy)
+            held_squares(0, 1)
+            recurrent_matmul(0, 3)
+            first_variance(others, ps_x)
+            for t in others:
+                first_variance_sum(t)
+            inverse_std_of_a(0, 1, GROUP)
+            halve_covariance()
+            scale_x(0, (0,))
+            copy_out(0, 3)
+            transpose_w(1, ps_x)
+            transpose_xhat(0, ps_x, (0,))
+            copy_w(1, nc.vector.tensor_copy)
+            copy_xhatT(0, 0, 1)
+            transpose_w(2, ps_const, "cell")
+            transpose_w(3, ps_const, "gain")
+            copy_w(2, nc.vector.tensor_copy)
+            copy_w(3, nc.vector.tensor_copy)
+            copied_squares(0, 2)
+            copied_squares(0, 3)
+            recurrent_matmul(1, 2)
+            x_side_matmul(0, 0)
+            aggregate_r(0)
+            scale_mean(0)
+            take_inverse_stds(0)
+            for j in HELD_BANKS:
+                gain_r(0, j)
+            scale_x(0, others)
+            transpose_xhat(0, ps_x, others)
+            copy_out(1, 2)
+            copy_xhatT(0, 1, GROUP)
+            spread_rows("gain", gain_cols)
+            recurrent_matmul(1, 3)
+            copy_out(1, 3)
+            x_side_matmul(0, 1)
+            gain_copied(0)
+            for j in HELD_BANKS:
+                recurrent_matmul(1, j)
+            recurrent_matmul(2, 2)
+            add_sides(0, 0)
+            copied_squares(1, 2)
+            copied_squares(1, 3)
+            vector_stats(1)
+            held_mean(1, 1)
+            add_sides(0, 1)
+            held_squares(1, 1)
+            gate_activation(0, 0, 1, ACT.Sigmoid)
+            x_side_matmul(0, 2)
+            copy_out(2, 2)
+            spread_rows("cell", cell_cols)
+            transpose_h0(1, 0, ps_x)
+            copy_h0(1, 0)
+            transpose_h0(1, 1, ps_x)
+            copy_h0(1, 1)
+            recurrent_matmul(2, 3)
 
-            for step in range(0, ROW_TILES + 5):
-                phase, coming = step % GROUP, step // GROUP + 1
-                prepare = 1 <= coming < N_GROUPS
-                after_coming = phase == 3 and coming + 1 < N_GROUPS
+            for step in range(1, ROW_TILES + 5):
+                def prepare(lead, piece, *args):
+                    for grp in range(1, N_GROUPS):
+                        if step == (max(1, grp * GROUP - lead) if lead < 5 else grp * GROUP - lead):
+                            piece(grp, *args)
 
-                if prepare and phase == 1:
-                    scale_x(coming)
-                piece_of(step, 4, tanh_of_cy)
-                piece_of(step, 2, new_cell)
-                piece_of(step, 1, add_sides, 0)
-                piece_of(step, 1, x_side_matmul, 2)
-                piece_of(step, 1, add_sides, 1)
+                prepare(0, transpose_xhat, ps_x)
                 piece_of(step, 1, x_side_matmul, 3)
-                piece_of(step, 1, gate_activation, 0, 1, ACT.Sigmoid)
+                if step > 1:
+                    piece_of(step, 1, add_sides, 0)
+                piece_of(step, 3, gain_cell)
                 piece_of(step, 0, aggregate_r)
+                if step > 1:
+                    piece_of(step, 1, add_sides, 1)
+                else:
+                    piece_of(step, 1, add_sides, 2)
+                piece_of(step, 2, gate_activation, 3, 3, ACT.Sigmoid)
+                piece_of(step, -1, copy_out, 3)
+                prepare(0, copy_xhatT)
+                if step > 1:
+                    piece_of(step, 1, gate_activation, 0, 1, ACT.Sigmoid)
+                piece_of(step, 0, x_side_matmul, 0)
+                prepare(1, copy_variance)
+                piece_of(step, 4, tanh_of_cy)
+                piece_of(step, -1, copied_squares, 2)
+                piece_of(step, -1, copied_squares, 3)
+                for j in HELD_BANKS:
+                    piece_of(step, 0, gain_r, j)
+                piece_of(step, 2, kept_cell)
+                piece_of(step, 2, fresh_cell)
+                piece_of(step, 0, scale_mean)
+                piece_of(step, 2, new_cell)
                 if 0 <= step < ROW_TILES + 3:
                     take_inverse_stds(step)
-                for j in range(BANKS):
-                    piece_of(step, 0, gain_r, j)
-                for j in range(BANKS):
-                    piece_of(step, -1, recurrent_matmul, j)
-                if prepare and phase == 0:
-                    x_times_cov(coming, ps_misc)
-                if prepare and phase == 1:
-                    transpose_h0(coming, 1, ps_misc)
-                for j in SCALAR_BANKS:
-                    piece_of(step, -1, scalar_mean, j)
+                if finishes_on_gpsimd(step - 3):
+                    piece_of(step, 3, finish_cy_gpsimd)
                 piece_of(step, 4, finish_hy)
-                piece_of(step, 1, add_sides, 2)
-                piece_of(step, 0, x_side_matmul, 0)
-                piece_of(step, 1, gate_activation, 2, 2, ACT.Tanh)
-                if prepare and phase == 1:
-                    copy_h0(coming, 1)
-                for j in SCALAR_BANKS:
-                    piece_of(step, -1, scalar_squares, j)
-                for j in VECTOR_BANKS:
-                    piece_of(step, -1, vector_stats, j)
-                piece_of(step, 3, gain_cell)
-                if prepare and phase == 2:
-                    quantise_h0(coming)
-                if prepare and phase == 0:
-                    variance_of_a(coming)
-                piece_of(step, 1, add_sides, 3)
+                prepare(1, inverse_std_of_a)
+                prepare(1, scale_group)
+                for j in HELD_BANKS:
+                    piece_of(step, -1, recurrent_matmul, j)
+                piece_of(step, -2, recurrent_matmul, 2)
+                if step > 1:
+                    piece_of(step, 1, add_sides, 2)
                 piece_of(step, 0, x_side_matmul, 1)
-                piece_of(step, 1, gate_activation, 3, 3, ACT.Sigmoid)
-                if after_coming:
-                    transpose_x(coming + 1, ps_misc)
-                if prepare and phase == 0:
-                    transpose_h0(coming, 0, ps_misc)
-                if prepare and phase == 1:
-                    transpose_xhat(coming, ps_misc)
+                prepare(2, weigh_covx)
+                piece_of(step, 1, gate_activation, 2, 2, ACT.Tanh)
+                piece_of(step, -1, held_mean, 1)
+                piece_of(step, -1, held_squares, 1)
+                piece_of(step, -2, copy_out, 2)
+                piece_of(step, 0, gain_copied)
+                piece_of(step, 1, add_sides, 3)
+                piece_of(step, 2, cell_stats)
+                if not finishes_on_gpsimd(step - 3):
+                    piece_of(step, 3, finish_cy)
+                piece_of(step, -1, vector_stats)
                 piece_of(step, 2, aggregate_cell)
-                piece_of(step, 3, finish_cy)
-
-                if after_coming:
-                    copy_xT(coming + 1)
-                if prepare and phase == 0:
-                    copy_h0(coming, 0)
-                    inverse_std_of_a(coming)
-                if prepare and phase == 1:
-                    copy_xhatT(coming)
-                if 1 <= coming and coming + 1 < N_GROUPS and phase == 2:
-                    load_h0(coming + 1)
-                    load_c0(coming + 1)
+                prepare(6, transpose_h0, 0, ps_x)
+                prepare(6, copy_h0, 0)
+                prepare(5, transpose_h0, 1, ps_x)
+                prepare(5, copy_h0, 1)
+                prepare(4, transpose_x, ps_x)
+                prepare(4, copy_xT)
+                prepare(4, quantise_h0)
+                prepare(2, sum_variance, ps_x)
+                piece_of(step, 0, x_side_matmul, 2)
+                prepare(3, cov_times_x, ps_x)
+                piece_of(step, -2, recurrent_matmul, 3)
+                if step % GROUP == 3 and step // GROUP + 3 < N_GROUPS:
+                    load_h0(step // GROUP + 3)
+                if step % GROUP == 2 and step // GROUP + 2 < N_GROUPS:
+                    load_c0(step // GROUP + 2)

@@ -27,7 +27,7 @@ N_GROUPS = ROW_TILES // GROUP
 W_TILES = G // P
 C_STAT_WIDTH = 6 + 3
 STAT_TILES = 4
-X_BANKS = 3
+X_BANKS = 2
 HELD_BANKS = (0, 1)
 COPIED_BANKS = (2, 3)
 SCALAR_BANKS = (1, 2, 3)
@@ -74,6 +74,7 @@ def tile_multilstm_pa_t_kernel(
         ps_held = ctx.enter_context(tc.psum_pool(name="ps_held", bufs=len(HELD_BANKS)))
         ps_flow = ctx.enter_context(tc.psum_pool(name="ps_flow", bufs=1))
         ps_x = ctx.enter_context(tc.psum_pool(name="ps_x", bufs=X_BANKS))
+        ps_prep = ctx.enter_context(tc.psum_pool(name="ps_prep", bufs=1))
         ps_const = ctx.enter_context(tc.psum_pool(name="ps_const", bufs=1))
 
         groups = {}
@@ -208,11 +209,14 @@ def tile_multilstm_pa_t_kernel(
                 )
             groups[grp]["covx_ps"] = covx_ps
 
+        def copy_covx(grp):
+            covx = prepared.tile([V, GROUP, P], F32)
+            nc.scalar.copy(out=covx[:], in_=groups[grp]["covx_ps"][:])
+            groups[grp]["covx"] = covx
+
         def weigh_covx(grp):
             x_covx = prepared.tile([V, GROUP, P], F32)
-            nc.vector.tensor_tensor(
-                out=x_covx[:], in0=groups[grp]["covx_ps"][:], in1=groups[grp]["xT"][:], op=ALU.mult
-            )
+            nc.gpsimd.tensor_tensor(out=x_covx[:], in0=groups[grp]["covx"][:], in1=groups[grp]["xT"][:], op=ALU.mult)
             groups[grp]["x_covx"] = x_covx
 
         def sum_variance(grp, banks):
@@ -611,12 +615,12 @@ def tile_multilstm_pa_t_kernel(
             transpose_h0(0, 0, ps_held)
             copy_h0(0, 0)
             covariance(0, ps_x)
-            spread_vectors(ps_x)
+            spread_vectors(ps_prep)
             transpose_h0(0, 1, ps_held)
             copy_h0(0, 1)
             covariance(1, ps_x)
             gain_w(0)
-            transpose_x(0, ps_x)
+            transpose_x(0, ps_prep)
             copy_xT(0)
             quantise_h0(0)
             for c in range(1, W_TILES // CHUNK):
@@ -630,7 +634,7 @@ def tile_multilstm_pa_t_kernel(
             copy_out(0, 2)
             held_mean(0, 1)
             vector_stats(0)
-            first_variance((0,), ps_x)
+            first_variance((0,), ps_prep)
             first_variance_sum(0)
             inverse_std_of_a(0, 0, 1)
             transpose_w(0, ps_x)
@@ -645,7 +649,7 @@ def tile_multilstm_pa_t_kernel(
             scale_x(0, (0,))
             copy_out(0, 3)
             transpose_w(1, ps_x)
-            transpose_xhat(0, ps_x, (0,))
+            transpose_xhat(0, ps_prep, (0,))
             copy_w(1, nc.vector.tensor_copy)
             copy_xhatT(0, 0, 1)
             transpose_w(2, ps_const, "cell")
@@ -662,7 +666,7 @@ def tile_multilstm_pa_t_kernel(
             for j in HELD_BANKS:
                 gain_r(0, j)
             scale_x(0, others)
-            transpose_xhat(0, ps_x, others)
+            transpose_xhat(0, ps_prep, others)
             copy_out(1, 2)
             copy_xhatT(0, 1, GROUP)
             spread_rows("gain", gain_cols)
@@ -673,90 +677,82 @@ def tile_multilstm_pa_t_kernel(
             for j in HELD_BANKS:
                 recurrent_matmul(1, j)
             recurrent_matmul(2, 2)
-            add_sides(0, 0)
             copied_squares(1, 2)
             copied_squares(1, 3)
             vector_stats(1)
             held_mean(1, 1)
-            add_sides(0, 1)
-            held_squares(1, 1)
-            gate_activation(0, 0, 1, ACT.Sigmoid)
-            x_side_matmul(0, 2)
-            copy_out(2, 2)
             spread_rows("cell", cell_cols)
-            transpose_h0(1, 0, ps_x)
+            transpose_h0(1, 0, ps_prep)
+            held_squares(1, 1)
             copy_h0(1, 0)
-            transpose_h0(1, 1, ps_x)
+            copy_out(2, 2)
+            transpose_x(1, ps_prep)
+            copy_xT(1)
+            transpose_h0(1, 1, ps_prep)
             copy_h0(1, 1)
+            quantise_h0(1)
             recurrent_matmul(2, 3)
+            cov_times_x(1, ps_prep)
 
             for step in range(1, ROW_TILES + 5):
                 def prepare(lead, piece, *args):
                     for grp in range(1, N_GROUPS):
-                        if step == (max(1, grp * GROUP - lead) if lead < 5 else grp * GROUP - lead):
+                        if step == grp * GROUP - lead:
                             piece(grp, *args)
 
-                prepare(0, transpose_xhat, ps_x)
-                piece_of(step, 1, x_side_matmul, 3)
-                if step > 1:
-                    piece_of(step, 1, add_sides, 0)
-                piece_of(step, 3, gain_cell)
-                piece_of(step, 0, aggregate_r)
-                if step > 1:
-                    piece_of(step, 1, add_sides, 1)
-                else:
-                    piece_of(step, 1, add_sides, 2)
-                piece_of(step, 2, gate_activation, 3, 3, ACT.Sigmoid)
+                piece_of(step, 1, add_sides, 0)
+                piece_of(step, 1, x_side_matmul, 2)
+                piece_of(step, 4, tanh_of_cy)
                 piece_of(step, -1, copy_out, 3)
                 prepare(0, copy_xhatT)
-                if step > 1:
-                    piece_of(step, 1, gate_activation, 0, 1, ACT.Sigmoid)
-                piece_of(step, 0, x_side_matmul, 0)
-                prepare(1, copy_variance)
-                piece_of(step, 4, tanh_of_cy)
+                prepare(5, copy_xT)
+                prepare(3, copy_covx)
+                prepare(2, copy_variance)
+                piece_of(step, 3, gain_cell)
+                piece_of(step, 0, aggregate_r)
+                piece_of(step, 1, add_sides, 1)
+                piece_of(step, 1, x_side_matmul, 3)
                 piece_of(step, -1, copied_squares, 2)
+                piece_of(step, 1, gate_activation, 0, 1, ACT.Sigmoid)
                 piece_of(step, -1, copied_squares, 3)
                 for j in HELD_BANKS:
                     piece_of(step, 0, gain_r, j)
+                prepare(6, transpose_h0, 0, ps_prep)
+                prepare(5, transpose_h0, 1, ps_prep)
                 piece_of(step, 2, kept_cell)
                 piece_of(step, 2, fresh_cell)
                 piece_of(step, 0, scale_mean)
                 piece_of(step, 2, new_cell)
                 if 0 <= step < ROW_TILES + 3:
                     take_inverse_stds(step)
-                if finishes_on_gpsimd(step - 3):
-                    piece_of(step, 3, finish_cy_gpsimd)
                 piece_of(step, 4, finish_hy)
-                prepare(1, inverse_std_of_a)
-                prepare(1, scale_group)
+                prepare(3, weigh_covx)
+                prepare(2, inverse_std_of_a)
+                prepare(2, scale_group)
                 for j in HELD_BANKS:
                     piece_of(step, -1, recurrent_matmul, j)
                 piece_of(step, -2, recurrent_matmul, 2)
-                if step > 1:
-                    piece_of(step, 1, add_sides, 2)
-                piece_of(step, 0, x_side_matmul, 1)
-                prepare(2, weigh_covx)
+                piece_of(step, 1, add_sides, 2)
+                piece_of(step, 0, x_side_matmul, 0)
                 piece_of(step, 1, gate_activation, 2, 2, ACT.Tanh)
                 piece_of(step, -1, held_mean, 1)
-                piece_of(step, -1, held_squares, 1)
                 piece_of(step, -2, copy_out, 2)
+                piece_of(step, -1, held_squares, 1)
                 piece_of(step, 0, gain_copied)
                 piece_of(step, 1, add_sides, 3)
+                piece_of(step, 0, x_side_matmul, 1)
+                piece_of(step, 1, gate_activation, 3, 3, ACT.Sigmoid)
+                prepare(6, copy_h0, 0)
+                prepare(5, copy_h0, 1)
                 piece_of(step, 2, cell_stats)
-                if not finishes_on_gpsimd(step - 3):
-                    piece_of(step, 3, finish_cy)
+                piece_of(step, 3, finish_cy)
                 piece_of(step, -1, vector_stats)
                 piece_of(step, 2, aggregate_cell)
-                prepare(6, transpose_h0, 0, ps_x)
-                prepare(6, copy_h0, 0)
-                prepare(5, transpose_h0, 1, ps_x)
-                prepare(5, copy_h0, 1)
-                prepare(4, transpose_x, ps_x)
-                prepare(4, copy_xT)
                 prepare(4, quantise_h0)
-                prepare(2, sum_variance, ps_x)
-                piece_of(step, 0, x_side_matmul, 2)
-                prepare(3, cov_times_x, ps_x)
+                prepare(6, transpose_x, ps_prep)
+                prepare(4, cov_times_x, ps_prep)
+                prepare(3, sum_variance, ps_prep)
+                prepare(1, transpose_xhat, ps_prep)
                 piece_of(step, -2, recurrent_matmul, 3)
                 if step % GROUP == 3 and step // GROUP + 3 < N_GROUPS:
                     load_h0(step // GROUP + 3)

@@ -72,9 +72,8 @@ def tile_multilstm_pa_t_kernel(
         result = ctx.enter_context(tc.tile_pool(name="result", bufs=3))
         small = ctx.enter_context(tc.tile_pool(name="small", bufs=8))
         ps_held = ctx.enter_context(tc.psum_pool(name="ps_held", bufs=len(HELD_BANKS)))
-        ps_flow = ctx.enter_context(tc.psum_pool(name="ps_flow", bufs=1))
+        ps_flow = ctx.enter_context(tc.psum_pool(name="ps_flow", bufs=2))
         ps_x = ctx.enter_context(tc.psum_pool(name="ps_x", bufs=X_BANKS))
-        ps_prep = ctx.enter_context(tc.psum_pool(name="ps_prep", bufs=1))
         ps_const = ctx.enter_context(tc.psum_pool(name="ps_const", bufs=1))
 
         groups = {}
@@ -126,8 +125,6 @@ def tile_multilstm_pa_t_kernel(
 
         gain_h = const.tile([P, len(HELD_BANKS) * BANK], BF16)
         nc.sync.dma_start(out=gain_h[:], in_=lnh_w1[0 : len(HELD_BANKS) * BANK].partition_broadcast(P))
-        bias_c_rows = const.tile([P, H], BF16)
-        nc.sync.dma_start(out=bias_c_rows[:], in_=lnc_b1.partition_broadcast(P))
         nc.sync.dma_start(out=x_all[:, GROUP:ROW_TILES, :], in_=x_rows[:, GROUP:ROW_TILES, :])
         load_h0(1)
         load_c0(0)
@@ -196,7 +193,7 @@ def tile_multilstm_pa_t_kernel(
             groups[grp]["xT_ps"] = xT_ps
 
         def copy_xT(grp):
-            xT = prepared.tile([V, GROUP, P], F32 if grp == 0 else BF16, name="xT_first" if grp == 0 else "xT")
+            xT = prepared.tile([V, GROUP, P], F32 if grp < 2 else BF16, name="xT_first" if grp < 2 else "xT")
             nc.scalar.copy(out=xT[:], in_=groups[grp]["xT_ps"][:])
             groups[grp]["xT"] = xT
 
@@ -246,22 +243,22 @@ def tile_multilstm_pa_t_kernel(
             for t in range(first, last):
                 groups[grp]["rstd_a", t] = rstd_a[:, t - first : t - first + 1]
 
-        def first_variance(tiles, banks):
+        def first_variance(grp, tiles, banks):
             xcov_ps = banks.tile([P, len(tiles), V], F32, tag="bank")
             for k, t in enumerate(tiles):
                 nc.tensor.matmul(
-                    out=xcov_ps[:, k, :], lhsT=groups[0]["xT"][:, t, :], rhs=cov[:], start=True, stop=True
+                    out=xcov_ps[:, k, :], lhsT=groups[grp]["xT"][:, t, :], rhs=cov[:], start=True, stop=True
                 )
-                made["xcov", t] = xcov_ps[:, k, :]
+                groups[grp]["xcov", t] = xcov_ps[:, k, :]
 
-        def first_variance_sum(t):
+        def first_variance_sum(grp, t):
             if t == 0:
                 var_a = small.tile([P, GROUP], F32)
-                groups[0]["var_a"] = var_a
+                groups[grp]["var_a"] = var_a
             unread_x = setup.tile([P, V], F32)
             nc.vector.scalar_tensor_tensor(
-                out=unread_x[:], in0=made["xcov", t], scalar=1.0, in1=x_all[:, t, :],
-                op0=ALU.mult, op1=ALU.mult, accum_out=groups[0]["var_a"][:, t : t + 1],
+                out=unread_x[:], in0=groups[grp]["xcov", t], scalar=1.0, in1=x_all[:, grp * GROUP + t, :],
+                op0=ALU.mult, op1=ALU.mult, accum_out=groups[grp]["var_a"][:, t : t + 1],
             )
 
         def scale_group(grp):
@@ -498,7 +495,8 @@ def tile_multilstm_pa_t_kernel(
             )
 
         def x_side_matmul(i, j):
-            x_ps = ps_x.tile([P, BANK], F32, tag="bank")
+            banks = ps_flow if i >= ROW_TILES - 2 and j >= 2 else ps_x
+            x_ps = banks.tile([P, BANK], F32, tag="bank")
             nc.tensor.matmul(
                 out=x_ps[:], lhsT=groups[i // GROUP]["xhatT"][:, i % GROUP, :], rhs=w_x[:, bank(j)],
                 start=True, stop=False,
@@ -531,12 +529,9 @@ def tile_multilstm_pa_t_kernel(
         def products_engine(i):
             return nc.vector if i == ROW_TILES - 1 else nc.gpsimd
 
-        def finishes_on_gpsimd(i):
-            return False
-
         def kept_cell(i):
             kept = cell.tile([P, H], F32)
-            products_engine(i).tensor_tensor(
+            nc.gpsimd.tensor_tensor(
                 out=kept[:], in0=state[i]["gates"][:, bank(1)], in1=groups[i // GROUP]["c0"][:, i % GROUP, :],
                 op=ALU.mult,
             )
@@ -569,17 +564,6 @@ def tile_multilstm_pa_t_kernel(
                 op0=ALU.subtract, op1=ALU.mult,
             )
             state[i]["cy"] = cy
-
-        def finish_cy_gpsimd(i):
-            scaled = cell.tile([P, H], F32)
-            nc.gpsimd.tensor_scalar(
-                out=scaled[:], in0=state[i]["cy"][:], scalar1=inverse_stds[i + 3][:, 1:2], scalar2=0.0,
-                op0=ALU.mult, op1=ALU.add,
-            )
-            cy = result.tile([P, H], F32)
-            nc.gpsimd.tensor_tensor(out=cy[:], in0=scaled[:], in1=bias_c_rows[:], op=ALU.add)
-            state[i]["cy"] = cy
-            nc.sync.dma_start(out=cy_rows[:, i, :], in_=cy[:])
 
         def finish_cy(i):
             cy = state[i]["cy"]
@@ -615,12 +599,12 @@ def tile_multilstm_pa_t_kernel(
             transpose_h0(0, 0, ps_held)
             copy_h0(0, 0)
             covariance(0, ps_x)
-            spread_vectors(ps_prep)
+            spread_vectors(ps_flow)
             transpose_h0(0, 1, ps_held)
             copy_h0(0, 1)
             covariance(1, ps_x)
             gain_w(0)
-            transpose_x(0, ps_prep)
+            transpose_x(0, ps_flow)
             copy_xT(0)
             quantise_h0(0)
             for c in range(1, W_TILES // CHUNK):
@@ -634,22 +618,22 @@ def tile_multilstm_pa_t_kernel(
             copy_out(0, 2)
             held_mean(0, 1)
             vector_stats(0)
-            first_variance((0,), ps_prep)
-            first_variance_sum(0)
+            first_variance(0, (0,), ps_flow)
+            first_variance_sum(0, 0)
             inverse_std_of_a(0, 0, 1)
             transpose_w(0, ps_x)
             copy_w(0, nc.vector.tensor_copy)
             held_squares(0, 1)
             recurrent_matmul(0, 3)
-            first_variance(others, ps_x)
+            first_variance(0, others, ps_x)
             for t in others:
-                first_variance_sum(t)
+                first_variance_sum(0, t)
             inverse_std_of_a(0, 1, GROUP)
             halve_covariance()
             scale_x(0, (0,))
             copy_out(0, 3)
             transpose_w(1, ps_x)
-            transpose_xhat(0, ps_prep, (0,))
+            transpose_xhat(0, ps_flow, (0,))
             copy_w(1, nc.vector.tensor_copy)
             copy_xhatT(0, 0, 1)
             transpose_w(2, ps_const, "cell")
@@ -666,7 +650,7 @@ def tile_multilstm_pa_t_kernel(
             for j in HELD_BANKS:
                 gain_r(0, j)
             scale_x(0, others)
-            transpose_xhat(0, ps_prep, others)
+            transpose_xhat(0, ps_flow, others)
             copy_out(1, 2)
             copy_xhatT(0, 1, GROUP)
             spread_rows("gain", gain_cols)
@@ -677,39 +661,41 @@ def tile_multilstm_pa_t_kernel(
             for j in HELD_BANKS:
                 recurrent_matmul(1, j)
             recurrent_matmul(2, 2)
+            recurrent_matmul(2, 3)
             copied_squares(1, 2)
             copied_squares(1, 3)
             vector_stats(1)
             held_mean(1, 1)
-            spread_rows("cell", cell_cols)
-            transpose_h0(1, 0, ps_prep)
-            held_squares(1, 1)
-            copy_h0(1, 0)
             copy_out(2, 2)
-            transpose_x(1, ps_prep)
-            copy_xT(1)
-            transpose_h0(1, 1, ps_prep)
-            copy_h0(1, 1)
-            quantise_h0(1)
-            recurrent_matmul(2, 3)
-            cov_times_x(1, ps_prep)
+            held_squares(1, 1)
+            copy_out(2, 3)
+            spread_rows("cell", cell_cols)
+            transpose_h0(1, 0, ps_flow)
+            copy_h0(1, 0)
 
-            for step in range(1, ROW_TILES + 5):
+            for step in range(1, ROW_TILES):
                 def prepare(lead, piece, *args):
-                    for grp in range(1, N_GROUPS):
+                    for grp in range(2, N_GROUPS):
                         if step == grp * GROUP - lead:
                             piece(grp, *args)
 
+                def prepare_second(at, piece, *args):
+                    if step == at:
+                        piece(1, *args)
+
                 piece_of(step, 1, add_sides, 0)
                 piece_of(step, 1, x_side_matmul, 2)
+                prepare_second(1, transpose_x, ps_flow)
                 piece_of(step, 4, tanh_of_cy)
-                piece_of(step, -1, copy_out, 3)
+                prepare_second(1, copy_xT)
+                prepare_second(4, copy_xhatT)
                 prepare(0, copy_xhatT)
                 prepare(5, copy_xT)
                 prepare(3, copy_covx)
                 prepare(2, copy_variance)
                 piece_of(step, 3, gain_cell)
                 piece_of(step, 0, aggregate_r)
+                prepare_second(2, quantise_h0)
                 piece_of(step, 1, add_sides, 1)
                 piece_of(step, 1, x_side_matmul, 3)
                 piece_of(step, -1, copied_squares, 2)
@@ -717,8 +703,6 @@ def tile_multilstm_pa_t_kernel(
                 piece_of(step, -1, copied_squares, 3)
                 for j in HELD_BANKS:
                     piece_of(step, 0, gain_r, j)
-                prepare(6, transpose_h0, 0, ps_prep)
-                prepare(5, transpose_h0, 1, ps_prep)
                 piece_of(step, 2, kept_cell)
                 piece_of(step, 2, fresh_cell)
                 piece_of(step, 0, scale_mean)
@@ -727,34 +711,84 @@ def tile_multilstm_pa_t_kernel(
                     take_inverse_stds(step)
                 piece_of(step, 4, finish_hy)
                 prepare(3, weigh_covx)
+                if step == 2:
+                    for t in range(GROUP):
+                        first_variance_sum(1, t)
+                prepare_second(2, inverse_std_of_a)
+                prepare_second(2, scale_group)
                 prepare(2, inverse_std_of_a)
                 prepare(2, scale_group)
                 for j in HELD_BANKS:
                     piece_of(step, -1, recurrent_matmul, j)
                 piece_of(step, -2, recurrent_matmul, 2)
+                piece_of(step, -2, recurrent_matmul, 3)
                 piece_of(step, 1, add_sides, 2)
                 piece_of(step, 0, x_side_matmul, 0)
                 piece_of(step, 1, gate_activation, 2, 2, ACT.Tanh)
                 piece_of(step, -1, held_mean, 1)
                 piece_of(step, -2, copy_out, 2)
                 piece_of(step, -1, held_squares, 1)
+                piece_of(step, -2, copy_out, 3)
                 piece_of(step, 0, gain_copied)
                 piece_of(step, 1, add_sides, 3)
+                prepare(6, transpose_h0, 0, ps_flow)
+                prepare(5, transpose_h0, 1, ps_flow)
+                prepare_second(1, transpose_h0, 1, ps_flow)
                 piece_of(step, 0, x_side_matmul, 1)
                 piece_of(step, 1, gate_activation, 3, 3, ACT.Sigmoid)
                 prepare(6, copy_h0, 0)
                 prepare(5, copy_h0, 1)
+                prepare_second(1, copy_h0, 1)
                 piece_of(step, 2, cell_stats)
                 piece_of(step, 3, finish_cy)
                 piece_of(step, -1, vector_stats)
                 piece_of(step, 2, aggregate_cell)
-                prepare(4, quantise_h0)
-                prepare(6, transpose_x, ps_prep)
-                prepare(4, cov_times_x, ps_prep)
-                prepare(3, sum_variance, ps_prep)
-                prepare(1, transpose_xhat, ps_prep)
-                piece_of(step, -2, recurrent_matmul, 3)
+                prepare(3, quantise_h0)
+                prepare(6, transpose_x, ps_flow)
+                prepare(4, cov_times_x, ps_flow)
+                prepare(3, sum_variance, ps_flow)
+                prepare_second(1, first_variance, range(GROUP), ps_flow)
+                prepare(1, transpose_xhat, ps_flow)
+                prepare_second(3, transpose_xhat, ps_flow)
                 if step % GROUP == 3 and step // GROUP + 3 < N_GROUPS:
                     load_h0(step // GROUP + 3)
                 if step % GROUP == 2 and step // GROUP + 2 < N_GROUPS:
                     load_c0(step // GROUP + 2)
+
+            last = ROW_TILES - 1
+            add_sides(last, 0)
+            tanh_of_cy(last - 3)
+            gain_cell(last - 2)
+            kept_cell(last - 1)
+            fresh_cell(last - 1)
+            x_side_matmul(last, 2)
+            add_sides(last, 1)
+            gate_activation(last, 0, 1, ACT.Sigmoid)
+            x_side_matmul(last, 3)
+            new_cell(last - 1)
+            take_inverse_stds(last + 1)
+            finish_hy(last - 3)
+            add_sides(last, 2)
+            gate_activation(last, 2, 2, ACT.Tanh)
+            kept_cell(last)
+            cell_stats(last - 1)
+            add_sides(last, 3)
+            aggregate_cell(last - 1)
+            take_inverse_stds(last + 2)
+            gate_activation(last, 3, 3, ACT.Sigmoid)
+            fresh_cell(last)
+            finish_cy(last - 2)
+            new_cell(last)
+            tanh_of_cy(last - 2)
+            gain_cell(last - 1)
+            cell_stats(last)
+            finish_cy(last - 1)
+            aggregate_cell(last)
+            finish_hy(last - 2)
+            take_inverse_stds(last + 3)
+            tanh_of_cy(last - 1)
+            gain_cell(last)
+            finish_cy(last)
+            tanh_of_cy(last)
+            finish_hy(last - 1)
+            finish_hy(last)

@@ -497,20 +497,26 @@ def tile_multilstm_pa_t_kernel(
         def x_side_matmul(i, j):
             banks = ps_flow if i >= ROW_TILES - 2 and j >= 2 else ps_x
             x_ps = banks.tile([P, BANK], F32, tag="bank")
-            nc.tensor.matmul(
-                out=x_ps[:], lhsT=groups[i // GROUP]["xhatT"][:, i % GROUP, :], rhs=w_x[:, bank(j)],
-                start=True, stop=False,
-            )
-            for q in range(BANK // P):
-                col = j * (BANK // P) + q
+            def product(start):
                 nc.tensor.matmul(
-                    out=x_ps[:, q * P : (q + 1) * P],
-                    lhsT=bias_cols[:, col : col + 1].to_broadcast([P, P]),
-                    rhs=ident_f32[:],
-                    is_transpose=True,
-                    start=False,
-                    stop=(q == BANK // P - 1),
+                    out=x_ps[:], lhsT=groups[i // GROUP]["xhatT"][:, i % GROUP, :], rhs=w_x[:, bank(j)],
+                    start=start, stop=not start,
                 )
+
+            def biases(start):
+                for q in range(BANK // P):
+                    col = j * (BANK // P) + q
+                    nc.tensor.matmul(
+                        out=x_ps[:, q * P : (q + 1) * P],
+                        lhsT=bias_cols[:, col : col + 1].to_broadcast([P, P]),
+                        rhs=ident_f32[:],
+                        is_transpose=True,
+                        start=start and q == 0,
+                        stop=not start and q == BANK // P - 1,
+                    )
+
+            for k, part in enumerate((product, biases) if j % 2 == 0 else (biases, product)):
+                part(k == 0)
             state[i]["x_ps", j] = x_ps
 
         def add_sides(i, j):

@@ -464,9 +464,7 @@ def tile_multilstm_pa_t_kernel(
 
         def scale_mean(i):
             small_mean = small.tile([P, 1], F32)
-            nc.gpsimd.tensor_scalar(
-                out=small_mean[:], in0=moments[i][:, 0:1], scalar1=1.0 / BANK, scalar2=0.0, op0=ALU.mult, op1=ALU.add
-            )
+            nc.scalar.activation(out=small_mean[:], in_=moments[i][:, 0:1], func=ACT.Copy, scale=1.0 / BANK)
             state[i]["small_mean"] = small_mean
 
         def take_inverse_stds(m):
@@ -693,6 +691,8 @@ def tile_multilstm_pa_t_kernel(
                 piece_of(step, 1, x_side_matmul, 2)
                 prepare_second(1, transpose_x, ps_flow)
                 piece_of(step, 4, tanh_of_cy)
+                prepare_second(3, scale_x)
+                prepare(1, scale_x)
                 prepare_second(1, copy_xT)
                 prepare_second(4, copy_xhatT)
                 prepare(0, copy_xhatT)
@@ -705,13 +705,13 @@ def tile_multilstm_pa_t_kernel(
                 piece_of(step, 1, add_sides, 1)
                 piece_of(step, 1, x_side_matmul, 3)
                 piece_of(step, -1, copied_squares, 2)
+                piece_of(step, 0, scale_mean)
                 piece_of(step, 1, gate_activation, 0, 1, ACT.Sigmoid)
                 piece_of(step, -1, copied_squares, 3)
                 for j in HELD_BANKS:
                     piece_of(step, 0, gain_r, j)
                 piece_of(step, 2, kept_cell)
                 piece_of(step, 2, fresh_cell)
-                piece_of(step, 0, scale_mean)
                 piece_of(step, 2, new_cell)
                 if 0 <= step < ROW_TILES + 3:
                     take_inverse_stds(step)
@@ -721,9 +721,7 @@ def tile_multilstm_pa_t_kernel(
                     for t in range(GROUP):
                         first_variance_sum(1, t)
                 prepare_second(2, inverse_std_of_a)
-                prepare_second(2, scale_group)
                 prepare(2, inverse_std_of_a)
-                prepare(2, scale_group)
                 for j in HELD_BANKS:
                     piece_of(step, -1, recurrent_matmul, j)
                 piece_of(step, -2, recurrent_matmul, 2)

@@ -170,9 +170,9 @@ def tile_multilstm_pa_t_kernel(
                     nc.tensor.transpose(out=hT_ps[:, t, u, :], in_=words[:, u : H // 2 : 2], identity=ident_f32[:])
             groups[grp]["hT_ps"] = hT_ps
 
-        def copy_h0(grp, half):
+        def copy_h0(grp, half, copy=None):
             grouped_words = groups[grp]["grouped"][:].bitcast(F32).rearrange("p (t b u) -> p t b u", t=GROUP, u=2)
-            nc.scalar.copy(
+            (copy or nc.scalar.copy)(
                 out=grouped_words[:, 2 * half : 2 * half + 2, :, :],
                 in_=groups[grp]["hT_ps"][:].rearrange("p t u b -> p t b u"),
             )
@@ -193,7 +193,7 @@ def tile_multilstm_pa_t_kernel(
             groups[grp]["xT_ps"] = xT_ps
 
         def copy_xT(grp):
-            xT = prepared.tile([V, GROUP, P], F32 if grp < 2 else BF16, name="xT_first" if grp < 2 else "xT")
+            xT = prepared.tile([V, GROUP, P], F32 if grp == 0 else BF16, name="xT_first" if grp == 0 else "xT")
             nc.scalar.copy(out=xT[:], in_=groups[grp]["xT_ps"][:])
             groups[grp]["xT"] = xT
 
@@ -246,9 +246,12 @@ def tile_multilstm_pa_t_kernel(
         def first_variance(grp, tiles, banks):
             xcov_ps = banks.tile([P, len(tiles), V], F32, tag="bank")
             for k, t in enumerate(tiles):
-                nc.tensor.matmul(
-                    out=xcov_ps[:, k, :], lhsT=groups[grp]["xT"][:, t, :], rhs=cov[:], start=True, stop=True
-                )
+                factors = (cov[:],) if grp == 0 else (cov_halves[:, 0, :], cov_halves[:, 1, :])
+                for n, factor in enumerate(factors):
+                    nc.tensor.matmul(
+                        out=xcov_ps[:, k, :], lhsT=groups[grp]["xT"][:, t, :], rhs=factor,
+                        start=(n == 0), stop=(n == len(factors) - 1),
+                    )
                 groups[grp]["xcov", t] = xcov_ps[:, k, :]
 
         def first_variance_sum(grp, t):
@@ -690,6 +693,7 @@ def tile_multilstm_pa_t_kernel(
                 piece_of(step, 1, add_sides, 0)
                 piece_of(step, 1, x_side_matmul, 2)
                 prepare_second(1, transpose_x, ps_flow)
+                piece_of(step, -1, copied_squares, 2)
                 piece_of(step, 4, tanh_of_cy)
                 prepare_second(3, scale_x)
                 prepare(1, scale_x)
@@ -704,7 +708,6 @@ def tile_multilstm_pa_t_kernel(
                 prepare_second(2, quantise_h0)
                 piece_of(step, 1, add_sides, 1)
                 piece_of(step, 1, x_side_matmul, 3)
-                piece_of(step, -1, copied_squares, 2)
                 piece_of(step, 0, scale_mean)
                 piece_of(step, 1, gate_activation, 0, 1, ACT.Sigmoid)
                 piece_of(step, -1, copied_squares, 3)
@@ -729,10 +732,10 @@ def tile_multilstm_pa_t_kernel(
                 piece_of(step, 1, add_sides, 2)
                 piece_of(step, 0, x_side_matmul, 0)
                 piece_of(step, 1, gate_activation, 2, 2, ACT.Tanh)
-                piece_of(step, -1, held_mean, 1)
                 piece_of(step, -2, copy_out, 2)
-                piece_of(step, -1, held_squares, 1)
+                piece_of(step, -1, held_mean, 1)
                 piece_of(step, -2, copy_out, 3)
+                piece_of(step, -1, held_squares, 1)
                 piece_of(step, 0, gain_copied)
                 piece_of(step, 1, add_sides, 3)
                 prepare(6, transpose_h0, 0, ps_flow)
@@ -740,12 +743,12 @@ def tile_multilstm_pa_t_kernel(
                 prepare_second(1, transpose_h0, 1, ps_flow)
                 piece_of(step, 0, x_side_matmul, 1)
                 piece_of(step, 1, gate_activation, 3, 3, ACT.Sigmoid)
-                prepare(6, copy_h0, 0)
                 prepare(5, copy_h0, 1)
-                prepare_second(1, copy_h0, 1)
                 piece_of(step, 2, cell_stats)
                 piece_of(step, 3, finish_cy)
                 piece_of(step, -1, vector_stats)
+                prepare_second(1, copy_h0, 1, nc.vector.tensor_copy)
+                prepare(6, copy_h0, 0, nc.vector.tensor_copy)
                 piece_of(step, 2, aggregate_cell)
                 prepare(3, quantise_h0)
                 prepare(6, transpose_x, ps_flow)

@@ -145,19 +145,21 @@ def tile_multilstm_pa_t_kernel(
         nc.scalar.activation(out=table_warmer[:], in_=neg_half[:, 0:1], func=ACT.Sigmoid)
         r_stats_tiles = []
         c_stats_tiles = []
-        for k in range(STAT_TILES):
+        for k in range(STAT_TILES + 1):
             r_stats = const.tile([P, STAT_WIDTH], F32, name="r_stats%d" % k)
             nc.vector.memset(r_stats[:], 0.0)
             r_stats_tiles.append(r_stats)
             c_stats = const.tile([P, C_STAT_WIDTH], F32, name="c_stats%d" % k)
             nc.vector.memset(c_stats[:], 0.0)
             c_stats_tiles.append(c_stats)
-        for r_stats, c_stats in zip(r_stats_tiles, c_stats_tiles):
+        nc.vector.memset(r_stats_tiles[STAT_TILES][:, 0:1], float(BANK))
+        for r_stats in r_stats_tiles:
             nc.vector.memset(r_stats[:, 6 : 6 + 3 * len(SCALAR_BANKS) : 3], float(BANK))
-            for stats, width, count in ((r_stats, STAT_WIDTH, G), (c_stats, C_STAT_WIDTH, H)):
-                nc.vector.tensor_scalar_add(
-                    out=stats[:, width - 1 : width], in0=stats[:, width - 3 : width - 2], scalar1=EPS * count
-                )
+        for stats, count in [(tile, G) for tile in r_stats_tiles] + [(tile, H) for tile in c_stats_tiles]:
+            width = stats.shape[1]
+            nc.vector.tensor_scalar_add(
+                out=stats[:, width - 1 : width], in0=stats[:, width - 3 : width - 2], scalar1=EPS * count
+            )
 
         def transpose_h0(grp, half, banks):
             if half == 0:
@@ -410,13 +412,16 @@ def tile_multilstm_pa_t_kernel(
             )
             state.setdefault(i, {})["r_ps", j] = r_ps
 
+        def stats_of(i):
+            return r_stats_tiles[STAT_TILES if i == ROW_TILES - 1 else i % STAT_TILES]
+
         def mean_col(i, j):
-            col = 6 + 3 * SCALAR_BANKS.index(j) + 1
-            return r_stats_tiles[i % STAT_TILES][:, col : col + 1]
+            col = (3 + 3 * j if j > 0 else 0) + 1
+            return stats_of(i)[:, col : col + 1]
 
         def squares_col(i, j):
-            col = 6 + 3 * SCALAR_BANKS.index(j) + 2
-            return r_stats_tiles[i % STAT_TILES][:, col : col + 1]
+            col = (3 + 3 * j if j > 0 else 0) + 2
+            return stats_of(i)[:, col : col + 1]
 
         def held_mean(i, j):
             unread = wide.tile([P, BANK], BF16, bufs=1)
@@ -451,7 +456,8 @@ def tile_multilstm_pa_t_kernel(
             )
 
         def vector_stats(i):
-            nc.vector.bn_stats(out=r_stats_tiles[i % STAT_TILES][:, 0:6], in_=state[i]["r_ps", 0][:])
+            if i < ROW_TILES - 1:
+                nc.vector.bn_stats(out=stats_of(i)[:, 0:6], in_=state[i]["r_ps", 0][:])
 
         moments = {}
         inverse_stds = {}
@@ -463,7 +469,7 @@ def tile_multilstm_pa_t_kernel(
             return moments[m]
 
         def aggregate_r(i):
-            nc.vector.bn_aggr(out=moments_of(i)[:, 0:2], in_=r_stats_tiles[i % STAT_TILES][:])
+            nc.vector.bn_aggr(out=moments_of(i)[:, 0:2], in_=stats_of(i)[:])
 
         def scale_mean(i):
             small_mean = small.tile([P, 1], F32)
@@ -733,8 +739,12 @@ def tile_multilstm_pa_t_kernel(
                 piece_of(step, 0, x_side_matmul, 0)
                 piece_of(step, 1, gate_activation, 2, 2, ACT.Tanh)
                 piece_of(step, -2, copy_out, 2)
+                if step == ROW_TILES - 2:
+                    held_mean(ROW_TILES - 1, 0)
                 piece_of(step, -1, held_mean, 1)
                 piece_of(step, -2, copy_out, 3)
+                if step == ROW_TILES - 2:
+                    held_squares(ROW_TILES - 1, 0)
                 piece_of(step, -1, held_squares, 1)
                 piece_of(step, 0, gain_copied)
                 piece_of(step, 1, add_sides, 3)
@@ -743,12 +753,12 @@ def tile_multilstm_pa_t_kernel(
                 prepare_second(1, transpose_h0, 1, ps_flow)
                 piece_of(step, 0, x_side_matmul, 1)
                 piece_of(step, 1, gate_activation, 3, 3, ACT.Sigmoid)
+                prepare(6, copy_h0, 0)
                 prepare(5, copy_h0, 1)
                 piece_of(step, 2, cell_stats)
                 piece_of(step, 3, finish_cy)
                 piece_of(step, -1, vector_stats)
                 prepare_second(1, copy_h0, 1, nc.vector.tensor_copy)
-                prepare(6, copy_h0, 0, nc.vector.tensor_copy)
                 piece_of(step, 2, aggregate_cell)
                 prepare(3, quantise_h0)
                 prepare(6, transpose_x, ps_flow)

@@ -12,7 +12,6 @@ FP8X4 = mybir.dt.float8_e4m3fn_x4
 FP4X4 = mybir.dt.float4_e2m1fn_x4
 ALU = mybir.AluOpType
 ACT = mybir.ActivationFunctionType
-AX = mybir.AxisListType
 
 P = 128
 PACK = 4
@@ -20,18 +19,21 @@ B, V, H = 4096, 128, 512
 G = 4 * H
 EPS = 1e-5
 BANK = 512
-BANKS = G // BANK
 ROW_TILES = B // P
 GROUP = 4
 N_GROUPS = ROW_TILES // GROUP
 W_TILES = G // P
-C_STAT_WIDTH = 6 + 3
-STAT_TILES = 4
-X_BANKS = 2
+CELL_TILES = H // P
+LAST = ROW_TILES - 1
 HELD_BANKS = (0, 1)
 COPIED_BANKS = (2, 3)
 SCALAR_BANKS = (1, 2, 3)
 STAT_WIDTH = 6 + 3 * len(SCALAR_BANKS) + 3
+C_STAT_WIDTH = 6 + 3
+STAT_TILES = 4
+X_BANKS = 2
+FLOW_BANKS = 2
+CELL_LAG = 3
 
 FLOPS = 2 * B * G * (V + H)
 
@@ -72,7 +74,7 @@ def tile_multilstm_pa_t_kernel(
         result = ctx.enter_context(tc.tile_pool(name="result", bufs=3))
         small = ctx.enter_context(tc.tile_pool(name="small", bufs=8))
         ps_held = ctx.enter_context(tc.psum_pool(name="ps_held", bufs=len(HELD_BANKS)))
-        ps_flow = ctx.enter_context(tc.psum_pool(name="ps_flow", bufs=2))
+        ps_flow = ctx.enter_context(tc.psum_pool(name="ps_flow", bufs=FLOW_BANKS))
         ps_x = ctx.enter_context(tc.psum_pool(name="ps_x", bufs=X_BANKS))
         ps_const = ctx.enter_context(tc.psum_pool(name="ps_const", bufs=1))
 
@@ -104,11 +106,11 @@ def tile_multilstm_pa_t_kernel(
             )
         for slot, vec in enumerate((lnc_w1, lnc_b1)):
             nc.sync.dma_start(
-                out=vec_rows[3 * W_TILES + slot * (H // P) : 3 * W_TILES + (slot + 1) * (H // P), :],
+                out=vec_rows[3 * W_TILES + slot * CELL_TILES : 3 * W_TILES + (slot + 1) * CELL_TILES, :],
                 in_=vec.rearrange("(t p) -> t p", p=P),
             )
         nc.sync.dma_start(
-            out=vec_rows[3 * W_TILES + 2 * (H // P) : 3 * W_TILES + 4 * (H // P), :],
+            out=vec_rows[3 * W_TILES + 2 * CELL_TILES : 3 * W_TILES + 4 * CELL_TILES, :],
             in_=lnh_w1[len(HELD_BANKS) * BANK : G].rearrange("(t p) -> t p", p=P),
         )
 
@@ -121,7 +123,6 @@ def tile_multilstm_pa_t_kernel(
                 out=w_scales[32 * quad : 32 * quad + 4, :].bitcast(I32),
                 in_=w_hh1_scales[0, 4 * quad : 4 * quad + 4, :].bitcast(I32),
             )
-
 
         gain_h = const.tile([P, len(HELD_BANKS) * BANK], BF16)
         nc.sync.dma_start(out=gain_h[:], in_=lnh_w1[0 : len(HELD_BANKS) * BANK].partition_broadcast(P))
@@ -149,6 +150,7 @@ def tile_multilstm_pa_t_kernel(
             r_stats = const.tile([P, STAT_WIDTH], F32, name="r_stats%d" % k)
             nc.vector.memset(r_stats[:], 0.0)
             r_stats_tiles.append(r_stats)
+        for k in range(STAT_TILES):
             c_stats = const.tile([P, C_STAT_WIDTH], F32, name="c_stats%d" % k)
             nc.vector.memset(c_stats[:], 0.0)
             c_stats_tiles.append(c_stats)
@@ -172,9 +174,9 @@ def tile_multilstm_pa_t_kernel(
                     nc.tensor.transpose(out=hT_ps[:, t, u, :], in_=words[:, u : H // 2 : 2], identity=ident_f32[:])
             groups[grp]["hT_ps"] = hT_ps
 
-        def copy_h0(grp, half, copy=None):
+        def copy_h0(grp, half, copy):
             grouped_words = groups[grp]["grouped"][:].bitcast(F32).rearrange("p (t b u) -> p t b u", t=GROUP, u=2)
-            (copy or nc.scalar.copy)(
+            copy(
                 out=grouped_words[:, 2 * half : 2 * half + 2, :, :],
                 in_=groups[grp]["hT_ps"][:].rearrange("p t u b -> p t b u"),
             )
@@ -241,11 +243,10 @@ def tile_multilstm_pa_t_kernel(
             )
             rstd_a = small.tile([P, width], F32)
             nc.gpsimd.tensor_tensor(out=rstd_a[:], in0=var_eps[:], in1=neg_half[:, 0:width], op=ALU.pow)
-            groups[grp]["rstd_a"] = rstd_a[:]
             for t in range(first, last):
                 groups[grp]["rstd_a", t] = rstd_a[:, t - first : t - first + 1]
 
-        def first_variance(grp, tiles, banks):
+        def x_times_cov(grp, tiles, banks):
             xcov_ps = banks.tile([P, len(tiles), V], F32, tag="bank")
             for k, t in enumerate(tiles):
                 factors = (cov[:],) if grp == 0 else (cov_halves[:, 0, :], cov_halves[:, 1, :])
@@ -256,7 +257,7 @@ def tile_multilstm_pa_t_kernel(
                     )
                 groups[grp]["xcov", t] = xcov_ps[:, k, :]
 
-        def first_variance_sum(grp, t):
+        def sum_x_xcov(grp, t):
             if t == 0:
                 var_a = small.tile([P, GROUP], F32)
                 groups[grp]["var_a"] = var_a
@@ -265,14 +266,6 @@ def tile_multilstm_pa_t_kernel(
                 out=unread_x[:], in0=groups[grp]["xcov", t], scalar=1.0, in1=x_all[:, grp * GROUP + t, :],
                 op0=ALU.mult, op1=ALU.mult, accum_out=groups[grp]["var_a"][:, t : t + 1],
             )
-
-        def scale_group(grp):
-            xhat = prepared.tile([P, GROUP, V], F32)
-            nc.gpsimd.tensor_tensor(
-                out=xhat[:], in0=x_all[:, grp * GROUP : (grp + 1) * GROUP, :],
-                in1=groups[grp]["rstd_a"].unsqueeze(2).to_broadcast([P, GROUP, V]), op=ALU.mult,
-            )
-            groups[grp]["xhat"] = xhat
 
         def scale_x(grp, tiles=range(GROUP)):
             for t in tiles:
@@ -307,8 +300,9 @@ def tile_multilstm_pa_t_kernel(
         w_x = const.tile([V, G], F32)
         vec_cols = const.tile([P, 3 * W_TILES], F32)
         bias_cols = const.tile([P, W_TILES], F32)
-        cell_cols = const.tile([P, 2 * (H // P)], BF16)
-        gain_cols = const.tile([P, 2 * (H // P)], BF16)
+        cell_cols = const.tile([P, 2 * CELL_TILES], BF16)
+        gain_cols = const.tile([P, 2 * CELL_TILES], BF16)
+
         def column_sums(banks):
             wsum_ps = banks.tile([P, V], F32, tag="bank")
             for t in range(W_TILES):
@@ -351,9 +345,9 @@ def tile_multilstm_pa_t_kernel(
             vec_ps = banks.tile([P, P], BF16, tag="bank")
             nc.tensor.transpose(out=vec_ps[:], in_=vec_rows[:], identity=ident_bf[:])
             nc.vector.tensor_copy(out=vec_cols[:], in_=vec_ps[:, 0 : 3 * W_TILES])
-            nc.vector.tensor_copy(out=cell_cols[:], in_=vec_ps[:, 3 * W_TILES : 3 * W_TILES + 2 * (H // P)])
+            nc.vector.tensor_copy(out=cell_cols[:], in_=vec_ps[:, 3 * W_TILES : 3 * W_TILES + 2 * CELL_TILES])
             nc.vector.tensor_scalar_mul(
-                out=gain_cols[:], in0=vec_ps[:, 3 * W_TILES + 2 * (H // P) : 3 * W_TILES + 4 * (H // P)],
+                out=gain_cols[:], in0=vec_ps[:, 3 * W_TILES + 2 * CELL_TILES : 3 * W_TILES + 4 * CELL_TILES],
                 scalar1=float(BANK),
             )
             nc.vector.tensor_tensor(
@@ -364,9 +358,9 @@ def tile_multilstm_pa_t_kernel(
         def spread_rows(name, cols):
             rows = ps_const.tile([P, 2, H], BF16, tag=name)
             made[name] = rows
-            for k in range(2 * (H // P)):
+            for k in range(2 * CELL_TILES):
                 nc.tensor.transpose(
-                    out=rows[:, k // (H // P), (k % (H // P)) * P : (k % (H // P) + 1) * P],
+                    out=rows[:, k // CELL_TILES, (k % CELL_TILES) * P : (k % CELL_TILES + 1) * P],
                     in_=cols[:, k : k + 1].to_broadcast([P, P]),
                     identity=ident_bf[:],
                 )
@@ -388,8 +382,8 @@ def tile_multilstm_pa_t_kernel(
                 )
             made["wt_ps", j] = wt_ps
 
-        def copy_w(j, copy):
-            copy(out=w_x[:, j * BANK : (j + 1) * BANK], in_=made["wt_ps", j][:])
+        def copy_w(j):
+            nc.vector.tensor_copy(out=w_x[:, j * BANK : (j + 1) * BANK], in_=made["wt_ps", j][:])
 
         state = {}
 
@@ -413,15 +407,16 @@ def tile_multilstm_pa_t_kernel(
             state.setdefault(i, {})["r_ps", j] = r_ps
 
         def stats_of(i):
-            return r_stats_tiles[STAT_TILES if i == ROW_TILES - 1 else i % STAT_TILES]
+            return r_stats_tiles[STAT_TILES if i == LAST else i % STAT_TILES]
+
+        def triple(j):
+            return 0 if j == 0 else 6 + 3 * (j - 1)
 
         def mean_col(i, j):
-            col = (3 + 3 * j if j > 0 else 0) + 1
-            return stats_of(i)[:, col : col + 1]
+            return stats_of(i)[:, triple(j) + 1 : triple(j) + 2]
 
         def squares_col(i, j):
-            col = (3 + 3 * j if j > 0 else 0) + 2
-            return stats_of(i)[:, col : col + 1]
+            return stats_of(i)[:, triple(j) + 2 : triple(j) + 3]
 
         def held_mean(i, j):
             unread = wide.tile([P, BANK], BF16, bufs=1)
@@ -456,7 +451,7 @@ def tile_multilstm_pa_t_kernel(
             )
 
         def vector_stats(i):
-            if i < ROW_TILES - 1:
+            if i != LAST:
                 nc.vector.bn_stats(out=stats_of(i)[:, 0:6], in_=state[i]["r_ps", 0][:])
 
         moments = {}
@@ -478,7 +473,7 @@ def tile_multilstm_pa_t_kernel(
 
         def take_inverse_stds(m):
             lo = 0 if m < ROW_TILES else 1
-            hi = 2 if m >= 3 else 1
+            hi = 2 if m >= CELL_LAG else 1
             rstd = small.tile([P, 2], F32)
             nc.gpsimd.tensor_tensor(
                 out=rstd[:, lo:hi], in0=moments[m][:, 2 * lo + 1 : 2 * hi : 2], in1=neg_half[:, lo:hi], op=ALU.pow
@@ -504,6 +499,7 @@ def tile_multilstm_pa_t_kernel(
         def x_side_matmul(i, j):
             banks = ps_flow if i >= ROW_TILES - 2 and j >= 2 else ps_x
             x_ps = banks.tile([P, BANK], F32, tag="bank")
+
             def product(start):
                 nc.tensor.matmul(
                     out=x_ps[:], lhsT=groups[i // GROUP]["xhatT"][:, i % GROUP, :], rhs=w_x[:, bank(j)],
@@ -540,7 +536,7 @@ def tile_multilstm_pa_t_kernel(
             nc.scalar.activation(out=gate, in_=gate, func=func)
 
         def products_engine(i):
-            return nc.vector if i == ROW_TILES - 1 else nc.gpsimd
+            return nc.vector if i == LAST else nc.gpsimd
 
         def kept_cell(i):
             kept = cell.tile([P, H], F32)
@@ -568,12 +564,12 @@ def tile_multilstm_pa_t_kernel(
             nc.vector.bn_stats(out=c_stats_tiles[i % STAT_TILES][:, 0:6], in_=state[i]["c_new"][:])
 
         def aggregate_cell(i):
-            nc.vector.bn_aggr(out=moments_of(i + 3)[:, 2:4], in_=c_stats_tiles[i % STAT_TILES][:])
+            nc.vector.bn_aggr(out=moments_of(i + CELL_LAG)[:, 2:4], in_=c_stats_tiles[i % STAT_TILES][:])
 
         def gain_cell(i):
             cy = result.tile([P, H], F32)
             nc.vector.scalar_tensor_tensor(
-                out=cy[:], in0=state[i]["c_new"][:], scalar=moments[i + 3][:, 2:3], in1=made["cell"][:, 0, :],
+                out=cy[:], in0=state[i]["c_new"][:], scalar=moments[i + CELL_LAG][:, 2:3], in1=made["cell"][:, 0, :],
                 op0=ALU.subtract, op1=ALU.mult,
             )
             state[i]["cy"] = cy
@@ -581,7 +577,7 @@ def tile_multilstm_pa_t_kernel(
         def finish_cy(i):
             cy = state[i]["cy"]
             nc.vector.scalar_tensor_tensor(
-                out=cy[:], in0=cy[:], scalar=inverse_stds[i + 3][:, 1:2], in1=made["cell"][:, 1, :],
+                out=cy[:], in0=cy[:], scalar=inverse_stds[i + CELL_LAG][:, 1:2], in1=made["cell"][:, 1, :],
                 op0=ALU.mult, op1=ALU.add,
             )
             nc.sync.dma_start(out=cy_rows[:, i, :], in_=cy[:])
@@ -610,11 +606,11 @@ def tile_multilstm_pa_t_kernel(
             for c in range(W_TILES // CHUNK):
                 centre(c)
             transpose_h0(0, 0, ps_held)
-            copy_h0(0, 0)
+            copy_h0(0, 0, nc.scalar.copy)
             covariance(0, ps_x)
             spread_vectors(ps_flow)
             transpose_h0(0, 1, ps_held)
-            copy_h0(0, 1)
+            copy_h0(0, 1, nc.scalar.copy)
             covariance(1, ps_x)
             gain_w(0)
             transpose_x(0, ps_flow)
@@ -631,28 +627,28 @@ def tile_multilstm_pa_t_kernel(
             copy_out(0, 2)
             held_mean(0, 1)
             vector_stats(0)
-            first_variance(0, (0,), ps_flow)
-            first_variance_sum(0, 0)
+            x_times_cov(0, (0,), ps_flow)
+            sum_x_xcov(0, 0)
             inverse_std_of_a(0, 0, 1)
             transpose_w(0, ps_x)
-            copy_w(0, nc.vector.tensor_copy)
+            copy_w(0)
             held_squares(0, 1)
             recurrent_matmul(0, 3)
-            first_variance(0, others, ps_x)
+            x_times_cov(0, others, ps_x)
             for t in others:
-                first_variance_sum(0, t)
+                sum_x_xcov(0, t)
             inverse_std_of_a(0, 1, GROUP)
             halve_covariance()
             scale_x(0, (0,))
             copy_out(0, 3)
             transpose_w(1, ps_x)
             transpose_xhat(0, ps_flow, (0,))
-            copy_w(1, nc.vector.tensor_copy)
+            copy_w(1)
             copy_xhatT(0, 0, 1)
             transpose_w(2, ps_const, "cell")
             transpose_w(3, ps_const, "gain")
-            copy_w(2, nc.vector.tensor_copy)
-            copy_w(3, nc.vector.tensor_copy)
+            copy_w(2)
+            copy_w(3)
             copied_squares(0, 2)
             copied_squares(0, 3)
             recurrent_matmul(1, 2)
@@ -684,7 +680,7 @@ def tile_multilstm_pa_t_kernel(
             copy_out(2, 3)
             spread_rows("cell", cell_cols)
             transpose_h0(1, 0, ps_flow)
-            copy_h0(1, 0)
+            copy_h0(1, 0, nc.scalar.copy)
 
             for step in range(1, ROW_TILES):
                 def prepare(lead, piece, *args):
@@ -709,7 +705,7 @@ def tile_multilstm_pa_t_kernel(
                 prepare(5, copy_xT)
                 prepare(3, copy_covx)
                 prepare(2, copy_variance)
-                piece_of(step, 3, gain_cell)
+                piece_of(step, CELL_LAG, gain_cell)
                 piece_of(step, 0, aggregate_r)
                 prepare_second(2, quantise_h0)
                 piece_of(step, 1, add_sides, 1)
@@ -722,13 +718,11 @@ def tile_multilstm_pa_t_kernel(
                 piece_of(step, 2, kept_cell)
                 piece_of(step, 2, fresh_cell)
                 piece_of(step, 2, new_cell)
-                if 0 <= step < ROW_TILES + 3:
-                    take_inverse_stds(step)
+                take_inverse_stds(step)
                 piece_of(step, 4, finish_hy)
                 prepare(3, weigh_covx)
-                if step == 2:
-                    for t in range(GROUP):
-                        first_variance_sum(1, t)
+                for t in range(GROUP):
+                    prepare_second(2, sum_x_xcov, t)
                 prepare_second(2, inverse_std_of_a)
                 prepare(2, inverse_std_of_a)
                 for j in HELD_BANKS:
@@ -739,12 +733,12 @@ def tile_multilstm_pa_t_kernel(
                 piece_of(step, 0, x_side_matmul, 0)
                 piece_of(step, 1, gate_activation, 2, 2, ACT.Tanh)
                 piece_of(step, -2, copy_out, 2)
-                if step == ROW_TILES - 2:
-                    held_mean(ROW_TILES - 1, 0)
+                if step + 1 == LAST:
+                    held_mean(LAST, 0)
                 piece_of(step, -1, held_mean, 1)
                 piece_of(step, -2, copy_out, 3)
-                if step == ROW_TILES - 2:
-                    held_squares(ROW_TILES - 1, 0)
+                if step + 1 == LAST:
+                    held_squares(LAST, 0)
                 piece_of(step, -1, held_squares, 1)
                 piece_of(step, 0, gain_copied)
                 piece_of(step, 1, add_sides, 3)
@@ -753,10 +747,10 @@ def tile_multilstm_pa_t_kernel(
                 prepare_second(1, transpose_h0, 1, ps_flow)
                 piece_of(step, 0, x_side_matmul, 1)
                 piece_of(step, 1, gate_activation, 3, 3, ACT.Sigmoid)
-                prepare(6, copy_h0, 0)
-                prepare(5, copy_h0, 1)
+                prepare(6, copy_h0, 0, nc.scalar.copy)
+                prepare(5, copy_h0, 1, nc.scalar.copy)
                 piece_of(step, 2, cell_stats)
-                piece_of(step, 3, finish_cy)
+                piece_of(step, CELL_LAG, finish_cy)
                 piece_of(step, -1, vector_stats)
                 prepare_second(1, copy_h0, 1, nc.vector.tensor_copy)
                 piece_of(step, 2, aggregate_cell)
@@ -764,7 +758,7 @@ def tile_multilstm_pa_t_kernel(
                 prepare(6, transpose_x, ps_flow)
                 prepare(4, cov_times_x, ps_flow)
                 prepare(3, sum_variance, ps_flow)
-                prepare_second(1, first_variance, range(GROUP), ps_flow)
+                prepare_second(1, x_times_cov, range(GROUP), ps_flow)
                 prepare(1, transpose_xhat, ps_flow)
                 prepare_second(3, transpose_xhat, ps_flow)
                 if step % GROUP == 3 and step // GROUP + 3 < N_GROUPS:
@@ -772,40 +766,39 @@ def tile_multilstm_pa_t_kernel(
                 if step % GROUP == 2 and step // GROUP + 2 < N_GROUPS:
                     load_c0(step // GROUP + 2)
 
-            last = ROW_TILES - 1
-            add_sides(last, 0)
-            tanh_of_cy(last - 3)
-            gain_cell(last - 2)
-            kept_cell(last - 1)
-            fresh_cell(last - 1)
-            x_side_matmul(last, 2)
-            add_sides(last, 1)
-            gate_activation(last, 0, 1, ACT.Sigmoid)
-            x_side_matmul(last, 3)
-            new_cell(last - 1)
-            take_inverse_stds(last + 1)
-            finish_hy(last - 3)
-            add_sides(last, 2)
-            gate_activation(last, 2, 2, ACT.Tanh)
-            kept_cell(last)
-            cell_stats(last - 1)
-            add_sides(last, 3)
-            aggregate_cell(last - 1)
-            take_inverse_stds(last + 2)
-            gate_activation(last, 3, 3, ACT.Sigmoid)
-            fresh_cell(last)
-            finish_cy(last - 2)
-            new_cell(last)
-            tanh_of_cy(last - 2)
-            gain_cell(last - 1)
-            cell_stats(last)
-            finish_cy(last - 1)
-            aggregate_cell(last)
-            finish_hy(last - 2)
-            take_inverse_stds(last + 3)
-            tanh_of_cy(last - 1)
-            gain_cell(last)
-            finish_cy(last)
-            tanh_of_cy(last)
-            finish_hy(last - 1)
-            finish_hy(last)
+            add_sides(LAST, 0)
+            tanh_of_cy(LAST - 3)
+            gain_cell(LAST - 2)
+            kept_cell(LAST - 1)
+            fresh_cell(LAST - 1)
+            x_side_matmul(LAST, 2)
+            add_sides(LAST, 1)
+            gate_activation(LAST, 0, 1, ACT.Sigmoid)
+            x_side_matmul(LAST, 3)
+            new_cell(LAST - 1)
+            take_inverse_stds(LAST + 1)
+            finish_hy(LAST - 3)
+            add_sides(LAST, 2)
+            gate_activation(LAST, 2, 2, ACT.Tanh)
+            kept_cell(LAST)
+            cell_stats(LAST - 1)
+            add_sides(LAST, 3)
+            aggregate_cell(LAST - 1)
+            take_inverse_stds(LAST + 2)
+            gate_activation(LAST, 3, 3, ACT.Sigmoid)
+            fresh_cell(LAST)
+            finish_cy(LAST - 2)
+            new_cell(LAST)
+            tanh_of_cy(LAST - 2)
+            gain_cell(LAST - 1)
+            cell_stats(LAST)
+            finish_cy(LAST - 1)
+            aggregate_cell(LAST)
+            finish_hy(LAST - 2)
+            take_inverse_stds(LAST + 3)
+            tanh_of_cy(LAST - 1)
+            gain_cell(LAST)
+            finish_cy(LAST)
+            tanh_of_cy(LAST)
+            finish_hy(LAST - 1)
+            finish_hy(LAST)

from contextlib import ExitStack

import concourse.mybir as mybir
from concourse.masks import make_identity

F32 = mybir.dt.float32
BF16 = mybir.dt.bfloat16
I32 = mybir.dt.int32
U32 = mybir.dt.uint32
U8 = mybir.dt.uint8
FP8X4 = mybir.dt.float8_e4m3fn_x4
FP4X4 = mybir.dt.float4_e2m1fn_x4
ALU = mybir.AluOpType
ACT = mybir.ActivationFunctionType

P = 128
PACK = 4
B, V, H = 4096, 128, 512
G = 4 * H
EPS = 1e-5
BANK = 512
ROW_TILES = B // P
GROUP = 4
N_GROUPS = ROW_TILES // GROUP
W_TILES = G // P
CELL_TILES = H // P
LAST = ROW_TILES - 1
HELD_BANKS = (0, 1)
COPIED_BANKS = (2, 3)
SCALAR_BANKS = (1, 2, 3)
STAT_WIDTH = 6 + 3 * len(SCALAR_BANKS) + 3
C_STAT_WIDTH = 6 + 3
STAT_TILES = 4
X_BANKS = 2
FLOW_BANKS = 2
CELL_LAG = 3

FLOPS = 2 * B * G * (V + H)


def tile_multilstm_pa_t_kernel(
    tc,
    x,
    h0,
    c0,
    w_ih1,
    w_hh1_words,
    w_hh1_scales,
    lni_w1,
    lni_b1,
    lnh_w1,
    lnh_b1,
    lnc_w1,
    lnc_b1,
    out_0,
    out_1,
):
    nc = tc.nc

    x_rows = x.rearrange("(p i) v -> p i v", i=ROW_TILES)
    h0_rows = h0.rearrange("(p i) k -> p i k", i=ROW_TILES)
    c0_rows = c0.rearrange("(p i) h -> p i h", i=ROW_TILES)
    hy_rows = out_0.rearrange("(p i) h -> p i h", i=ROW_TILES)
    cy_rows = out_1.rearrange("(p i) h -> p i h", i=ROW_TILES)

    with ExitStack() as ctx:
        const = ctx.enter_context(tc.tile_pool(name="const", bufs=1))
        setup = ctx.enter_context(tc.tile_pool(name="setup", bufs=1))
        stream = ctx.enter_context(tc.tile_pool(name="stream", bufs=3))
        prepared = ctx.enter_context(tc.tile_pool(name="prepared", bufs=2))
        wide = ctx.enter_context(tc.tile_pool(name="wide", bufs=2))
        gate_pool = ctx.enter_context(tc.tile_pool(name="gate_pool", bufs=6))
        cell = ctx.enter_context(tc.tile_pool(name="cell", bufs=3))
        result = ctx.enter_context(tc.tile_pool(name="result", bufs=3))
        small = ctx.enter_context(tc.tile_pool(name="small", bufs=8))
        ps_held = ctx.enter_context(tc.psum_pool(name="ps_held", bufs=len(HELD_BANKS)))
        ps_flow = ctx.enter_context(tc.psum_pool(name="ps_flow", bufs=FLOW_BANKS))
        ps_x = ctx.enter_context(tc.psum_pool(name="ps_x", bufs=X_BANKS))
        ps_const = ctx.enter_context(tc.psum_pool(name="ps_const", bufs=1))

        groups = {}

        def load_h0(grp):
            h0_grp = stream.tile([P, GROUP, H], BF16)
            nc.sync.dma_start(out=h0_grp[:], in_=h0_rows[:, grp * GROUP : (grp + 1) * GROUP, :])
            groups[grp] = {"h0": h0_grp}

        def load_c0(grp):
            c0_grp = stream.tile([P, GROUP, H], BF16)
            nc.sync.dma_start(out=c0_grp[:], in_=c0_rows[:, grp * GROUP : (grp + 1) * GROUP, :])
            groups[grp]["c0"] = c0_grp

        w_nat = setup.tile([P, W_TILES, V], BF16)
        w_tiles = w_ih1.rearrange("(t p) v -> p t v", p=P)
        for c in range(4):
            nc.sync.dma_start(out=w_nat[:, 4 * c : 4 * c + 4, :], in_=w_tiles[:, 4 * c : 4 * c + 4, :])
        load_h0(0)
        x_all = const.tile([P, ROW_TILES, V], BF16)
        nc.sync.dma_start(out=x_all[:, 0:GROUP, :], in_=x_rows[:, 0:GROUP, :])
        vec_rows = setup.tile([P, P], BF16)
        nc.vector.memset(vec_rows[:], 0.0)
        for slot, vec in enumerate((lni_w1, lni_b1, lnh_b1)):
            nc.sync.dma_start(
                out=vec_rows[slot * W_TILES : (slot + 1) * W_TILES, :],
                in_=vec.rearrange("(t p) -> t p", p=P),
            )
        for slot, vec in enumerate((lnc_w1, lnc_b1)):
            nc.sync.dma_start(
                out=vec_rows[3 * W_TILES + slot * CELL_TILES : 3 * W_TILES + (slot + 1) * CELL_TILES, :],
                in_=vec.rearrange("(t p) -> t p", p=P),
            )
        nc.sync.dma_start(
            out=vec_rows[3 * W_TILES + 2 * CELL_TILES : 3 * W_TILES + 4 * CELL_TILES, :],
            in_=lnh_w1[len(HELD_BANKS) * BANK : G].rearrange("(t p) -> t p", p=P),
        )

        w_words = const.tile([P, 2 * G], U8, align_bytes=64)
        nc.sync.dma_start(out=w_words[:].bitcast(I32), in_=w_hh1_words[0].bitcast(I32))
        w_scales = const.tile([P, G], U8, align_bytes=64)
        nc.gpsimd.memset(w_scales[:].bitcast(I32), 0)
        for quad in range(4):
            nc.sync.dma_start(
                out=w_scales[32 * quad : 32 * quad + 4, :].bitcast(I32),
                in_=w_hh1_scales[0, 4 * quad : 4 * quad + 4, :].bitcast(I32),
            )

        gain_h = const.tile([P, len(HELD_BANKS) * BANK], BF16)
        nc.sync.dma_start(out=gain_h[:], in_=lnh_w1[0 : len(HELD_BANKS) * BANK].partition_broadcast(P))
        nc.sync.dma_start(out=x_all[:, GROUP:ROW_TILES, :], in_=x_rows[:, GROUP:ROW_TILES, :])
        load_h0(1)
        load_c0(0)
        load_h0(2)
        load_c0(1)

        ident_bf = const.tile([P, P], BF16)
        make_identity(nc, ident_bf[:])
        ident_f32 = const.tile([P, P], F32)
        make_identity(nc, ident_f32[:])
        ones_bf = const.tile([P, P], BF16)
        nc.vector.memset(ones_bf[:], 1.0)
        ones_f32 = const.tile([P, 1], F32)
        nc.vector.memset(ones_f32[:], 1.0)
        neg_half = const.tile([P, GROUP], F32)
        nc.vector.memset(neg_half[:], -0.5)
        table_warmer = const.tile([P, 1], F32)
        nc.scalar.activation(out=table_warmer[:], in_=neg_half[:, 0:1], func=ACT.Sigmoid)
        r_stats_tiles = []
        c_stats_tiles = []
        for k in range(STAT_TILES + 1):
            r_stats = const.tile([P, STAT_WIDTH], F32, name="r_stats%d" % k)
            nc.vector.memset(r_stats[:], 0.0)
            r_stats_tiles.append(r_stats)
        for k in range(STAT_TILES):
            c_stats = const.tile([P, C_STAT_WIDTH], F32, name="c_stats%d" % k)
            nc.vector.memset(c_stats[:], 0.0)
            c_stats_tiles.append(c_stats)
        nc.vector.memset(r_stats_tiles[STAT_TILES][:, 0:1], float(BANK))
        for r_stats in r_stats_tiles:
            nc.vector.memset(r_stats[:, 6 : 6 + 3 * len(SCALAR_BANKS) : 3], float(BANK))
        for stats, count in [(tile, G) for tile in r_stats_tiles] + [(tile, H) for tile in c_stats_tiles]:
            width = stats.shape[1]
            nc.vector.tensor_scalar_add(
                out=stats[:, width - 1 : width], in0=stats[:, width - 3 : width - 2], scalar1=EPS * count
            )

        def transpose_h0(grp, half, banks):
            if half == 0:
                grouped = prepared.tile([P, GROUP * P * PACK], BF16, align_bytes=64)
                groups[grp]["grouped"] = grouped
            hT_ps = banks.tile([P, 2, 2, P], F32, tag="bank")
            for t in range(2):
                words = groups[grp]["h0"][:, 2 * half + t, :].bitcast(F32)
                for u in range(2):
                    nc.tensor.transpose(out=hT_ps[:, t, u, :], in_=words[:, u : H // 2 : 2], identity=ident_f32[:])
            groups[grp]["hT_ps"] = hT_ps

        def copy_h0(grp, half, copy):
            grouped_words = groups[grp]["grouped"][:].bitcast(F32).rearrange("p (t b u) -> p t b u", t=GROUP, u=2)
            copy(
                out=grouped_words[:, 2 * half : 2 * half + 2, :, :],
                in_=groups[grp]["hT_ps"][:].rearrange("p t u b -> p t b u"),
            )

        def quantise_h0(grp):
            h_codes = prepared.tile([P, GROUP * P], U32, align_bytes=64)
            h_scales = prepared.tile([P, GROUP * P], U8, align_bytes=64)
            nc.vector.quantize_mx(
                out=h_codes[:].bitcast(FP8X4), scales=h_scales[:], in_=groups[grp]["grouped"][:]
            )
            groups[grp]["h_codes"] = h_codes
            groups[grp]["h_scales"] = h_scales

        def transpose_x(grp, banks):
            xT_ps = banks.tile([V, GROUP, P], BF16, tag="bank")
            for t in range(GROUP):
                nc.tensor.transpose(out=xT_ps[:, t, :], in_=x_all[:, grp * GROUP + t, :], identity=ident_bf[:])
            groups[grp]["xT_ps"] = xT_ps

        def copy_xT(grp):
            xT = prepared.tile([V, GROUP, P], F32 if grp == 0 else BF16, name="xT_first" if grp == 0 else "xT")
            nc.scalar.copy(out=xT[:], in_=groups[grp]["xT_ps"][:])
            groups[grp]["xT"] = xT

        def cov_times_x(grp, banks):
            covx_ps = banks.tile([V, GROUP, P], F32, tag="bank")
            for half in range(2):
                nc.tensor.matmul(
                    out=covx_ps[:].rearrange("v t b -> v (t b)"), lhsT=cov_halves[:, half, :],
                    rhs=groups[grp]["xT"][:].rearrange("v t b -> v (t b)"), start=(half == 0), stop=(half == 1),
                )
            groups[grp]["covx_ps"] = covx_ps

        def copy_covx(grp):
            covx = prepared.tile([V, GROUP, P], F32)
            nc.scalar.copy(out=covx[:], in_=groups[grp]["covx_ps"][:])
            groups[grp]["covx"] = covx

        def weigh_covx(grp):
            x_covx = prepared.tile([V, GROUP, P], F32)
            nc.gpsimd.tensor_tensor(out=x_covx[:], in0=groups[grp]["covx"][:], in1=groups[grp]["xT"][:], op=ALU.mult)
            groups[grp]["x_covx"] = x_covx

        def sum_variance(grp, banks):
            var_ps = banks.tile([P, GROUP], F32, tag="bank")
            for t in range(GROUP):
                nc.tensor.matmul(
                    out=var_ps[:, t : t + 1], lhsT=groups[grp]["x_covx"][:, t, :], rhs=ones_f32[:],
                    start=True, stop=True,
                )
            groups[grp]["var_ps"] = var_ps

        def copy_variance(grp):
            var_a = small.tile([P, GROUP], F32)
            nc.scalar.copy(out=var_a[:], in_=groups[grp]["var_ps"][:])
            groups[grp]["var_a"] = var_a

        def inverse_std_of_a(grp, first=0, last=GROUP):
            width = last - first
            var_eps = small.tile([P, width], F32)
            nc.gpsimd.tensor_scalar(
                out=var_eps[:], in0=groups[grp]["var_a"][:, first:last], scalar1=1.0, scalar2=EPS,
                op0=ALU.mult, op1=ALU.add,
            )
            rstd_a = small.tile([P, width], F32)
            nc.gpsimd.tensor_tensor(out=rstd_a[:], in0=var_eps[:], in1=neg_half[:, 0:width], op=ALU.pow)
            for t in range(first, last):
                groups[grp]["rstd_a", t] = rstd_a[:, t - first : t - first + 1]

        def x_times_cov(grp, tiles, banks):
            xcov_ps = banks.tile([P, len(tiles), V], F32, tag="bank")
            for k, t in enumerate(tiles):
                factors = (cov[:],) if grp == 0 else (cov_halves[:, 0, :], cov_halves[:, 1, :])
                for n, factor in enumerate(factors):
                    nc.tensor.matmul(
                        out=xcov_ps[:, k, :], lhsT=groups[grp]["xT"][:, t, :], rhs=factor,
                        start=(n == 0), stop=(n == len(factors) - 1),
                    )
                groups[grp]["xcov", t] = xcov_ps[:, k, :]

        def sum_x_xcov(grp, t):
            if t == 0:
                var_a = small.tile([P, GROUP], F32)
                groups[grp]["var_a"] = var_a
            unread_x = setup.tile([P, V], F32)
            nc.vector.scalar_tensor_tensor(
                out=unread_x[:], in0=groups[grp]["xcov", t], scalar=1.0, in1=x_all[:, grp * GROUP + t, :],
                op0=ALU.mult, op1=ALU.mult, accum_out=groups[grp]["var_a"][:, t : t + 1],
            )

        def scale_x(grp, tiles=range(GROUP)):
            for t in tiles:
                if t == 0:
                    xhat = prepared.tile([P, GROUP, V], F32)
                    groups[grp]["xhat"] = xhat
                nc.scalar.activation(
                    out=groups[grp]["xhat"][:, t, :], in_=x_all[:, grp * GROUP + t, :], func=ACT.Copy,
                    scale=groups[grp]["rstd_a", t],
                )

        def transpose_xhat(grp, banks, tiles=range(GROUP)):
            xhatT_ps = banks.tile([V, len(tiles), P], F32, tag="bank")
            for k, t in enumerate(tiles):
                nc.tensor.transpose(
                    out=xhatT_ps[:, k, :], in_=groups[grp]["xhat"][:, t, :], identity=ident_f32[:]
                )
            groups[grp]["xhatT_ps"] = xhatT_ps

        def copy_xhatT(grp, first=0, last=GROUP):
            if first == 0:
                xhatT = prepared.tile([V, GROUP, P], F32)
                groups[grp]["xhatT"] = xhatT
            nc.scalar.copy(out=groups[grp]["xhatT"][:, first:last, :], in_=groups[grp]["xhatT_ps"][:])

        CHUNK = 4
        made = {}
        w_centred = setup.tile([P, W_TILES, V], F32)
        w_gained = setup.tile([P, W_TILES, V], F32)
        cov = const.tile([V, V], F32)
        cov_halves = const.tile([V, 2, V], BF16)
        w_x = const.tile([V, G], F32)
        vec_cols = const.tile([P, 3 * W_TILES], F32)
        bias_cols = const.tile([P, W_TILES], F32)
        cell_cols = const.tile([P, 2 * CELL_TILES], BF16)
        gain_cols = const.tile([P, 2 * CELL_TILES], BF16)

        def column_sums(banks):
            wsum_ps = banks.tile([P, V], F32, tag="bank")
            for t in range(W_TILES):
                nc.tensor.matmul(
                    out=wsum_ps[:], lhsT=ones_bf[:], rhs=w_nat[:, t, :], start=(t == 0), stop=(t == W_TILES - 1)
                )
            made["wsum_ps"] = wsum_ps

        def centre(c):
            tiles = slice(c * CHUNK, (c + 1) * CHUNK)
            nc.vector.scalar_tensor_tensor(
                out=w_centred[:, tiles, :],
                in0=made["wsum_ps"][:].unsqueeze(1).to_broadcast([P, CHUNK, V]),
                scalar=-1.0 / G,
                in1=w_nat[:, tiles, :],
                op0=ALU.mult,
                op1=ALU.add,
            )

        def covariance(c, banks):
            if c == 0:
                cov_ps = banks.tile([V, V], F32, tag="bank")
                made["cov_ps"] = cov_ps
            for t in range(c * CHUNK, (c + 1) * CHUNK):
                nc.tensor.matmul(
                    out=made["cov_ps"][:], lhsT=w_centred[:, t, :], rhs=w_centred[:, t, :],
                    start=(t == 0), stop=(t == W_TILES - 1),
                )

        def scale_covariance():
            nc.vector.tensor_scalar_mul(out=cov[:], in0=made["cov_ps"][:], scalar1=1.0 / G)

        def halve_covariance():
            nc.gpsimd.tensor_copy(out=cov_halves[:, 0, :], in_=cov[:])
            nc.gpsimd.tensor_tensor(
                out=cov_halves[:, 1, :], in0=cov[:], in1=cov_halves[:, 0, :], op=ALU.subtract
            )

        def spread_vectors(banks):
            vec_ps = banks.tile([P, P], BF16, tag="bank")
            nc.tensor.transpose(out=vec_ps[:], in_=vec_rows[:], identity=ident_bf[:])
            nc.vector.tensor_copy(out=vec_cols[:], in_=vec_ps[:, 0 : 3 * W_TILES])
            nc.vector.tensor_copy(out=cell_cols[:], in_=vec_ps[:, 3 * W_TILES : 3 * W_TILES + 2 * CELL_TILES])
            nc.vector.tensor_scalar_mul(
                out=gain_cols[:], in0=vec_ps[:, 3 * W_TILES + 2 * CELL_TILES : 3 * W_TILES + 4 * CELL_TILES],
                scalar1=float(BANK),
            )
            nc.vector.tensor_tensor(
                out=bias_cols[:], in0=vec_cols[:, W_TILES : 2 * W_TILES], in1=vec_cols[:, 2 * W_TILES : 3 * W_TILES],
                op=ALU.add,
            )

        def spread_rows(name, cols):
            rows = ps_const.tile([P, 2, H], BF16, tag=name)
            made[name] = rows
            for k in range(2 * CELL_TILES):
                nc.tensor.transpose(
                    out=rows[:, k // CELL_TILES, (k % CELL_TILES) * P : (k % CELL_TILES + 1) * P],
                    in_=cols[:, k : k + 1].to_broadcast([P, P]),
                    identity=ident_bf[:],
                )

        def gain_w(c):
            tiles = slice(c * CHUNK, (c + 1) * CHUNK)
            nc.vector.tensor_tensor(
                out=w_gained[:, tiles, :],
                in0=w_centred[:, tiles, :],
                in1=vec_cols[:, tiles].unsqueeze(2).to_broadcast([P, CHUNK, V]),
                op=ALU.mult,
            )

        def transpose_w(j, banks, tag="bank"):
            wt_ps = banks.tile([V, BANK], F32, tag=tag)
            for q in range(BANK // P):
                nc.tensor.transpose(
                    out=wt_ps[:, q * P : (q + 1) * P], in_=w_gained[:, j * (BANK // P) + q, :], identity=ident_f32[:]
                )
            made["wt_ps", j] = wt_ps

        def copy_w(j):
            nc.vector.tensor_copy(out=w_x[:, j * BANK : (j + 1) * BANK], in_=made["wt_ps", j][:])

        state = {}

        def bank(j):
            return slice(j * BANK, (j + 1) * BANK)

        def recurrent_matmul(i, j):
            ops = groups[i // GROUP]
            rows = slice((i % GROUP) * P, (i % GROUP + 1) * P)
            banks = ps_held if j in HELD_BANKS else ps_flow
            r_ps = banks.tile([P, BANK], F32, tag="bank")
            nc.tensor.matmul_mx(
                out=r_ps[:],
                lhsT=ops["h_codes"][:, rows].bitcast(FP8X4),
                lhsT_scale=ops["h_scales"][:, rows],
                rhs=w_words[:, 2 * j * BANK : 2 * (j + 1) * BANK].bitcast(FP4X4),
                rhs_scale=w_scales[:, bank(j)],
                start=True,
                stop=True,
            )
            state.setdefault(i, {})["r_ps", j] = r_ps

        def stats_of(i):
            return r_stats_tiles[STAT_TILES if i == LAST else i % STAT_TILES]

        def triple(j):
            return 0 if j == 0 else 6 + 3 * (j - 1)

        def mean_col(i, j):
            return stats_of(i)[:, triple(j) + 1 : triple(j) + 2]

        def squares_col(i, j):
            return stats_of(i)[:, triple(j) + 2 : triple(j) + 3]

        def held_mean(i, j):
            unread = wide.tile([P, BANK], BF16, bufs=1)
            nc.scalar.activation(
                out=unread[:], in_=state[i]["r_ps", j][:], func=ACT.Identity, scale=1.0 / BANK,
                accum_out=mean_col(i, j),
            )

        def held_squares(i, j):
            unread = wide.tile([P, BANK], BF16, bufs=1)
            nc.scalar.activation(
                out=unread[:], in_=state[i]["r_ps", j][:], func=ACT.Square, scale=-1.0,
                bias=mean_col(i, j), accum_out=squares_col(i, j),
            )

        def copy_out(i, j):
            if j == COPIED_BANKS[0]:
                r_copied = wide.tile([P, len(COPIED_BANKS) * BANK], F32, bufs=4)
                state[i]["r_copied"] = r_copied
            k = COPIED_BANKS.index(j)
            nc.scalar.activation(
                out=state[i]["r_copied"][:, k * BANK : (k + 1) * BANK], in_=state[i]["r_ps", j][:],
                func=ACT.Identity, scale=1.0 / BANK, accum_out=mean_col(i, j),
            )

        def copied_squares(i, j):
            k = COPIED_BANKS.index(j)
            unread = wide.tile([P, BANK], BF16, bufs=1)
            nc.scalar.activation(
                out=unread[:], in_=state[i]["r_copied"][:, k * BANK : (k + 1) * BANK], func=ACT.Square,
                scale=-float(BANK), bias=mean_col(i, j), accum_out=squares_col(i, j),
            )

        def vector_stats(i):
            if i != LAST:
                nc.vector.bn_stats(out=stats_of(i)[:, 0:6], in_=state[i]["r_ps", 0][:])

        moments = {}
        inverse_stds = {}

        def moments_of(m):
            if m not in moments:
                mean_var = small.tile([P, 4], F32)
                moments[m] = mean_var
            return moments[m]

        def aggregate_r(i):
            nc.vector.bn_aggr(out=moments_of(i)[:, 0:2], in_=stats_of(i)[:])

        def scale_mean(i):
            small_mean = small.tile([P, 1], F32)
            nc.scalar.activation(out=small_mean[:], in_=moments[i][:, 0:1], func=ACT.Copy, scale=1.0 / BANK)
            state[i]["small_mean"] = small_mean

        def take_inverse_stds(m):
            lo = 0 if m < ROW_TILES else 1
            hi = 2 if m >= CELL_LAG else 1
            rstd = small.tile([P, 2], F32)
            nc.gpsimd.tensor_tensor(
                out=rstd[:, lo:hi], in0=moments[m][:, 2 * lo + 1 : 2 * hi : 2], in1=neg_half[:, lo:hi], op=ALU.pow
            )
            inverse_stds[m] = rstd

        def gain_r(i, j):
            if j == 0:
                r_gained = wide.tile([P, G], F32, bufs=3)
                state[i]["r_gained"] = r_gained
            nc.vector.scalar_tensor_tensor(
                out=state[i]["r_gained"][:, bank(j)], in0=state[i]["r_ps", j][:], scalar=moments[i][:, 0:1],
                in1=gain_h[:, bank(j)], op0=ALU.subtract, op1=ALU.mult,
            )

        def gain_copied(i):
            nc.vector.scalar_tensor_tensor(
                out=state[i]["r_gained"][:, len(HELD_BANKS) * BANK : G], in0=state[i]["r_copied"][:],
                scalar=state[i]["small_mean"][:], in1=made["gain"][:].rearrange("p c n -> p (c n)"),
                op0=ALU.subtract, op1=ALU.mult,
            )

        def x_side_matmul(i, j):
            banks = ps_flow if i >= ROW_TILES - 2 and j >= 2 else ps_x
            x_ps = banks.tile([P, BANK], F32, tag="bank")

            def product(start):
                nc.tensor.matmul(
                    out=x_ps[:], lhsT=groups[i // GROUP]["xhatT"][:, i % GROUP, :], rhs=w_x[:, bank(j)],
                    start=start, stop=not start,
                )

            def biases(start):
                for q in range(BANK // P):
                    col = j * (BANK // P) + q
                    nc.tensor.matmul(
                        out=x_ps[:, q * P : (q + 1) * P],
                        lhsT=bias_cols[:, col : col + 1].to_broadcast([P, P]),
                        rhs=ident_f32[:],
                        is_transpose=True,
                        start=start and q == 0,
                        stop=not start and q == BANK // P - 1,
                    )

            for k, part in enumerate((product, biases) if j % 2 == 0 else (biases, product)):
                part(k == 0)
            state[i]["x_ps", j] = x_ps

        def add_sides(i, j):
            if j == 0:
                gates = gate_pool.tile([P, G], F32)
                state[i]["gates"] = gates
            nc.vector.scalar_tensor_tensor(
                out=state[i]["gates"][:, bank(j)], in0=state[i]["r_gained"][:, bank(j)],
                scalar=inverse_stds[i][:, 0:1], in1=state[i]["x_ps", j][:], op0=ALU.mult, op1=ALU.add,
            )

        def gate_activation(i, first, last, func):
            gate = state[i]["gates"][:, first * BANK : (last + 1) * BANK]
            nc.scalar.activation(out=gate, in_=gate, func=func)

        def products_engine(i):
            return nc.vector if i == LAST else nc.gpsimd

        def kept_cell(i):
            kept = cell.tile([P, H], F32)
            nc.gpsimd.tensor_tensor(
                out=kept[:], in0=state[i]["gates"][:, bank(1)], in1=groups[i // GROUP]["c0"][:, i % GROUP, :],
                op=ALU.mult,
            )
            state[i]["kept"] = kept

        def fresh_cell(i):
            fresh = cell.tile([P, H], F32)
            products_engine(i).tensor_tensor(
                out=fresh[:], in0=state[i]["gates"][:, bank(0)], in1=state[i]["gates"][:, bank(2)], op=ALU.mult
            )
            state[i]["fresh"] = fresh

        def new_cell(i):
            c_new = cell.tile([P, H], F32)
            products_engine(i).tensor_tensor(
                out=c_new[:], in0=state[i]["kept"][:], in1=state[i]["fresh"][:], op=ALU.add
            )
            state[i]["c_new"] = c_new

        def cell_stats(i):
            nc.vector.bn_stats(out=c_stats_tiles[i % STAT_TILES][:, 0:6], in_=state[i]["c_new"][:])

        def aggregate_cell(i):
            nc.vector.bn_aggr(out=moments_of(i + CELL_LAG)[:, 2:4], in_=c_stats_tiles[i % STAT_TILES][:])

        def gain_cell(i):
            cy = result.tile([P, H], F32)
            nc.vector.scalar_tensor_tensor(
                out=cy[:], in0=state[i]["c_new"][:], scalar=moments[i + CELL_LAG][:, 2:3], in1=made["cell"][:, 0, :],
                op0=ALU.subtract, op1=ALU.mult,
            )
            state[i]["cy"] = cy

        def finish_cy(i):
            cy = state[i]["cy"]
            nc.vector.scalar_tensor_tensor(
                out=cy[:], in0=cy[:], scalar=inverse_stds[i + CELL_LAG][:, 1:2], in1=made["cell"][:, 1, :],
                op0=ALU.mult, op1=ALU.add,
            )
            nc.sync.dma_start(out=cy_rows[:, i, :], in_=cy[:])

        def tanh_of_cy(i):
            tanh_cy = cell.tile([P, H], F32)
            nc.scalar.activation(out=tanh_cy[:], in_=state[i]["cy"][:], func=ACT.Tanh)
            state[i]["tanh_cy"] = tanh_cy

        def finish_hy(i):
            hy = result.tile([P, H], F32)
            products_engine(i).tensor_tensor(
                out=hy[:], in0=state[i]["gates"][:, bank(3)], in1=state[i]["tanh_cy"][:], op=ALU.mult
            )
            nc.sync.dma_start(out=hy_rows[:, i, :], in_=hy[:])


        def piece_of(step, lag, piece, *args):
            i = step - lag
            if 0 <= i < ROW_TILES:
                piece(i, *args)

        with tc.manual_schedule():
            others = tuple(range(1, GROUP))
            column_sums(ps_flow)
            for c in range(W_TILES // CHUNK):
                centre(c)
            transpose_h0(0, 0, ps_held)
            copy_h0(0, 0, nc.scalar.copy)
            covariance(0, ps_x)
            spread_vectors(ps_flow)
            transpose_h0(0, 1, ps_held)
            copy_h0(0, 1, nc.scalar.copy)
            covariance(1, ps_x)
            gain_w(0)
            transpose_x(0, ps_flow)
            copy_xT(0)
            quantise_h0(0)
            for c in range(1, W_TILES // CHUNK):
                gain_w(c)
            covariance(2, ps_x)
            covariance(3, ps_x)
            scale_covariance()
            recurrent_matmul(0, 2)
            recurrent_matmul(0, 0)
            recurrent_matmul(0, 1)
            copy_out(0, 2)
            held_mean(0, 1)
            vector_stats(0)
            x_times_cov(0, (0,), ps_flow)
            sum_x_xcov(0, 0)
            inverse_std_of_a(0, 0, 1)
            transpose_w(0, ps_x)
            copy_w(0)
            held_squares(0, 1)
            recurrent_matmul(0, 3)
            x_times_cov(0, others, ps_x)
            for t in others:
                sum_x_xcov(0, t)
            inverse_std_of_a(0, 1, GROUP)
            halve_covariance()
            scale_x(0, (0,))
            copy_out(0, 3)
            transpose_w(1, ps_x)
            transpose_xhat(0, ps_flow, (0,))
            copy_w(1)
            copy_xhatT(0, 0, 1)
            transpose_w(2, ps_const, "cell")
            transpose_w(3, ps_const, "gain")
            copy_w(2)
            copy_w(3)
            copied_squares(0, 2)
            copied_squares(0, 3)
            recurrent_matmul(1, 2)
            x_side_matmul(0, 0)
            aggregate_r(0)
            scale_mean(0)
            take_inverse_stds(0)
            for j in HELD_BANKS:
                gain_r(0, j)
            scale_x(0, others)
            transpose_xhat(0, ps_flow, others)
            copy_out(1, 2)
            copy_xhatT(0, 1, GROUP)
            spread_rows("gain", gain_cols)
            recurrent_matmul(1, 3)
            copy_out(1, 3)
            x_side_matmul(0, 1)
            gain_copied(0)
            for j in HELD_BANKS:
                recurrent_matmul(1, j)
            recurrent_matmul(2, 2)
            recurrent_matmul(2, 3)
            copied_squares(1, 2)
            copied_squares(1, 3)
            vector_stats(1)
            held_mean(1, 1)
            copy_out(2, 2)
            held_squares(1, 1)
            copy_out(2, 3)
            spread_rows("cell", cell_cols)
            transpose_h0(1, 0, ps_flow)
            copy_h0(1, 0, nc.scalar.copy)

            for step in range(1, ROW_TILES):
                def prepare(lead, piece, *args):
                    for grp in range(2, N_GROUPS):
                        if step == grp * GROUP - lead:
                            piece(grp, *args)

                def prepare_second(at, piece, *args):
                    if step == at:
                        piece(1, *args)

                piece_of(step, 1, add_sides, 0)
                piece_of(step, 1, x_side_matmul, 2)
                prepare_second(1, transpose_x, ps_flow)
                piece_of(step, -1, copied_squares, 2)
                piece_of(step, 4, tanh_of_cy)
                prepare_second(3, scale_x)
                prepare(1, scale_x)
                prepare_second(1, copy_xT)
                prepare_second(4, copy_xhatT)
                prepare(0, copy_xhatT)
                prepare(5, copy_xT)
                prepare(3, copy_covx)
                prepare(2, copy_variance)
                piece_of(step, CELL_LAG, gain_cell)
                piece_of(step, 0, aggregate_r)
                prepare_second(2, quantise_h0)
                piece_of(step, 1, add_sides, 1)
                piece_of(step, 1, x_side_matmul, 3)
                piece_of(step, 0, scale_mean)
                piece_of(step, 1, gate_activation, 0, 1, ACT.Sigmoid)
                piece_of(step, -1, copied_squares, 3)
                for j in HELD_BANKS:
                    piece_of(step, 0, gain_r, j)
                piece_of(step, 2, kept_cell)
                piece_of(step, 2, fresh_cell)
                piece_of(step, 2, new_cell)
                take_inverse_stds(step)
                piece_of(step, 4, finish_hy)
                prepare(3, weigh_covx)
                for t in range(GROUP):
                    prepare_second(2, sum_x_xcov, t)
                prepare_second(2, inverse_std_of_a)
                prepare(2, inverse_std_of_a)
                for j in HELD_BANKS:
                    piece_of(step, -1, recurrent_matmul, j)
                piece_of(step, -2, recurrent_matmul, 2)
                piece_of(step, -2, recurrent_matmul, 3)
                piece_of(step, 1, add_sides, 2)
                piece_of(step, 0, x_side_matmul, 0)
                piece_of(step, 1, gate_activation, 2, 2, ACT.Tanh)
                piece_of(step, -2, copy_out, 2)
                if step + 1 == LAST:
                    held_mean(LAST, 0)
                piece_of(step, -1, held_mean, 1)
                piece_of(step, -2, copy_out, 3)
                if step + 1 == LAST:
                    held_squares(LAST, 0)
                piece_of(step, -1, held_squares, 1)
                piece_of(step, 0, gain_copied)
                piece_of(step, 1, add_sides, 3)
                prepare(6, transpose_h0, 0, ps_flow)
                prepare(5, transpose_h0, 1, ps_flow)
                prepare_second(1, transpose_h0, 1, ps_flow)
                piece_of(step, 0, x_side_matmul, 1)
                piece_of(step, 1, gate_activation, 3, 3, ACT.Sigmoid)
                prepare(6, copy_h0, 0, nc.scalar.copy)
                prepare(5, copy_h0, 1, nc.scalar.copy)
                piece_of(step, 2, cell_stats)
                piece_of(step, CELL_LAG, finish_cy)
                piece_of(step, -1, vector_stats)
                prepare_second(1, copy_h0, 1, nc.vector.tensor_copy)
                piece_of(step, 2, aggregate_cell)
                prepare(3, quantise_h0)
                prepare(6, transpose_x, ps_flow)
                prepare(4, cov_times_x, ps_flow)
                prepare(3, sum_variance, ps_flow)
                prepare_second(1, x_times_cov, range(GROUP), ps_flow)
                prepare(1, transpose_xhat, ps_flow)
                prepare_second(3, transpose_xhat, ps_flow)
                if step % GROUP == 3 and step // GROUP + 3 < N_GROUPS:
                    load_h0(step // GROUP + 3)
                if step % GROUP == 2 and step // GROUP + 2 < N_GROUPS:
                    load_c0(step // GROUP + 2)

            add_sides(LAST, 0)
            tanh_of_cy(LAST - 3)
            gain_cell(LAST - 2)
            kept_cell(LAST - 1)
            fresh_cell(LAST - 1)
            x_side_matmul(LAST, 2)
            add_sides(LAST, 1)
            gate_activation(LAST, 0, 1, ACT.Sigmoid)
            x_side_matmul(LAST, 3)
            new_cell(LAST - 1)
            take_inverse_stds(LAST + 1)
            finish_hy(LAST - 3)
            add_sides(LAST, 2)
            gate_activation(LAST, 2, 2, ACT.Tanh)
            kept_cell(LAST)
            cell_stats(LAST - 1)
            add_sides(LAST, 3)
            aggregate_cell(LAST - 1)
            take_inverse_stds(LAST + 2)
            gate_activation(LAST, 3, 3, ACT.Sigmoid)
            fresh_cell(LAST)
            finish_cy(LAST - 2)
            new_cell(LAST)
            tanh_of_cy(LAST - 2)
            gain_cell(LAST - 1)
            cell_stats(LAST)
            finish_cy(LAST - 1)
            aggregate_cell(LAST)
            finish_hy(LAST - 2)
            take_inverse_stds(LAST + 3)
            tanh_of_cy(LAST - 1)
            gain_cell(LAST)
            finish_cy(LAST)
            tanh_of_cy(LAST)
            finish_hy(LAST - 1)
            finish_hy(LAST)
